import numpy as np
import ml_dtypes


def mxq(x, axis, fmt="e4m3"):
    dtype, down = {"e4m3": (ml_dtypes.float8_e4m3fn, 7), "e5m2": (ml_dtypes.float8_e5m2, 14)}[fmt]
    v = np.moveaxis(np.asarray(x, np.float32).astype(ml_dtypes.bfloat16).astype(np.float64), axis, -1)
    blocks = v.reshape(v.shape[:-1] + (-1, 32))
    amax = np.abs(blocks).max(-1, keepdims=True)
    byte = np.maximum(np.where(amax > 0, np.frexp(amax)[1] - 1 + 127, 0) - down, 1)
    scale = np.exp2(byte - 127.0)
    codes = (blocks / scale).astype(np.float32).astype(dtype).astype(np.float64)
    return np.moveaxis((codes * scale).reshape(v.shape), -1, axis)


WIDE = False


def mx_kscale(k):
    if not WIDE:
        return np.ones(k)
    levels = np.array([10, -10, 5, -5, 0])
    a = np.random.permutation(np.resize(levels, k // 512 * 4)).reshape(k // 512, 4)
    idx = np.arange(k)
    return np.exp2(a[idx // 512, idx % 128 // 32])


BF16 = ml_dtypes.bfloat16


def bf(x):
    return np.asarray(x, np.float32).astype(BF16)


def f64(x):
    return np.asarray(x).astype(np.float64)


B, N, C, F = 4, 32, 1024, 1024
KP = 5 * C
EPS_GN = 1e-5


def setup_inputs():
    s = np.concatenate([np.ones(C), mx_kscale(KP - C)])
    t = mx_kscale(C)
    gap = 0.65 * np.sqrt(2.0 * np.log(N))
    mean = 0.65 * np.random.standard_normal((B, N, C))
    lo = mean - gap - 0.35 * np.random.standard_normal((B, N, C))
    hi = mean + gap + 0.35 * np.random.standard_normal((B, N, C))
    std = 0.8 + 0.1 * np.random.standard_normal((B, N, C))
    return {"x": bf(np.random.standard_normal((B, N, C))),
            "agg": bf(np.concatenate([mean, lo, hi, std], axis=-1) * s[C:]),
            "W_post": bf(np.random.standard_normal((KP, C)) / np.sqrt(KP) / s[:, None] * t),
            "b_post": bf(np.random.standard_normal(C) * 0.5 * t),
            "W_lin": bf(np.random.standard_normal((C, C)) / np.sqrt(C) / t[:, None]),
            "b_lin": bf(np.random.standard_normal(C) * 0.5),
            "gn_weight": bf(1.0 + 0.2 * np.random.standard_normal(C)),
            "gn_bias": bf(0.2 * np.random.standard_normal(C)),
            "gn_alpha": bf(0.6 + 0.2 * np.random.standard_normal(C))}


def reference(x, agg, W_post, b_post, W_lin, b_lin, gn_weight, gn_bias, gn_alpha):
    res = f64(x)
    cat = np.concatenate([res, f64(agg)], axis=-1)
    out = (mxq(cat, 2, "e4m3") @ mxq(f64(W_post), 0, "e4m3")) + f64(b_post)
    out = (mxq(out, 2, "e4m3") @ mxq(f64(W_lin), 0, "e4m3")) + f64(b_lin)
    flat = out.reshape(B * N, C)
    mu = flat.mean(axis=0, keepdims=True)
    centered = flat - f64(gn_alpha) * mu
    v = (centered * centered).mean(axis=0, keepdims=True)
    normed = f64(gn_weight) * centered / np.sqrt(v + EPS_GN) + f64(gn_bias)
    return np.maximum(normed, 0.0).reshape(B, N, C) + res

@@ -1,0 +1,288 @@
+from contextlib import ExitStack
+
+import concourse.bass as bass
+import concourse.mybir as mybir
+import concourse.tile as tile
+from concourse.masks import make_identity
+
+F32 = mybir.dt.float32
+BF16 = mybir.dt.bfloat16
+U32 = mybir.dt.uint32
+U8 = mybir.dt.uint8
+FP8X4 = mybir.dt.float8_e4m3fn_x4
+ALU = mybir.AluOpType
+ACT = mybir.ActivationFunctionType
+
+P = 128
+C = 1024
+KP = 5 * C
+N_POST = KP // 512
+N_TILES = C // P
+EPS_GN = 1e-5
+FLOPS = 2 * P * (KP * C + C * C)
+
+V_COLS = 480
+RAW_BUFS = 8
+LIN_PIECES = ((0, 512), (512, 256), (768, 256))
+
+
+def tile_gnnlayer_pb_kernel(
+    tc, x, agg, W_post, b_post, W_lin, b_lin, gn_weight, gn_bias, gn_alpha, out
+):
+    nc = tc.nc
+    with ExitStack() as ctx:
+        keep = ctx.enter_context(tc.tile_pool(name="keep", bufs=1))
+        rawp = ctx.enter_context(tc.tile_pool(name="rawp", bufs=RAW_BUFS))
+        grpp = ctx.enter_context(tc.tile_pool(name="grpp", bufs=3))
+        psum = ctx.enter_context(tc.psum_pool(name="psum", bufs=1))
+
+        one = keep.tile([P, 1], F32, name="one")
+        nc.vector.memset(one[:], 1.0)
+        one_s = keep.tile([P, 1], F32, name="one_s")
+        nc.scalar.activation(out=one_s[:], in_=one[:], func=ACT.Sqrt)
+
+        par_raw = keep.tile([P, P], BF16, name="par_raw")
+        nc.vector.memset(par_raw[:], 0.0)
+
+        ident = keep.tile([P, P], F32, name="ident")
+        make_identity(nc, ident[:])
+        ident_bf = keep.tile([P, P], BF16, name="ident_bf")
+        make_identity(nc, ident_bf[:])
+
+        x_sb = keep.tile([P, C], BF16, name="x_sb")
+        agg_sb = keep.tile([P, 4 * C], BF16, name="agg_sb")
+        agg_f = agg.rearrange("b n c -> (b n) c")
+        nc.sync.dma_start(out=x_sb[:], in_=x.rearrange("b n c -> (b n) c"))
+        nc.sync.dma_start(out=agg_sb[:, 0:2048], in_=agg_f[:, 0:2048])
+        nc.sync.dma_start(out=agg_sb[:, 2048:4096], in_=agg_f[:, 2048:4096])
+        for v, vec in enumerate((b_post, b_lin, gn_weight, gn_bias, gn_alpha)):
+            nc.scalar.dma_start(
+                out=par_raw[8 * v : 8 * v + 8, :], in_=vec.rearrange("(t p) -> t p", p=P)
+            )
+
+        n_units = N_POST + len(LIN_PIECES)
+        raw = {}
+        grp = {}
+        codes = {}
+        scales = {}
+
+        def load(i):
+            if i < N_POST:
+                r = rawp.tile([P, 4, C], BF16, name="raw%d" % i, tag="raw")
+                nc.sync.dma_start(
+                    out=r[:],
+                    in_=W_post[512 * i : 512 * (i + 1), :].rearrange("(p j) c -> p j c", j=4),
+                )
+                raw[i] = r
+            elif i < N_POST + 2:
+                gg = i - N_POST
+                r = rawp.tile([P, 4, C], BF16, name="rawl%d" % gg, tag="raw")
+                nc.sync.dma_start(
+                    out=r[:],
+                    in_=W_lin[512 * gg : 512 * (gg + 1), :].rearrange("(t p) n -> p t n", p=P),
+                )
+                raw[i] = r
+
+        def regroup_copy(eng_copy, dst, src):
+            eng_copy(
+                out=dst.rearrange("p (c i) t -> p c t i", i=4),
+                in_=src.rearrange("p t (c i) -> p c t i", i=4),
+            )
+
+        def regroup(i):
+            if i < N_POST:
+                g = grpp.tile([P, C, 4], BF16, name="grp%d" % i, tag="grp", align_bytes=64)
+                r = raw[i]
+                regroup_copy(nc.vector.tensor_copy, g[:, 0:V_COLS, :], r[:, :, 0:V_COLS])
+                regroup_copy(nc.scalar.copy, g[:, V_COLS:C, :], r[:, :, V_COLS:C])
+            else:
+                c0, w = LIN_PIECES[i - N_POST]
+                g = grpp.tile([P, 2, w, 4], BF16, name="grp%d" % i, tag="grp", align_bytes=64)
+                regroup_copy(nc.vector.tensor_copy, g[:, 0, :, :], raw[N_POST][:, :, c0 : c0 + w])
+                regroup_copy(nc.scalar.copy, g[:, 1, :, :], raw[N_POST + 1][:, :, c0 : c0 + w])
+            grp[i] = g
+
+        def quant(i):
+            if i < N_POST:
+                cd = keep.tile([P, C], U32, name="wc%d" % i, align_bytes=64)
+                sc_ = keep.tile([P, C], U8, name="ws%d" % i, align_bytes=64)
+                nc.vector.quantize_mx(
+                    out=cd[:].bitcast(FP8X4),
+                    scales=sc_[:],
+                    in_=grp[i][:].rearrange("p c t -> p (c t)"),
+                )
+            else:
+                c0, w = LIN_PIECES[i - N_POST]
+                cd = keep.tile([P, 2, w], U32, name="wc%d" % i, align_bytes=64)
+                sc_ = keep.tile([P, 2, w], U8, name="ws%d" % i, align_bytes=64)
+                nc.vector.quantize_mx(
+                    out=cd[:].rearrange("p g c -> p (g c)").bitcast(FP8X4),
+                    scales=sc_[:].rearrange("p g c -> p (g c)"),
+                    in_=grp[i][:].rearrange("p g c t -> p (g c t)"),
+                )
+            codes[i] = cd
+            scales[i] = sc_
+
+        for i in range(RAW_BUFS - 1):
+            load(i)
+
+        x_w = x_sb[:].bitcast(F32).rearrange("n (g p u) -> n g p u", p=P, u=2)
+        agg_w = agg_sb[:].bitcast(F32).rearrange("n (g p u) -> n g p u", p=P, u=2)
+        a_grp = keep.tile([P, N_POST * 512], BF16, name="a_grp", align_bytes=64)
+        a_codes = keep.tile([P, N_POST * P], U32, name="a_codes", align_bytes=64)
+        a_scales = keep.tile([P, N_POST * P], U8, name="a_scales", align_bytes=64)
+        a_grp_w = a_grp[:].bitcast(F32)
+        for b in range(N_POST // 2):
+            pt = psum.tile([P, 4, P], F32, name="pt%d" % b, tag="bk%d" % b)
+            for gg in range(2):
+                g = 2 * b + gg
+                words = x_w[:, g, :, :] if g < 2 else agg_w[:, g - 2, :, :]
+                for u in range(2):
+                    nc.tensor.transpose(pt[:, 2 * gg + u, :], words[:, :, u], ident[:])
+            dst = a_grp_w[:, 512 * b : 512 * (b + 1)].rearrange("p (g n u) -> p g n u", g=2, u=2)
+            src = pt[:].rearrange("p (g u) n -> p g n u", u=2)
+            nc.scalar.copy(out=dst, in_=src)
+        for b in range(N_POST // 2):
+            nc.vector.quantize_mx(
+                out=a_codes[:, 256 * b : 256 * (b + 1)].bitcast(FP8X4),
+                scales=a_scales[:, 256 * b : 256 * (b + 1)],
+                in_=a_grp[:, 1024 * b : 1024 * (b + 1)],
+            )
+
+        par_ps = psum.tile([P, P], BF16, name="par_ps", tag="bk7")
+        nc.tensor.transpose(par_ps[:], par_raw[:], ident_bf[:])
+        par = keep.tile([P, 40], F32, name="par")
+        nc.vector.tensor_copy(out=par[:], in_=par_ps[:, 0:40])
+        bpost = par[:, 0:8]
+        blin = par[:, 8:16]
+        gw = par[:, 16:24]
+        gb = par[:, 24:32]
+        alpha = par[:, 32:40]
+        nalpha = keep.tile([P, 8], F32, name="nalpha")
+        nc.vector.tensor_scalar(
+            out=nalpha[:], in0=alpha, scalar1=-1.0, scalar2=None, op0=ALU.mult
+        )
+        p1 = keep.tile([P, 8], F32, name="p1")
+        nc.vector.tensor_tensor(out=p1[:], in0=nalpha[:], in1=blin, op=ALU.mult)
+        nc.vector.tensor_tensor(out=p1[:], in0=p1[:], in1=blin, op=ALU.add)
+
+        h_pl = keep.tile([P, 8, P], BF16, name="h_pl")
+        h_grp = keep.tile([P, 2, P, 4], BF16, name="h_grp", align_bytes=64)
+        h_codes = keep.tile([P, 2, P], U32, name="h_codes", align_bytes=64)
+        h_scales = keep.tile([P, 2, P], U8, name="h_scales", align_bytes=64)
+        st = keep.tile([P, 8, 6], F32, name="st")
+        mv = keep.tile([P, 8, 2], F32, name="mv")
+        shift = keep.tile([P, 8], F32, name="shift")
+        dd = keep.tile([P, 8], F32, name="dd")
+        vv = keep.tile([P, 8], F32, name="vv")
+        sd = keep.tile([P, 8], F32, name="sd")
+        rs = keep.tile([P, 8], F32, name="rs")
+        scl = keep.tile([P, 8], F32, name="scl")
+        b2 = keep.tile([P, 8], F32, name="b2")
+        y_sb = keep.tile([P, 8, P], F32, name="y_sb")
+        o_sb = keep.tile([P, C], F32, name="o_sb")
+        out_f = out.rearrange("b n c -> (b n) c")
+
+        acc = []
+        for m in range(N_TILES):
+            acc_m = psum.tile([P, P], F32, name="acc%d" % m, tag="bk%d" % m)
+            acc.append(acc_m)
+
+        def mm_post(g):
+            for m in range(N_TILES):
+                nc.tensor.matmul_mx(
+                    out=acc[m][:],
+                    lhsT=codes[g][:, P * m : P * (m + 1)].bitcast(FP8X4),
+                    lhsT_scale=scales[g][:, P * m : P * (m + 1)],
+                    rhs=a_codes[:, P * g : P * (g + 1)].bitcast(FP8X4),
+                    rhs_scale=a_scales[:, P * g : P * (g + 1)],
+                    start=(g == 0),
+                    stop=(g == N_POST - 1),
+                )
+
+        def h_chain():
+            for m in range(N_TILES):
+                if m % 2 == 0:
+                    nc.scalar.activation(
+                        out=h_pl[:, m, :], in_=acc[m][:], func=ACT.Identity,
+                        bias=bpost[:, m : m + 1], scale=1.0,
+                    )
+                else:
+                    nc.vector.tensor_scalar(
+                        out=h_pl[:, m, :], in0=acc[m][:], scalar1=bpost[:, m : m + 1],
+                        scalar2=None, op0=ALU.add,
+                    )
+            for gg in range(2):
+                regroup_copy(
+                    nc.vector.tensor_copy, h_grp[:, gg, :, :], h_pl[:, 4 * gg : 4 * gg + 4, :]
+                )
+            nc.vector.quantize_mx(
+                out=h_codes[:].rearrange("p g n -> p (g n)").bitcast(FP8X4),
+                scales=h_scales[:].rearrange("p g n -> p (g n)"),
+                in_=h_grp[:].rearrange("p g n t -> p (g n t)"),
+            )
+
+        def stage2(i):
+            c0, w = LIN_PIECES[i - N_POST]
+            m0 = c0 // P
+            nb = w // P
+            o_ps = []
+            for j in range(nb):
+                m = m0 + j
+                o_m = psum.tile([P, P], F32, name="o%d" % m, tag="bk%d" % m)
+                o_ps.append(o_m)
+                for gg in range(2):
+                    nc.tensor.matmul_mx(
+                        out=o_m[:],
+                        lhsT=codes[i][:, gg, P * j : P * (j + 1)].bitcast(FP8X4),
+                        lhsT_scale=scales[i][:, gg, P * j : P * (j + 1)],
+                        rhs=h_codes[:, gg, :].bitcast(FP8X4),
+                        rhs_scale=h_scales[:, gg, :],
+                        start=(gg == 0),
+                        stop=(gg == 1),
+                    )
+            for j in range(nb):
+                m = m0 + j
+                nc.vector.bn_stats(out=st[:, m, :], in_=o_ps[j][:])
+                nc.vector.bn_aggr(out=mv[:, m, :], in_=st[:, m, :])
+            sl = slice(m0, m0 + nb)
+            mean = mv[:, sl, 0]
+            var = mv[:, sl, 1]
+            nc.vector.tensor_tensor(out=shift[:, sl], in0=mean, in1=nalpha[:, sl], op=ALU.mult)
+            nc.vector.tensor_tensor(out=shift[:, sl], in0=shift[:, sl], in1=p1[:, sl], op=ALU.add)
+            nc.vector.tensor_tensor(out=dd[:, sl], in0=shift[:, sl], in1=mean, op=ALU.add)
+            nc.vector.tensor_tensor(out=dd[:, sl], in0=dd[:, sl], in1=dd[:, sl], op=ALU.mult)
+            nc.vector.scalar_tensor_tensor(
+                out=vv[:, sl], in0=dd[:, sl], scalar=EPS_GN, in1=var, op0=ALU.add, op1=ALU.add
+            )
+            nc.scalar.activation(out=sd[:, sl], in_=vv[:, sl], func=ACT.Sqrt)
+            nc.vector.reciprocal(out=rs[:, sl], in_=sd[:, sl])
+            nc.vector.tensor_tensor(out=scl[:, sl], in0=rs[:, sl], in1=gw[:, sl], op=ALU.mult)
+            nc.vector.tensor_tensor(out=b2[:, sl], in0=scl[:, sl], in1=shift[:, sl], op=ALU.mult)
+            nc.vector.tensor_tensor(out=b2[:, sl], in0=b2[:, sl], in1=gb[:, sl], op=ALU.add)
+            for j in range(nb):
+                m = m0 + j
+                nc.scalar.activation(
+                    out=y_sb[:, m, :], in_=o_ps[j][:], func=ACT.Relu,
+                    bias=b2[:, m : m + 1], scale=scl[:, m : m + 1],
+                )
+            y_t = psum.tile([P, w], F32, name="yt%d" % m0, tag="bk%d" % m0)
+            for j in range(nb):
+                nc.tensor.transpose(y_t[:, P * j : P * (j + 1)], y_sb[:, m0 + j, :], ident[:])
+            nc.vector.tensor_tensor(
+                out=o_sb[:, c0 : c0 + w], in0=y_t[:], in1=x_sb[:, c0 : c0 + w], op=ALU.add
+            )
+            nc.sync.dma_start(out=out_f[:, c0 : c0 + w], in_=o_sb[:, c0 : c0 + w])
+
+        for i in range(n_units + 1):
+            if i < n_units:
+                regroup(i)
+                load(i + RAW_BUFS - 1)
+            if i >= 1:
+                quant(i - 1)
+                if i - 1 < N_POST:
+                    mm_post(i - 1)
+                    if i - 1 == N_POST - 1:
+                        h_chain()
+                else:
+                    stage2(i - 1)

@@ -1,8 +1,6 @@
 from contextlib import ExitStack
 
-import concourse.bass as bass
 import concourse.mybir as mybir
-import concourse.tile as tile
 from concourse.masks import make_identity
 
 F32 = mybir.dt.float32
@@ -17,13 +15,15 @@ P = 128
 C = 1024
 KP = 5 * C
 N_POST = KP // 512
-N_TILES = C // P
 EPS_GN = 1e-5
 FLOPS = 2 * P * (KP * C + C * C)
 
-V_COLS = 480
+V_COLS = 496
 RAW_BUFS = 8
-LIN_PIECES = ((0, 512), (512, 256), (768, 256))
+LW = 256
+GROUPS = ((0, 4), (4, 4))
+VE = 0
+SE = 1
 
 
 def tile_gnnlayer_pb_kernel(
@@ -35,15 +35,16 @@ def tile_gnnlayer_pb_kernel(
         rawp = ctx.enter_context(tc.tile_pool(name="rawp", bufs=RAW_BUFS))
         grpp = ctx.enter_context(tc.tile_pool(name="grpp", bufs=3))
         psum = ctx.enter_context(tc.psum_pool(name="psum", bufs=1))
+        ctx.enter_context(tc.manual_schedule())
 
         one = keep.tile([P, 1], F32, name="one")
         nc.vector.memset(one[:], 1.0)
         one_s = keep.tile([P, 1], F32, name="one_s")
         nc.scalar.activation(out=one_s[:], in_=one[:], func=ACT.Sqrt)
-
+        eps_t = keep.tile([P, 1], F32, name="eps_t")
+        nc.vector.memset(eps_t[:], EPS_GN)
         par_raw = keep.tile([P, P], BF16, name="par_raw")
         nc.vector.memset(par_raw[:], 0.0)
-
         ident = keep.tile([P, P], F32, name="ident")
         make_identity(nc, ident[:])
         ident_bf = keep.tile([P, P], BF16, name="ident_bf")
@@ -52,79 +53,21 @@ def tile_gnnlayer_pb_kernel(
         x_sb = keep.tile([P, C], BF16, name="x_sb")
         agg_sb = keep.tile([P, 4 * C], BF16, name="agg_sb")
         agg_f = agg.rearrange("b n c -> (b n) c")
-        nc.sync.dma_start(out=x_sb[:], in_=x.rearrange("b n c -> (b n) c"))
-        nc.sync.dma_start(out=agg_sb[:, 0:2048], in_=agg_f[:, 0:2048])
-        nc.sync.dma_start(out=agg_sb[:, 2048:4096], in_=agg_f[:, 2048:4096])
-        for v, vec in enumerate((b_post, b_lin, gn_weight, gn_bias, gn_alpha)):
-            nc.scalar.dma_start(
-                out=par_raw[8 * v : 8 * v + 8, :], in_=vec.rearrange("(t p) -> t p", p=P)
-            )
+        out_f = out.rearrange("b n c -> (b n) c")
+        lin_v = W_lin.rearrange("(a p) n -> p a n", p=P)
 
-        n_units = N_POST + len(LIN_PIECES)
         raw = {}
         grp = {}
         codes = {}
         scales = {}
-
-        def load(i):
-            if i < N_POST:
-                r = rawp.tile([P, 4, C], BF16, name="raw%d" % i, tag="raw")
-                nc.sync.dma_start(
-                    out=r[:],
-                    in_=W_post[512 * i : 512 * (i + 1), :].rearrange("(p j) c -> p j c", j=4),
-                )
-                raw[i] = r
-            elif i < N_POST + 2:
-                gg = i - N_POST
-                r = rawp.tile([P, 4, C], BF16, name="rawl%d" % gg, tag="raw")
-                nc.sync.dma_start(
-                    out=r[:],
-                    in_=W_lin[512 * gg : 512 * (gg + 1), :].rearrange("(t p) n -> p t n", p=P),
-                )
-                raw[i] = r
-
-        def regroup_copy(eng_copy, dst, src):
-            eng_copy(
-                out=dst.rearrange("p (c i) t -> p c t i", i=4),
-                in_=src.rearrange("p t (c i) -> p c t i", i=4),
-            )
-
-        def regroup(i):
-            if i < N_POST:
-                g = grpp.tile([P, C, 4], BF16, name="grp%d" % i, tag="grp", align_bytes=64)
-                r = raw[i]
-                regroup_copy(nc.vector.tensor_copy, g[:, 0:V_COLS, :], r[:, :, 0:V_COLS])
-                regroup_copy(nc.scalar.copy, g[:, V_COLS:C, :], r[:, :, V_COLS:C])
-            else:
-                c0, w = LIN_PIECES[i - N_POST]
-                g = grpp.tile([P, 2, w, 4], BF16, name="grp%d" % i, tag="grp", align_bytes=64)
-                regroup_copy(nc.vector.tensor_copy, g[:, 0, :, :], raw[N_POST][:, :, c0 : c0 + w])
-                regroup_copy(nc.scalar.copy, g[:, 1, :, :], raw[N_POST + 1][:, :, c0 : c0 + w])
-            grp[i] = g
-
-        def quant(i):
-            if i < N_POST:
-                cd = keep.tile([P, C], U32, name="wc%d" % i, align_bytes=64)
-                sc_ = keep.tile([P, C], U8, name="ws%d" % i, align_bytes=64)
-                nc.vector.quantize_mx(
-                    out=cd[:].bitcast(FP8X4),
-                    scales=sc_[:],
-                    in_=grp[i][:].rearrange("p c t -> p (c t)"),
-                )
-            else:
-                c0, w = LIN_PIECES[i - N_POST]
-                cd = keep.tile([P, 2, w], U32, name="wc%d" % i, align_bytes=64)
-                sc_ = keep.tile([P, 2, w], U8, name="ws%d" % i, align_bytes=64)
-                nc.vector.quantize_mx(
-                    out=cd[:].rearrange("p g c -> p (g c)").bitcast(FP8X4),
-                    scales=sc_[:].rearrange("p g c -> p (g c)"),
-                    in_=grp[i][:].rearrange("p g c t -> p (g c t)"),
-                )
-            codes[i] = cd
-            scales[i] = sc_
-
-        for i in range(RAW_BUFS - 1):
-            load(i)
+        lraw = {}
+        lgrp = {}
+        lcodes = {}
+        lscales = {}
+        pts = {}
+        acc = {}
+        o_ps = {}
+        y_t = {}
 
         x_w = x_sb[:].bitcast(F32).rearrange("n (g p u) -> n g p u", p=P, u=2)
         agg_w = agg_sb[:].bitcast(F32).rearrange("n (g p u) -> n g p u", p=P, u=2)
@@ -132,40 +75,14 @@ def tile_gnnlayer_pb_kernel(
         a_codes = keep.tile([P, N_POST * P], U32, name="a_codes", align_bytes=64)
         a_scales = keep.tile([P, N_POST * P], U8, name="a_scales", align_bytes=64)
         a_grp_w = a_grp[:].bitcast(F32)
-        for b in range(N_POST // 2):
-            pt = psum.tile([P, 4, P], F32, name="pt%d" % b, tag="bk%d" % b)
-            for gg in range(2):
-                g = 2 * b + gg
-                words = x_w[:, g, :, :] if g < 2 else agg_w[:, g - 2, :, :]
-                for u in range(2):
-                    nc.tensor.transpose(pt[:, 2 * gg + u, :], words[:, :, u], ident[:])
-            dst = a_grp_w[:, 512 * b : 512 * (b + 1)].rearrange("p (g n u) -> p g n u", g=2, u=2)
-            src = pt[:].rearrange("p (g u) n -> p g n u", u=2)
-            nc.scalar.copy(out=dst, in_=src)
-        for b in range(N_POST // 2):
-            nc.vector.quantize_mx(
-                out=a_codes[:, 256 * b : 256 * (b + 1)].bitcast(FP8X4),
-                scales=a_scales[:, 256 * b : 256 * (b + 1)],
-                in_=a_grp[:, 1024 * b : 1024 * (b + 1)],
-            )
-
-        par_ps = psum.tile([P, P], BF16, name="par_ps", tag="bk7")
-        nc.tensor.transpose(par_ps[:], par_raw[:], ident_bf[:])
         par = keep.tile([P, 40], F32, name="par")
-        nc.vector.tensor_copy(out=par[:], in_=par_ps[:, 0:40])
         bpost = par[:, 0:8]
         blin = par[:, 8:16]
         gw = par[:, 16:24]
         gb = par[:, 24:32]
         alpha = par[:, 32:40]
-        nalpha = keep.tile([P, 8], F32, name="nalpha")
-        nc.vector.tensor_scalar(
-            out=nalpha[:], in0=alpha, scalar1=-1.0, scalar2=None, op0=ALU.mult
-        )
+        a1 = keep.tile([P, 8], F32, name="a1")
         p1 = keep.tile([P, 8], F32, name="p1")
-        nc.vector.tensor_tensor(out=p1[:], in0=nalpha[:], in1=blin, op=ALU.mult)
-        nc.vector.tensor_tensor(out=p1[:], in0=p1[:], in1=blin, op=ALU.add)
-
         h_pl = keep.tile([P, 8, P], BF16, name="h_pl")
         h_grp = keep.tile([P, 2, P, 4], BF16, name="h_grp", align_bytes=64)
         h_codes = keep.tile([P, 2, P], U32, name="h_codes", align_bytes=64)
@@ -175,114 +92,496 @@ def tile_gnnlayer_pb_kernel(
         shift = keep.tile([P, 8], F32, name="shift")
         dd = keep.tile([P, 8], F32, name="dd")
         vv = keep.tile([P, 8], F32, name="vv")
+        qq = keep.tile([P, 8], F32, name="qq")
         sd = keep.tile([P, 8], F32, name="sd")
-        rs = keep.tile([P, 8], F32, name="rs")
+        rs_ = keep.tile([P, 8], F32, name="rs_")
         scl = keep.tile([P, 8], F32, name="scl")
         b2 = keep.tile([P, 8], F32, name="b2")
         y_sb = keep.tile([P, 8, P], F32, name="y_sb")
         o_sb = keep.tile([P, C], F32, name="o_sb")
-        out_f = out.rearrange("b n c -> (b n) c")
 
-        acc = []
-        for m in range(N_TILES):
-            acc_m = psum.tile([P, P], F32, name="acc%d" % m, tag="bk%d" % m)
-            acc.append(acc_m)
+        def ld_x():
+            nc.sync.dma_start(out=x_sb[:], in_=x.rearrange("b n c -> (b n) c"))
 
-        def mm_post(g):
-            for m in range(N_TILES):
-                nc.tensor.matmul_mx(
-                    out=acc[m][:],
-                    lhsT=codes[g][:, P * m : P * (m + 1)].bitcast(FP8X4),
-                    lhsT_scale=scales[g][:, P * m : P * (m + 1)],
-                    rhs=a_codes[:, P * g : P * (g + 1)].bitcast(FP8X4),
-                    rhs_scale=a_scales[:, P * g : P * (g + 1)],
-                    start=(g == 0),
-                    stop=(g == N_POST - 1),
-                )
-
-        def h_chain():
-            for m in range(N_TILES):
-                if m % 2 == 0:
-                    nc.scalar.activation(
-                        out=h_pl[:, m, :], in_=acc[m][:], func=ACT.Identity,
-                        bias=bpost[:, m : m + 1], scale=1.0,
-                    )
-                else:
-                    nc.vector.tensor_scalar(
-                        out=h_pl[:, m, :], in0=acc[m][:], scalar1=bpost[:, m : m + 1],
-                        scalar2=None, op0=ALU.add,
-                    )
-            for gg in range(2):
-                regroup_copy(
-                    nc.vector.tensor_copy, h_grp[:, gg, :, :], h_pl[:, 4 * gg : 4 * gg + 4, :]
-                )
-            nc.vector.quantize_mx(
-                out=h_codes[:].rearrange("p g n -> p (g n)").bitcast(FP8X4),
-                scales=h_scales[:].rearrange("p g n -> p (g n)"),
-                in_=h_grp[:].rearrange("p g n t -> p (g n t)"),
+        def ld_agg(h):
+            nc.sync.dma_start(
+                out=agg_sb[:, 2048 * h : 2048 * (h + 1)], in_=agg_f[:, 2048 * h : 2048 * (h + 1)]
             )
 
-        def stage2(i):
-            c0, w = LIN_PIECES[i - N_POST]
-            m0 = c0 // P
-            nb = w // P
-            o_ps = []
-            for j in range(nb):
-                m = m0 + j
+        def ld_par():
+            for v, vec in enumerate((b_post, b_lin, gn_weight, gn_bias, gn_alpha)):
+                nc.scalar.dma_start(
+                    out=par_raw[8 * v : 8 * v + 8, :], in_=vec.rearrange("(t p) -> t p", p=P)
+                )
+
+        def ld_w(i):
+            r = rawp.tile([P, 4, C], BF16, name="raw%d" % i, tag="raw")
+            nc.sync.dma_start(
+                out=r[:], in_=W_post[512 * i : 512 * (i + 1), :].rearrange("(p j) c -> p j c", j=4)
+            )
+            raw[i] = r
+
+        def ld_lin(h):
+            r = rawp.tile([P, 8, 512], BF16, name="lraw%d" % h, tag="raw")
+            nc.sync.dma_start(out=r[:], in_=lin_v[:, :, 512 * h : 512 * (h + 1)])
+            lraw[h] = r
+
+        def t_act(b):
+            pt = psum.tile([P, 4, P], F32, name="pt%d" % b, tag="bk%d" % b)
+            for gg in range(2):
+                g = 2 * b + gg
+                words = x_w[:, g, :, :] if g < 2 else agg_w[:, g - 2, :, :]
+                for u in range(2):
+                    nc.tensor.transpose(pt[:, 2 * gg + u, :], words[:, :, u], ident[:])
+            pts[b] = pt
+
+        def copy_on(eng):
+            return nc.vector.tensor_copy if eng == VE else nc.scalar.copy
+
+        def ae(b, eng):
+            dst = a_grp_w[:, 512 * b : 512 * (b + 1)].rearrange("p (g n u) -> p g n u", g=2, u=2)
+            copy_on(eng)(out=dst, in_=pts[b][:].rearrange("p (g u) n -> p g n u", u=2))
+
+        def aq(b):
+            nc.vector.quantize_mx(
+                out=a_codes[:, 256 * b : 256 * (b + 1)].bitcast(FP8X4),
+                scales=a_scales[:, 256 * b : 256 * (b + 1)],
+                in_=a_grp[:, 1024 * b : 1024 * (b + 1)],
+            )
+
+        def par_t():
+            par_ps = psum.tile([P, P], BF16, name="par_ps", tag="bk7")
+            nc.tensor.transpose(par_ps[:], par_raw[:], ident_bf[:])
+            pts[9] = par_ps
+
+        def par_v():
+            nc.vector.tensor_copy(out=par[:], in_=pts[9][:, 0:40])
+            nc.vector.tensor_scalar(
+                out=a1[:], in0=alpha, scalar1=-1.0, scalar2=1.0, op0=ALU.mult, op1=ALU.add
+            )
+            nc.vector.tensor_tensor(out=p1[:], in0=a1[:], in1=blin, op=ALU.mult)
+
+        def regroup_copy(eng, dst, src):
+            copy_on(eng)(
+                out=dst.rearrange("p (c i) t -> p c t i", i=4),
+                in_=src.rearrange("p t (c i) -> p c t i", i=4),
+            )
+
+        def unit_grp(i):
+            if i not in grp:
+                g = grpp.tile([P, C, 4], BF16, name="grp%d" % i, tag="grp", align_bytes=64)
+                grp[i] = g
+            return grp[i]
+
+        def rv(i):
+            regroup_copy(VE, unit_grp(i)[:, 0:V_COLS, :], raw[i][:, :, 0:V_COLS])
+
+        def rs(i):
+            regroup_copy(SE, unit_grp(i)[:, V_COLS:C, :], raw[i][:, :, V_COLS:C])
+
+        def q(i):
+            cd = keep.tile([P, C], U32, name="wc%d" % i, align_bytes=64)
+            sc_ = keep.tile([P, C], U8, name="ws%d" % i, align_bytes=64)
+            nc.vector.quantize_mx(
+                out=cd[:].bitcast(FP8X4), scales=sc_[:], in_=grp[i][:].rearrange("p c t -> p (c t)")
+            )
+            codes[i] = cd
+            scales[i] = sc_
+
+        def mm(g, m):
+            if m not in acc:
+                acc_m = psum.tile([P, P], F32, name="acc%d" % m, tag="bk%d" % m)
+                acc[m] = acc_m
+            nc.tensor.matmul_mx(
+                out=acc[m][:],
+                lhsT=codes[g][:, P * m : P * (m + 1)].bitcast(FP8X4),
+                lhsT_scale=scales[g][:, P * m : P * (m + 1)],
+                rhs=a_codes[:, P * g : P * (g + 1)].bitcast(FP8X4),
+                rhs_scale=a_scales[:, P * g : P * (g + 1)],
+                start=(g == 0),
+                stop=(g == N_POST - 1),
+            )
+
+        def r_lin(j, gg, lo, hi, eng):
+            if j not in lgrp:
+                g = keep.tile([P, 2, LW, 4], BF16, name="lgrp%d" % j, align_bytes=64)
+                lgrp[j] = g
+            c0 = LW * j
+            r = lraw[c0 // 512]
+            c0 = c0 % 512
+            regroup_copy(
+                eng, lgrp[j][:, gg, lo:hi, :], r[:, 4 * gg : 4 * gg + 4, c0 + lo : c0 + hi]
+            )
+
+        def q_lin(j):
+            cd = keep.tile([P, 2, LW], U32, name="lc%d" % j, align_bytes=64)
+            sc_ = keep.tile([P, 2, LW], U8, name="ls%d" % j, align_bytes=64)
+            nc.vector.quantize_mx(
+                out=cd[:].rearrange("p g c -> p (g c)").bitcast(FP8X4),
+                scales=sc_[:].rearrange("p g c -> p (g c)"),
+                in_=lgrp[j][:].rearrange("p g c t -> p (g c t)"),
+            )
+            lcodes[j] = cd
+            lscales[j] = sc_
+
+        def he(m, eng):
+            if eng == SE:
+                nc.scalar.activation(
+                    out=h_pl[:, m, :], in_=acc[m][:], func=ACT.Identity,
+                    bias=bpost[:, m : m + 1], scale=1.0,
+                )
+            else:
+                nc.vector.tensor_scalar(
+                    out=h_pl[:, m, :], in0=acc[m][:], scalar1=bpost[:, m : m + 1],
+                    scalar2=None, op0=ALU.add,
+                )
+
+        def hr(gg):
+            regroup_copy(VE, h_grp[:, gg, :, :], h_pl[:, 4 * gg : 4 * gg + 4, :])
+
+        def hq(gg):
+            nc.vector.quantize_mx(
+                out=h_codes[:, gg, :].bitcast(FP8X4),
+                scales=h_scales[:, gg, :],
+                in_=h_grp[:, gg, :, :].rearrange("p n t -> p (n t)"),
+            )
+
+        def s2(m, gg):
+            if m not in o_ps:
                 o_m = psum.tile([P, P], F32, name="o%d" % m, tag="bk%d" % m)
-                o_ps.append(o_m)
-                for gg in range(2):
-                    nc.tensor.matmul_mx(
-                        out=o_m[:],
-                        lhsT=codes[i][:, gg, P * j : P * (j + 1)].bitcast(FP8X4),
-                        lhsT_scale=scales[i][:, gg, P * j : P * (j + 1)],
-                        rhs=h_codes[:, gg, :].bitcast(FP8X4),
-                        rhs_scale=h_scales[:, gg, :],
-                        start=(gg == 0),
-                        stop=(gg == 1),
-                    )
-            for j in range(nb):
-                m = m0 + j
-                nc.vector.bn_stats(out=st[:, m, :], in_=o_ps[j][:])
-                nc.vector.bn_aggr(out=mv[:, m, :], in_=st[:, m, :])
+                o_ps[m] = o_m
+            j = (P * m) // LW
+            k = (P * m) % LW
+            nc.tensor.matmul_mx(
+                out=o_ps[m][:],
+                lhsT=lcodes[j][:, gg, k : k + P].bitcast(FP8X4),
+                lhsT_scale=lscales[j][:, gg, k : k + P],
+                rhs=h_codes[:, gg, :].bitcast(FP8X4),
+                rhs_scale=h_scales[:, gg, :],
+                start=(gg == 0),
+                stop=(gg == 1),
+            )
+
+        def bs(m):
+            nc.vector.bn_stats(out=st[:, m, :], in_=o_ps[m][:])
+
+        def ba(m):
+            nc.vector.bn_aggr(out=mv[:, m, :], in_=st[:, m, :])
+
+        def tt_v(o, a, b, op):
+            nc.vector.tensor_tensor(out=o, in0=a, in1=b, op=op)
+
+        def sm(kind, g):
+            m0, nb = GROUPS[g]
             sl = slice(m0, m0 + nb)
             mean = mv[:, sl, 0]
             var = mv[:, sl, 1]
-            nc.vector.tensor_tensor(out=shift[:, sl], in0=mean, in1=nalpha[:, sl], op=ALU.mult)
-            nc.vector.tensor_tensor(out=shift[:, sl], in0=shift[:, sl], in1=p1[:, sl], op=ALU.add)
-            nc.vector.tensor_tensor(out=dd[:, sl], in0=shift[:, sl], in1=mean, op=ALU.add)
-            nc.vector.tensor_tensor(out=dd[:, sl], in0=dd[:, sl], in1=dd[:, sl], op=ALU.mult)
-            nc.vector.scalar_tensor_tensor(
-                out=vv[:, sl], in0=dd[:, sl], scalar=EPS_GN, in1=var, op0=ALU.add, op1=ALU.add
-            )
-            nc.scalar.activation(out=sd[:, sl], in_=vv[:, sl], func=ACT.Sqrt)
-            nc.vector.reciprocal(out=rs[:, sl], in_=sd[:, sl])
-            nc.vector.tensor_tensor(out=scl[:, sl], in0=rs[:, sl], in1=gw[:, sl], op=ALU.mult)
-            nc.vector.tensor_tensor(out=b2[:, sl], in0=scl[:, sl], in1=shift[:, sl], op=ALU.mult)
-            nc.vector.tensor_tensor(out=b2[:, sl], in0=b2[:, sl], in1=gb[:, sl], op=ALU.add)
-            for j in range(nb):
-                m = m0 + j
+            if kind == "d1":
+                tt_v(dd[:, sl], mean, a1[:, sl], ALU.mult)
+            elif kind == "d2":
+                tt_v(dd[:, sl], dd[:, sl], p1[:, sl], ALU.add)
+            elif kind == "v1":
+                tt_v(vv[:, sl], dd[:, sl], dd[:, sl], ALU.mult)
+            elif kind == "v2":
+                tt_v(vv[:, sl], vv[:, sl], var, ALU.add)
+            elif kind == "sh":
+                tt_v(shift[:, sl], dd[:, sl], mean, ALU.subtract)
+            elif kind == "qq":
+                tt_v(qq[:, sl], shift[:, sl], gw[:, sl], ALU.mult)
+            elif kind == "SQ":
                 nc.scalar.activation(
-                    out=y_sb[:, m, :], in_=o_ps[j][:], func=ACT.Relu,
+                    out=sd[:, sl], in_=vv[:, sl], func=ACT.Sqrt, bias=eps_t[:, 0:1], scale=1.0
+                )
+            elif kind == "rc":
+                nc.vector.reciprocal(out=rs_[:, sl], in_=sd[:, sl])
+            elif kind == "sc":
+                tt_v(scl[:, sl], rs_[:, sl], gw[:, sl], ALU.mult)
+            elif kind == "b2a":
+                tt_v(b2[:, sl], rs_[:, sl], qq[:, sl], ALU.mult)
+            else:
+                tt_v(b2[:, sl], b2[:, sl], gb[:, sl], ALU.add)
+
+        def y(m, eng):
+            if eng == SE:
+                nc.scalar.activation(
+                    out=y_sb[:, m, :], in_=o_ps[m][:], func=ACT.Relu,
                     bias=b2[:, m : m + 1], scale=scl[:, m : m + 1],
                 )
-            y_t = psum.tile([P, w], F32, name="yt%d" % m0, tag="bk%d" % m0)
-            for j in range(nb):
-                nc.tensor.transpose(y_t[:, P * j : P * (j + 1)], y_sb[:, m0 + j, :], ident[:])
-            nc.vector.tensor_tensor(
-                out=o_sb[:, c0 : c0 + w], in0=y_t[:], in1=x_sb[:, c0 : c0 + w], op=ALU.add
-            )
-            nc.sync.dma_start(out=out_f[:, c0 : c0 + w], in_=o_sb[:, c0 : c0 + w])
+            else:
+                nc.vector.tensor_scalar(
+                    out=y_sb[:, m, :], in0=o_ps[m][:], scalar1=scl[:, m : m + 1],
+                    scalar2=b2[:, m : m + 1], op0=ALU.mult, op1=ALU.add,
+                )
 
-        for i in range(n_units + 1):
-            if i < n_units:
-                regroup(i)
-                load(i + RAW_BUFS - 1)
-            if i >= 1:
-                quant(i - 1)
-                if i - 1 < N_POST:
-                    mm_post(i - 1)
-                    if i - 1 == N_POST - 1:
-                        h_chain()
-                else:
-                    stage2(i - 1)
+        def group_of(m):
+            for g, (m0, nb) in enumerate(GROUPS):
+                if m0 <= m < m0 + nb:
+                    return g
+            return -1
+
+        def tt(m):
+            g = group_of(m)
+            m0, nb = GROUPS[g]
+            if g not in y_t:
+                y_g = psum.tile([P, P * nb], F32, name="yt%d" % g, tag="bk%d" % m0)
+                y_t[g] = y_g
+            nc.tensor.transpose(y_t[g][:, P * (m - m0) : P * (m - m0 + 1)], y_sb[:, m, :], ident[:])
+
+        def ad(g):
+            m0, nb = GROUPS[g]
+            cols = slice(P * m0, P * (m0 + nb))
+            nc.vector.scalar_tensor_tensor(
+                out=o_sb[:, cols], in0=y_t[g][:], scalar=0.0, in1=x_sb[:, cols],
+                op0=ALU.max, op1=ALU.add,
+            )
+
+        def st_out(g):
+            m0, nb = GROUPS[g]
+            cols = slice(P * m0, P * (m0 + nb))
+            nc.sync.dma_start(out=out_f[:, cols], in_=o_sb[:, cols])
+
+        ld_par()
+        ld_x()
+        ld_agg(0)
+        ld_agg(1)
+        t_act(0)
+        par_t()
+        ld_w(0)
+        ae(0, SE)
+        t_act(1)
+        aq(0)
+        t_act(2)
+        ae(1, SE)
+        t_act(3)
+        ae(2, SE)
+        aq(1)
+        t_act(4)
+        ld_w(1)
+        ae(3, SE)
+        aq(2)
+        ae(4, SE)
+        aq(3)
+        aq(4)
+        par_v()
+        rs(0)
+        rv(0)
+        ld_w(2)
+        rv(1)
+        rs(1)
+        ld_w(3)
+        q(0)
+        rv(2)
+        rs(2)
+        mm(0, 1)
+        mm(0, 0)
+        mm(0, 3)
+        mm(0, 7)
+        ld_w(4)
+        mm(0, 6)
+        mm(0, 5)
+        mm(0, 2)
+        mm(0, 4)
+        q(1)
+        rv(3)
+        rs(3)
+        mm(1, 4)
+        mm(1, 7)
+        mm(1, 0)
+        ld_w(5)
+        mm(1, 1)
+        mm(1, 6)
+        mm(1, 2)
+        mm(1, 3)
+        mm(1, 5)
+        q(2)
+        rv(4)
+        rs(4)
+        mm(2, 7)
+        mm(2, 3)
+        ld_w(6)
+        mm(2, 6)
+        mm(2, 5)
+        mm(2, 4)
+        mm(2, 1)
+        mm(2, 0)
+        mm(2, 2)
+        q(3)
+        rv(5)
+        rs(5)
+        mm(3, 0)
+        ld_w(7)
+        mm(3, 3)
+        mm(3, 7)
+        mm(3, 1)
+        mm(3, 2)
+        mm(3, 5)
+        mm(3, 4)
+        mm(3, 6)
+        q(4)
+        rv(6)
+        rs(6)
+        ld_w(8)
+        mm(4, 2)
+        mm(4, 3)
+        mm(4, 7)
+        mm(4, 5)
+        mm(4, 6)
+        mm(4, 4)
+        mm(4, 0)
+        mm(4, 1)
+        q(5)
+        rv(7)
+        rs(7)
+        ld_w(9)
+        mm(5, 6)
+        mm(5, 4)
+        mm(5, 1)
+        mm(5, 2)
+        mm(5, 3)
+        mm(5, 7)
+        mm(5, 0)
+        mm(5, 5)
+        q(6)
+        rv(8)
+        ld_lin(0)
+        rs(8)
+        mm(6, 1)
+        mm(6, 4)
+        mm(6, 3)
+        mm(6, 5)
+        mm(6, 6)
+        mm(6, 0)
+        mm(6, 2)
+        mm(6, 7)
+        q(7)
+        rv(9)
+        rs(9)
+        mm(7, 6)
+        mm(7, 1)
+        mm(7, 3)
+        mm(7, 7)
+        ld_lin(1)
+        mm(7, 0)
+        mm(7, 2)
+        mm(7, 4)
+        mm(7, 5)
+        q(8)
+        r_lin(1, 1, 0, 64, VE)
+        r_lin(1, 0, 128, 256, SE)
+        r_lin(0, 0, 0, 256, VE)
+        mm(8, 5)
+        mm(8, 4)
+        mm(8, 6)
+        mm(8, 1)
+        mm(8, 0)
+        mm(8, 7)
+        mm(8, 2)
+        r_lin(1, 1, 64, 256, SE)
+        mm(8, 3)
+        q(9)
+        r_lin(0, 1, 32, 256, SE)
+        r_lin(1, 0, 0, 128, VE)
+        mm(9, 6)
+        mm(9, 0)
+        r_lin(0, 1, 0, 32, VE)
+        mm(9, 2)
+        mm(9, 4)
+        q_lin(1)
+        mm(9, 7)
+        mm(9, 5)
+        r_lin(3, 0, 0, 256, SE)
+        mm(9, 3)
+        mm(9, 1)
+        he(5, VE)
+        he(3, VE)
+        he(6, VE)
+        he(1, VE)
+        he(0, SE)
+        he(2, VE)
+        r_lin(2, 1, 0, 256, SE)
+        q_lin(0)
+        hr(0)
+        he(7, VE)
+        he(4, SE)
+        hq(0)
+        r_lin(2, 0, 0, 96, VE)
+        r_lin(2, 0, 96, 256, SE)
+        s2(0, 0)
+        hr(1)
+        s2(1, 0)
+        s2(2, 0)
+        s2(3, 0)
+        hq(1)
+        r_lin(3, 1, 0, 256, SE)
+        q_lin(2)
+        s2(1, 1)
+        s2(0, 1)
+        s2(2, 1)
+        s2(3, 1)
+        bs(1)
+        bs(0)
+        s2(5, 0)
+        s2(4, 0)
+        s2(4, 1)
+        ba(1)
+        s2(5, 1)
+        bs(3)
+        q_lin(3)
+        bs(4)
+        ba(0)
+        s2(7, 0)
+        ba(3)
+        s2(6, 0)
+        ba(4)
+        s2(6, 1)
+        bs(5)
+        s2(7, 1)
+        bs(2)
+        bs(7)
+        ba(2)
+        bs(6)
+        sm("d1", 0)
+        ba(5)
+        ba(6)
+        sm("d2", 0)
+        ba(7)
+        sm("v1", 0)
+        sm("d1", 1)
+        sm("sh", 0)
+        sm("v2", 0)
+        sm("d2", 1)
+        sm("qq", 0)
+        sm("SQ", 0)
+        sm("v1", 1)
+        sm("sh", 1)
+        sm("rc", 0)
+        sm("v2", 1)
+        sm("qq", 1)
+        sm("b2a", 0)
+        sm("SQ", 1)
+        sm("sc", 0)
+        sm("b2b", 0)
+        sm("rc", 1)
+        y(0, VE)
+        y(2, SE)
+        sm("b2a", 1)
+        y(1, VE)
+        y(3, SE)
+        tt(0)
+        tt(2)
+        sm("b2b", 1)
+        sm("sc", 1)
+        tt(1)
+        tt(3)
+        y(7, VE)
+        y(4, SE)
+        y(5, VE)
+        y(6, SE)
+        tt(7)
+        ad(0)
+        tt(4)
+        tt(5)
+        tt(6)
+        st_out(0)
+        ad(1)
+        st_out(1)

@@ -21,7 +21,10 @@ FLOPS = 2 * P * (KP * C + C * C)
 V_COLS = 496
 RAW_BUFS = 8
 LW = 256
-GROUPS = ((0, 4), (4, 4))
+NVT = 4
+SGRP = ((4, 2), (6, 2))
+ADG = ((0, 4), (4, 2), (6, 2))
+O_BANK = (2, 3, 4, 5, 6, 7, 0, 1)
 VE = 0
 SE = 1
 
@@ -40,7 +43,7 @@ def tile_gnnlayer_pb_kernel(
         one = keep.tile([P, 1], F32, name="one")
         nc.vector.memset(one[:], 1.0)
         one_s = keep.tile([P, 1], F32, name="one_s")
-        nc.scalar.activation(out=one_s[:], in_=one[:], func=ACT.Sqrt)
+        nc.scalar.activation(out=one_s[:], in_=one[:], func=ACT.Abs_reciprocal_sqrt)
         eps_t = keep.tile([P, 1], F32, name="eps_t")
         nc.vector.memset(eps_t[:], EPS_GN)
         par_raw = keep.tile([P, P], BF16, name="par_raw")
@@ -83,20 +86,26 @@ def tile_gnnlayer_pb_kernel(
         alpha = par[:, 32:40]
         a1 = keep.tile([P, 8], F32, name="a1")
         p1 = keep.tile([P, 8], F32, name="p1")
-        h_pl = keep.tile([P, 8, P], BF16, name="h_pl")
+        nal = keep.tile([P, 8], F32, name="nal")
         h_grp = keep.tile([P, 2, P, 4], BF16, name="h_grp", align_bytes=64)
         h_codes = keep.tile([P, 2, P], U32, name="h_codes", align_bytes=64)
         h_scales = keep.tile([P, 2, P], U8, name="h_scales", align_bytes=64)
         st = keep.tile([P, 8, 6], F32, name="st")
         mv = keep.tile([P, 8, 2], F32, name="mv")
-        shift = keep.tile([P, 8], F32, name="shift")
+        shift_v = keep.tile([P, 8], F32, name="shift_v")
         dd = keep.tile([P, 8], F32, name="dd")
         vv = keep.tile([P, 8], F32, name="vv")
         qq = keep.tile([P, 8], F32, name="qq")
-        sd = keep.tile([P, 8], F32, name="sd")
-        rs_ = keep.tile([P, 8], F32, name="rs_")
-        scl = keep.tile([P, 8], F32, name="scl")
-        b2 = keep.tile([P, 8], F32, name="b2")
+        rr_v = keep.tile([P, 8], F32, name="rr_v")
+        scl_v = keep.tile([P, 8], F32, name="scl_v")
+        b2_v = keep.tile([P, 8], F32, name="b2_v")
+        junk = keep.tile([P, P], BF16, name="junk")
+        ssum = keep.tile([P, 8], F32, name="ssum")
+        ssq = keep.tile([P, 8], F32, name="ssq")
+        shift_s = keep.tile([P, 8], F32, name="shift_s")
+        rr_s = keep.tile([P, 8], F32, name="rr_s")
+        scl_s = keep.tile([P, 8], F32, name="scl_s")
+        b2_s = keep.tile([P, 8], F32, name="b2_s")
         y_sb = keep.tile([P, 8, P], F32, name="y_sb")
         o_sb = keep.tile([P, C], F32, name="o_sb")
 
@@ -127,7 +136,7 @@ def tile_gnnlayer_pb_kernel(
             lraw[h] = r
 
         def t_act(b):
-            pt = psum.tile([P, 4, P], F32, name="pt%d" % b, tag="bk%d" % b)
+            pt = psum.tile([P, 4, P], F32, name="pt%d" % b, tag="bk%d" % (b + 2))
             for gg in range(2):
                 g = 2 * b + gg
                 words = x_w[:, g, :, :] if g < 2 else agg_w[:, g - 2, :, :]
@@ -159,6 +168,9 @@ def tile_gnnlayer_pb_kernel(
             nc.vector.tensor_scalar(
                 out=a1[:], in0=alpha, scalar1=-1.0, scalar2=1.0, op0=ALU.mult, op1=ALU.add
             )
+            nc.vector.tensor_scalar(
+                out=nal[:], in0=alpha, scalar1=-1.0 / P, scalar2=None, op0=ALU.mult
+            )
             nc.vector.tensor_tensor(out=p1[:], in0=a1[:], in1=blin, op=ALU.mult)
 
         def regroup_copy(eng, dst, src):
@@ -173,33 +185,41 @@ def tile_gnnlayer_pb_kernel(
                 grp[i] = g
             return grp[i]
 
+        def v_cols(i):
+            return 512 if i == N_POST - 1 else V_COLS
+
         def rv(i):
-            regroup_copy(VE, unit_grp(i)[:, 0:V_COLS, :], raw[i][:, :, 0:V_COLS])
+            regroup_copy(VE, unit_grp(i)[:, 0 : v_cols(i), :], raw[i][:, :, 0 : v_cols(i)])
 
         def rs(i):
-            regroup_copy(SE, unit_grp(i)[:, V_COLS:C, :], raw[i][:, :, V_COLS:C])
+            regroup_copy(SE, unit_grp(i)[:, v_cols(i) : C, :], raw[i][:, :, v_cols(i) : C])
 
-        def q(i):
-            cd = keep.tile([P, C], U32, name="wc%d" % i, align_bytes=64)
-            sc_ = keep.tile([P, C], U8, name="ws%d" % i, align_bytes=64)
+        def q(i, lo, hi):
+            if i not in codes:
+                cd = keep.tile([P, C], U32, name="wc%d" % i, align_bytes=64)
+                sc_ = keep.tile([P, C], U8, name="ws%d" % i, align_bytes=64)
+                codes[i] = cd
+                scales[i] = sc_
             nc.vector.quantize_mx(
-                out=cd[:].bitcast(FP8X4), scales=sc_[:], in_=grp[i][:].rearrange("p c t -> p (c t)")
+                out=codes[i][:, lo:hi].bitcast(FP8X4),
+                scales=scales[i][:, lo:hi],
+                in_=grp[i][:, lo:hi, :].rearrange("p c t -> p (c t)"),
             )
-            codes[i] = cd
-            scales[i] = sc_
 
         def mm(g, m):
-            if m not in acc:
-                acc_m = psum.tile([P, P], F32, name="acc%d" % m, tag="bk%d" % m)
-                acc[m] = acc_m
+            b = m // 4
+            t = m % 4
+            if b not in acc:
+                acc_b = psum.tile([P, 4, P], F32, name="acc%d" % b, tag="bk%d" % b)
+                acc[b] = acc_b
             nc.tensor.matmul_mx(
-                out=acc[m][:],
+                out=acc[b][:, t, :],
                 lhsT=codes[g][:, P * m : P * (m + 1)].bitcast(FP8X4),
                 lhsT_scale=scales[g][:, P * m : P * (m + 1)],
                 rhs=a_codes[:, P * g : P * (g + 1)].bitcast(FP8X4),
                 rhs_scale=a_scales[:, P * g : P * (g + 1)],
-                start=(g == 0),
-                stop=(g == N_POST - 1),
+                start=(g == 0 and t == 0),
+                stop=(g == N_POST - 1 and t == 3),
             )
 
         def r_lin(j, gg, lo, hi, eng):
@@ -224,20 +244,13 @@ def tile_gnnlayer_pb_kernel(
             lcodes[j] = cd
             lscales[j] = sc_
 
-        def he(m, eng):
-            if eng == SE:
-                nc.scalar.activation(
-                    out=h_pl[:, m, :], in_=acc[m][:], func=ACT.Identity,
-                    bias=bpost[:, m : m + 1], scale=1.0,
-                )
-            else:
-                nc.vector.tensor_scalar(
-                    out=h_pl[:, m, :], in0=acc[m][:], scalar1=bpost[:, m : m + 1],
-                    scalar2=None, op0=ALU.add,
-                )
-
-        def hr(gg):
-            regroup_copy(VE, h_grp[:, gg, :, :], h_pl[:, 4 * gg : 4 * gg + 4, :])
+        def hw(gg):
+            nc.vector.tensor_tensor(
+                out=h_grp[:, gg, :, :],
+                in0=acc[gg][:].rearrange("p t n -> p n t"),
+                in1=bpost[:, 4 * gg : 4 * gg + 4].unsqueeze(1).to_broadcast([P, P, 4]),
+                op=ALU.add,
+            )
 
         def hq(gg):
             nc.vector.quantize_mx(
@@ -248,7 +261,7 @@ def tile_gnnlayer_pb_kernel(
 
         def s2(m, gg):
             if m not in o_ps:
-                o_m = psum.tile([P, P], F32, name="o%d" % m, tag="bk%d" % m)
+                o_m = psum.tile([P, P], F32, name="o%d" % m, tag="bk%d" % O_BANK[m])
                 o_ps[m] = o_m
             j = (P * m) // LW
             k = (P * m) % LW
@@ -271,9 +284,11 @@ def tile_gnnlayer_pb_kernel(
         def tt_v(o, a, b, op):
             nc.vector.tensor_tensor(out=o, in0=a, in1=b, op=op)
 
-        def sm(kind, g):
-            m0, nb = GROUPS[g]
-            sl = slice(m0, m0 + nb)
+        def rsqrt_s(o, a, scale):
+            nc.scalar.activation(out=o, in_=a, func=ACT.Abs_reciprocal_sqrt, bias=eps_t[:, 0:1], scale=scale)
+
+        def sm(kind):
+            sl = slice(0, NVT)
             mean = mv[:, sl, 0]
             var = mv[:, sl, 1]
             if kind == "d1":
@@ -285,50 +300,83 @@ def tile_gnnlayer_pb_kernel(
             elif kind == "v2":
                 tt_v(vv[:, sl], vv[:, sl], var, ALU.add)
             elif kind == "sh":
-                tt_v(shift[:, sl], dd[:, sl], mean, ALU.subtract)
+                tt_v(shift_v[:, sl], dd[:, sl], mean, ALU.subtract)
             elif kind == "qq":
-                tt_v(qq[:, sl], shift[:, sl], gw[:, sl], ALU.mult)
-            elif kind == "SQ":
-                nc.scalar.activation(
-                    out=sd[:, sl], in_=vv[:, sl], func=ACT.Sqrt, bias=eps_t[:, 0:1], scale=1.0
-                )
-            elif kind == "rc":
-                nc.vector.reciprocal(out=rs_[:, sl], in_=sd[:, sl])
+                tt_v(qq[:, sl], shift_v[:, sl], gw[:, sl], ALU.mult)
+            elif kind == "RRv":
+                rsqrt_s(rr_v[:, sl], vv[:, sl], 1.0)
             elif kind == "sc":
-                tt_v(scl[:, sl], rs_[:, sl], gw[:, sl], ALU.mult)
+                tt_v(scl_v[:, sl], rr_v[:, sl], gw[:, sl], ALU.mult)
             elif kind == "b2a":
-                tt_v(b2[:, sl], rs_[:, sl], qq[:, sl], ALU.mult)
+                tt_v(b2_v[:, sl], rr_v[:, sl], qq[:, sl], ALU.mult)
             else:
-                tt_v(b2[:, sl], b2[:, sl], gb[:, sl], ALU.add)
+                tt_v(b2_v[:, sl], b2_v[:, sl], gb[:, sl], ALU.add)
+
+        def col(t, m):
+            return t[:, m : m + 1]
+
+        def p1_s(m):
+            nc.scalar.activation(
+                out=junk[:], in_=o_ps[m][:], func=ACT.Identity, accum_out=col(ssum, m)
+            )
+
+        def sh_s(m):
+            nc.scalar.activation(
+                out=col(shift_s, m), in_=col(ssum, m), func=ACT.Identity,
+                bias=col(p1, m), scale=col(nal, m),
+            )
+
+        def p2_s(m):
+            nc.scalar.activation(
+                out=junk[:], in_=o_ps[m][:], func=ACT.Square, bias=col(shift_s, m), scale=1.0,
+                accum_out=col(ssq, m),
+            )
+
+        def rr_sg(k):
+            m0, nb = SGRP[k]
+            rsqrt_s(rr_s[:, m0 : m0 + nb], ssq[:, m0 : m0 + nb], 1.0 / P)
+
+        def sc_s(m):
+            nc.scalar.activation(
+                out=col(scl_s, m), in_=col(rr_s, m), func=ACT.Copy, scale=gw[:, m : m + 1]
+            )
+
+        def b2_sm(m):
+            nc.scalar.activation(
+                out=col(b2_s, m), in_=col(shift_s, m), func=ACT.Identity,
+                bias=gb[:, m : m + 1], scale=col(scl_s, m),
+            )
 
         def y(m, eng):
+            sc_t = scl_v if m < NVT else scl_s
+            b2_t = b2_v if m < NVT else b2_s
             if eng == SE:
                 nc.scalar.activation(
                     out=y_sb[:, m, :], in_=o_ps[m][:], func=ACT.Relu,
-                    bias=b2[:, m : m + 1], scale=scl[:, m : m + 1],
+                    bias=col(b2_t, m), scale=col(sc_t, m),
                 )
             else:
                 nc.vector.tensor_scalar(
-                    out=y_sb[:, m, :], in0=o_ps[m][:], scalar1=scl[:, m : m + 1],
-                    scalar2=b2[:, m : m + 1], op0=ALU.mult, op1=ALU.add,
+                    out=y_sb[:, m, :], in0=o_ps[m][:], scalar1=col(sc_t, m),
+                    scalar2=col(b2_t, m), op0=ALU.mult, op1=ALU.add,
                 )
 
         def group_of(m):
-            for g, (m0, nb) in enumerate(GROUPS):
+            for g, (m0, nb) in enumerate(ADG):
                 if m0 <= m < m0 + nb:
                     return g
             return -1
 
         def tt(m):
             g = group_of(m)
-            m0, nb = GROUPS[g]
+            m0, nb = ADG[g]
             if g not in y_t:
-                y_g = psum.tile([P, P * nb], F32, name="yt%d" % g, tag="bk%d" % m0)
+                y_g = psum.tile([P, P * nb], F32, name="yt%d" % g, tag="bk%d" % O_BANK[m0])
                 y_t[g] = y_g
             nc.tensor.transpose(y_t[g][:, P * (m - m0) : P * (m - m0 + 1)], y_sb[:, m, :], ident[:])
 
         def ad(g):
-            m0, nb = GROUPS[g]
+            m0, nb = ADG[g]
             cols = slice(P * m0, P * (m0 + nb))
             nc.vector.scalar_tensor_tensor(
                 out=o_sb[:, cols], in0=y_t[g][:], scalar=0.0, in1=x_sb[:, cols],
@@ -336,7 +384,7 @@ def tile_gnnlayer_pb_kernel(
             )
 
         def st_out(g):
-            m0, nb = GROUPS[g]
+            m0, nb = ADG[g]
             cols = slice(P * m0, P * (m0 + nb))
             nc.sync.dma_start(out=out_f[:, cols], in_=o_sb[:, cols])
 
@@ -349,239 +397,237 @@ def tile_gnnlayer_pb_kernel(
         ld_w(0)
         ae(0, SE)
         t_act(1)
-        aq(0)
         t_act(2)
+        aq(0)
         ae(1, SE)
         t_act(3)
+        ld_w(1)
+        t_act(4)
         ae(2, SE)
         aq(1)
-        t_act(4)
-        ld_w(1)
         ae(3, SE)
         aq(2)
         ae(4, SE)
         aq(3)
-        aq(4)
-        par_v()
         rs(0)
         rv(0)
         ld_w(2)
+        aq(4)
+        par_v()
         rv(1)
         rs(1)
         ld_w(3)
-        q(0)
+        q(0, 0, 1024)
         rv(2)
         rs(2)
-        mm(0, 1)
-        mm(0, 0)
-        mm(0, 3)
-        mm(0, 7)
         ld_w(4)
-        mm(0, 6)
-        mm(0, 5)
+        mm(0, 0)
+        mm(0, 1)
         mm(0, 2)
+        mm(0, 3)
         mm(0, 4)
-        q(1)
+        mm(0, 5)
+        mm(0, 6)
+        mm(0, 7)
+        q(1, 0, 1024)
         rv(3)
-        rs(3)
-        mm(1, 4)
-        mm(1, 7)
-        mm(1, 0)
         ld_w(5)
+        rs(3)
+        mm(1, 0)
         mm(1, 1)
-        mm(1, 6)
         mm(1, 2)
         mm(1, 3)
+        mm(1, 4)
         mm(1, 5)
-        q(2)
+        mm(1, 6)
+        mm(1, 7)
+        q(2, 0, 1024)
         rv(4)
-        rs(4)
-        mm(2, 7)
-        mm(2, 3)
         ld_w(6)
-        mm(2, 6)
-        mm(2, 5)
-        mm(2, 4)
-        mm(2, 1)
+        rs(4)
         mm(2, 0)
+        mm(2, 1)
         mm(2, 2)
-        q(3)
+        mm(2, 3)
+        mm(2, 4)
+        mm(2, 5)
+        mm(2, 6)
+        mm(2, 7)
+        q(3, 0, 1024)
+        ld_w(7)
         rv(5)
         rs(5)
         mm(3, 0)
-        ld_w(7)
-        mm(3, 3)
-        mm(3, 7)
         mm(3, 1)
         mm(3, 2)
-        mm(3, 5)
+        mm(3, 3)
         mm(3, 4)
+        mm(3, 5)
         mm(3, 6)
-        q(4)
+        mm(3, 7)
+        q(4, 0, 1024)
+        ld_w(8)
         rv(6)
         rs(6)
-        ld_w(8)
-        mm(4, 2)
-        mm(4, 3)
-        mm(4, 7)
-        mm(4, 5)
-        mm(4, 6)
-        mm(4, 4)
         mm(4, 0)
         mm(4, 1)
-        q(5)
+        mm(4, 2)
+        mm(4, 3)
+        mm(4, 4)
+        mm(4, 5)
+        mm(4, 6)
+        mm(4, 7)
+        q(5, 0, 1024)
+        ld_w(9)
         rv(7)
         rs(7)
-        ld_w(9)
-        mm(5, 6)
-        mm(5, 4)
+        mm(5, 0)
         mm(5, 1)
         mm(5, 2)
         mm(5, 3)
-        mm(5, 7)
-        mm(5, 0)
+        mm(5, 4)
         mm(5, 5)
-        q(6)
-        rv(8)
+        mm(5, 6)
+        mm(5, 7)
+        q(6, 0, 1024)
         ld_lin(0)
+        rv(8)
         rs(8)
+        mm(6, 0)
         mm(6, 1)
-        mm(6, 4)
+        mm(6, 2)
         mm(6, 3)
+        mm(6, 4)
         mm(6, 5)
         mm(6, 6)
-        mm(6, 0)
-        mm(6, 2)
         mm(6, 7)
-        q(7)
+        q(7, 0, 1024)
         rv(9)
-        rs(9)
-        mm(7, 6)
-        mm(7, 1)
-        mm(7, 3)
-        mm(7, 7)
         ld_lin(1)
+        rs(9)
         mm(7, 0)
+        mm(7, 1)
         mm(7, 2)
+        mm(7, 3)
         mm(7, 4)
         mm(7, 5)
-        q(8)
-        r_lin(1, 1, 0, 64, VE)
-        r_lin(1, 0, 128, 256, SE)
-        r_lin(0, 0, 0, 256, VE)
-        mm(8, 5)
-        mm(8, 4)
-        mm(8, 6)
-        mm(8, 1)
+        mm(7, 6)
+        mm(7, 7)
+        q(8, 0, 1024)
+        q(9, 0, 512)
+        r_lin(1, 0, 160, 256, SE)
         mm(8, 0)
-        mm(8, 7)
+        mm(8, 1)
         mm(8, 2)
-        r_lin(1, 1, 64, 256, SE)
+        q(9, 512, 1024)
         mm(8, 3)
-        q(9)
+        r_lin(0, 0, 224, 256, SE)
+        mm(8, 4)
+        mm(8, 5)
+        mm(8, 6)
         r_lin(0, 1, 32, 256, SE)
-        r_lin(1, 0, 0, 128, VE)
-        mm(9, 6)
+        mm(8, 7)
         mm(9, 0)
-        r_lin(0, 1, 0, 32, VE)
-        mm(9, 2)
-        mm(9, 4)
-        q_lin(1)
-        mm(9, 7)
-        mm(9, 5)
-        r_lin(3, 0, 0, 256, SE)
-        mm(9, 3)
         mm(9, 1)
-        he(5, VE)
-        he(3, VE)
-        he(6, VE)
-        he(1, VE)
-        he(0, SE)
-        he(2, VE)
-        r_lin(2, 1, 0, 256, SE)
-        q_lin(0)
-        hr(0)
-        he(7, VE)
-        he(4, SE)
-        hq(0)
+        mm(9, 2)
+        r_lin(1, 0, 0, 160, VE)
+        mm(9, 3)
+        mm(9, 4)
+        r_lin(0, 1, 0, 32, VE)
+        mm(9, 5)
+        mm(9, 6)
+        mm(9, 7)
+        r_lin(0, 0, 0, 224, VE)
+        r_lin(1, 1, 0, 256, SE)
+        hw(0)
         r_lin(2, 0, 0, 96, VE)
-        r_lin(2, 0, 96, 256, SE)
-        s2(0, 0)
-        hr(1)
-        s2(1, 0)
-        s2(2, 0)
-        s2(3, 0)
+        r_lin(3, 0, 0, 256, SE)
+        hq(0)
+        hw(1)
+        r_lin(3, 1, 0, 32, VE)
+        q_lin(0)
+        r_lin(3, 1, 32, 256, SE)
         hq(1)
-        r_lin(3, 1, 0, 256, SE)
-        q_lin(2)
+        q_lin(1)
+        s2(1, 0)
+        s2(0, 0)
+        r_lin(2, 1, 0, 256, SE)
         s2(1, 1)
         s2(0, 1)
+        q_lin(3)
+        s2(2, 0)
         s2(2, 1)
+        s2(3, 0)
         s2(3, 1)
         bs(1)
+        r_lin(2, 0, 96, 256, SE)
         bs(0)
-        s2(5, 0)
-        s2(4, 0)
-        s2(4, 1)
-        ba(1)
-        s2(5, 1)
-        bs(3)
-        q_lin(3)
-        bs(4)
-        ba(0)
         s2(7, 0)
-        ba(3)
-        s2(6, 0)
-        ba(4)
-        s2(6, 1)
-        bs(5)
         s2(7, 1)
         bs(2)
-        bs(7)
+        s2(6, 0)
+        s2(6, 1)
+        bs(3)
+        ba(0)
+        ba(1)
+        p1_s(7)
         ba(2)
-        bs(6)
-        sm("d1", 0)
-        ba(5)
-        ba(6)
-        sm("d2", 0)
-        ba(7)
-        sm("v1", 0)
-        sm("d1", 1)
-        sm("sh", 0)
-        sm("v2", 0)
-        sm("d2", 1)
-        sm("qq", 0)
-        sm("SQ", 0)
-        sm("v1", 1)
-        sm("sh", 1)
-        sm("rc", 0)
-        sm("v2", 1)
-        sm("qq", 1)
-        sm("b2a", 0)
-        sm("SQ", 1)
-        sm("sc", 0)
-        sm("b2b", 0)
-        sm("rc", 1)
-        y(0, VE)
-        y(2, SE)
-        sm("b2a", 1)
-        y(1, VE)
-        y(3, SE)
-        tt(0)
-        tt(2)
-        sm("b2b", 1)
-        sm("sc", 1)
-        tt(1)
-        tt(3)
-        y(7, VE)
-        y(4, SE)
-        y(5, VE)
-        y(6, SE)
-        tt(7)
-        ad(0)
-        tt(4)
-        tt(5)
+        ba(3)
+        p1_s(6)
+        q_lin(2)
+        sh_s(7)
+        sh_s(6)
+        sm("d1")
+        p2_s(7)
+        s2(5, 0)
+        p2_s(6)
+        sm("d2")
+        s2(5, 1)
+        s2(4, 0)
+        s2(4, 1)
+        sm("sh")
+        sm("v1")
+        rr_sg(1)
+        p1_s(5)
+        sm("qq")
+        sm("v2")
+        p1_s(4)
+        sc_s(6)
+        sh_s(5)
+        sc_s(7)
+        sm("RRv")
+        sh_s(4)
+        b2_sm(6)
+        p2_s(5)
+        sm("b2a")
+        b2_sm(7)
+        sm("sc")
+        p2_s(4)
+        y(6, VE)
+        sm("b2b")
+        y(7, SE)
+        rr_sg(0)
         tt(6)
-        st_out(0)
+        y(2, VE)
+        y(3, SE)
+        y(0, VE)
+        tt(7)
+        sc_s(4)
+        sc_s(5)
+        y(1, VE)
+        tt(2)
+        tt(3)
+        b2_sm(4)
+        b2_sm(5)
+        tt(0)
+        ad(2)
+        tt(1)
+        y(5, SE)
+        y(4, VE)
+        st_out(2)
+        ad(0)
+        tt(5)
+        tt(4)
         ad(1)
+        st_out(0)
         st_out(1)

@@ -18,8 +18,8 @@ N_POST = KP // 512
 EPS_GN = 1e-5
 FLOPS = 2 * P * (KP * C + C * C)
 
-V_COLS = 496
-RAW_BUFS = 8
+V_COLS = 464
+RAW_BUFS = 7
 LW = 256
 NVT = 4
 SGRP = ((4, 2), (6, 2))
@@ -36,9 +36,9 @@ def tile_gnnlayer_pb_kernel(
     with ExitStack() as ctx:
         keep = ctx.enter_context(tc.tile_pool(name="keep", bufs=1))
         rawp = ctx.enter_context(tc.tile_pool(name="rawp", bufs=RAW_BUFS))
-        grpp = ctx.enter_context(tc.tile_pool(name="grpp", bufs=3))
+        grpp = ctx.enter_context(tc.tile_pool(name="grpp", bufs=4))
         psum = ctx.enter_context(tc.psum_pool(name="psum", bufs=1))
-        ctx.enter_context(tc.manual_schedule())
+        pass
 
         one = keep.tile([P, 1], F32, name="one")
         nc.vector.memset(one[:], 1.0)
@@ -156,6 +156,13 @@ def tile_gnnlayer_pb_kernel(
                 out=a_codes[:, 256 * b : 256 * (b + 1)].bitcast(FP8X4),
                 scales=a_scales[:, 256 * b : 256 * (b + 1)],
                 in_=a_grp[:, 1024 * b : 1024 * (b + 1)],
+            )
+
+        def aq_agg():
+            nc.vector.quantize_mx(
+                out=a_codes[:, 256:1280].bitcast(FP8X4),
+                scales=a_scales[:, 256:1280],
+                in_=a_grp[:, 1024:5120],
             )
 
         def par_t():
@@ -404,26 +411,23 @@ def tile_gnnlayer_pb_kernel(
         ld_w(1)
         t_act(4)
         ae(2, SE)
-        aq(1)
         ae(3, SE)
-        aq(2)
         ae(4, SE)
-        aq(3)
         rs(0)
         rv(0)
         ld_w(2)
-        aq(4)
+        aq_agg()
         par_v()
         rv(1)
-        rs(1)
         ld_w(3)
+        rs(1)
         q(0, 0, 1024)
         rv(2)
-        rs(2)
         ld_w(4)
         mm(0, 0)
         mm(0, 1)
         mm(0, 2)
+        rs(2)
         mm(0, 3)
         mm(0, 4)
         mm(0, 5)
@@ -432,19 +436,18 @@ def tile_gnnlayer_pb_kernel(
         q(1, 0, 1024)
         rv(3)
         ld_w(5)
-        rs(3)
         mm(1, 0)
         mm(1, 1)
         mm(1, 2)
         mm(1, 3)
         mm(1, 4)
         mm(1, 5)
+        rs(3)
         mm(1, 6)
         mm(1, 7)
         q(2, 0, 1024)
         rv(4)
         ld_w(6)
-        rs(4)
         mm(2, 0)
         mm(2, 1)
         mm(2, 2)
@@ -453,10 +456,10 @@ def tile_gnnlayer_pb_kernel(
         mm(2, 5)
         mm(2, 6)
         mm(2, 7)
+        rs(4)
         q(3, 0, 1024)
         ld_w(7)
         rv(5)
-        rs(5)
         mm(3, 0)
         mm(3, 1)
         mm(3, 2)
@@ -465,10 +468,10 @@ def tile_gnnlayer_pb_kernel(
         mm(3, 5)
         mm(3, 6)
         mm(3, 7)
+        rs(5)
         q(4, 0, 1024)
         ld_w(8)
         rv(6)
-        rs(6)
         mm(4, 0)
         mm(4, 1)
         mm(4, 2)
@@ -477,10 +480,10 @@ def tile_gnnlayer_pb_kernel(
         mm(4, 5)
         mm(4, 6)
         mm(4, 7)
+        rs(6)
         q(5, 0, 1024)
         ld_w(9)
         rv(7)
-        rs(7)
         mm(5, 0)
         mm(5, 1)
         mm(5, 2)
@@ -489,10 +492,10 @@ def tile_gnnlayer_pb_kernel(
         mm(5, 5)
         mm(5, 6)
         mm(5, 7)
+        rs(7)
         q(6, 0, 1024)
         ld_lin(0)
         rv(8)
-        rs(8)
         mm(6, 0)
         mm(6, 1)
         mm(6, 2)
@@ -501,133 +504,129 @@ def tile_gnnlayer_pb_kernel(
         mm(6, 5)
         mm(6, 6)
         mm(6, 7)
-        q(7, 0, 1024)
+        rs(8)
         rv(9)
         ld_lin(1)
+        q(7, 0, 1024)
         rs(9)
+        q(9, 0, 512)
         mm(7, 0)
         mm(7, 1)
         mm(7, 2)
+        q(8, 0, 1024)
         mm(7, 3)
         mm(7, 4)
         mm(7, 5)
         mm(7, 6)
         mm(7, 7)
-        q(8, 0, 1024)
-        q(9, 0, 512)
-        r_lin(1, 0, 160, 256, SE)
+        r_lin(0, 0, 0, 256, VE)
         mm(8, 0)
+        r_lin(0, 1, 0, 256, SE)
         mm(8, 1)
+        mm(9, 0)
         mm(8, 2)
-        q(9, 512, 1024)
+        r_lin(1, 0, 0, 256, VE)
+        mm(9, 1)
         mm(8, 3)
-        r_lin(0, 0, 224, 256, SE)
+        mm(9, 2)
         mm(8, 4)
+        mm(9, 3)
         mm(8, 5)
         mm(8, 6)
-        r_lin(0, 1, 32, 256, SE)
         mm(8, 7)
-        mm(9, 0)
-        mm(9, 1)
-        mm(9, 2)
-        r_lin(1, 0, 0, 160, VE)
-        mm(9, 3)
+        q(9, 512, 1024)
+        r_lin(1, 1, 0, 256, SE)
+        hw(0)
         mm(9, 4)
-        r_lin(0, 1, 0, 32, VE)
         mm(9, 5)
         mm(9, 6)
         mm(9, 7)
-        r_lin(0, 0, 0, 224, VE)
-        r_lin(1, 1, 0, 256, SE)
-        hw(0)
-        r_lin(2, 0, 0, 96, VE)
-        r_lin(3, 0, 0, 256, SE)
+        q_lin(0)
+        r_lin(2, 0, 0, 256, SE)
         hq(0)
         hw(1)
-        r_lin(3, 1, 0, 32, VE)
-        q_lin(0)
-        r_lin(3, 1, 32, 256, SE)
-        hq(1)
-        q_lin(1)
-        s2(1, 0)
         s2(0, 0)
+        s2(1, 0)
+        q_lin(1)
         r_lin(2, 1, 0, 256, SE)
-        s2(1, 1)
-        s2(0, 1)
-        q_lin(3)
+        hq(1)
         s2(2, 0)
-        s2(2, 1)
         s2(3, 0)
+        s2(0, 1)
+        s2(1, 1)
+        r_lin(3, 0, 0, 256, SE)
+        s2(2, 1)
         s2(3, 1)
-        bs(1)
-        r_lin(2, 0, 96, 256, SE)
+        q_lin(2)
         bs(0)
-        s2(7, 0)
-        s2(7, 1)
+        r_lin(3, 1, 0, 256, SE)
+        bs(1)
+        s2(4, 0)
+        s2(5, 0)
         bs(2)
-        s2(6, 0)
-        s2(6, 1)
+        s2(4, 1)
+        s2(5, 1)
         bs(3)
         ba(0)
         ba(1)
-        p1_s(7)
         ba(2)
         ba(3)
-        p1_s(6)
-        q_lin(2)
-        sh_s(7)
-        sh_s(6)
-        sm("d1")
-        p2_s(7)
-        s2(5, 0)
-        p2_s(6)
-        sm("d2")
-        s2(5, 1)
-        s2(4, 0)
-        s2(4, 1)
-        sm("sh")
-        sm("v1")
-        rr_sg(1)
-        p1_s(5)
-        sm("qq")
-        sm("v2")
         p1_s(4)
-        sc_s(6)
-        sh_s(5)
-        sc_s(7)
-        sm("RRv")
+        p1_s(5)
+        sm("d1")
+        q_lin(3)
         sh_s(4)
-        b2_sm(6)
-        p2_s(5)
-        sm("b2a")
-        b2_sm(7)
-        sm("sc")
+        sh_s(5)
         p2_s(4)
-        y(6, VE)
-        sm("b2b")
-        y(7, SE)
+        sm("d2")
+        p2_s(5)
+        s2(6, 0)
+        sm("v1")
+        s2(7, 0)
+        sm("sh")
+        s2(6, 1)
+        s2(7, 1)
+        sm("v2")
         rr_sg(0)
-        tt(6)
-        y(2, VE)
-        y(3, SE)
-        y(0, VE)
-        tt(7)
+        sm("qq")
+        p1_s(6)
+        p1_s(7)
+        sm("RRv")
+        sh_s(6)
         sc_s(4)
         sc_s(5)
-        y(1, VE)
-        tt(2)
-        tt(3)
+        sh_s(7)
+        sm("b2a")
+        p2_s(6)
+        sm("sc")
+        p2_s(7)
+        sm("b2b")
         b2_sm(4)
         b2_sm(5)
-        tt(0)
-        ad(2)
-        tt(1)
+        y(0, VE)
+        y(3, SE)
+        y(1, VE)
+        rr_sg(1)
         y(5, SE)
+        y(2, VE)
+        tt(0)
         y(4, VE)
-        st_out(2)
-        ad(0)
+        tt(3)
+        sc_s(6)
+        sc_s(7)
+        tt(1)
         tt(5)
+        b2_sm(6)
+        tt(2)
+        b2_sm(7)
         tt(4)
+        y(6, VE)
+        y(7, SE)
+        ad(0)
+        tt(6)
+        tt(7)
         ad(1)
         st_out(0)
+        ad(2)
         st_out(1)
+        st_out(2)

@@ -12,21 +12,24 @@ ALU = mybir.AluOpType
 ACT = mybir.ActivationFunctionType
 
 P = 128
+PACK = 4
+K_PASS = P * PACK
 C = 1024
-KP = 5 * C
-N_POST = KP // 512
+K_POST = 5 * C
+N_POST = K_POST // K_PASS
+N_LIN = C // K_PASS
+N_TILES = C // P
+HALF = N_TILES // 2
 EPS_GN = 1e-5
-FLOPS = 2 * P * (KP * C + C * C)
+FLOPS = 2 * P * (K_POST * C + C * C)
 
-V_COLS = 464
+V_COLS = 496
 RAW_BUFS = 7
-LW = 256
-NVT = 4
-SGRP = ((4, 2), (6, 2))
-ADG = ((0, 4), (4, 2), (6, 2))
+GRP_BUFS = 4
+LIN_COLS = 256
+N_PIECES = C // LIN_COLS
+LIN_ON_VECTOR = ((0, 0), (1, 0))
 O_BANK = (2, 3, 4, 5, 6, 7, 0, 1)
-VE = 0
-SE = 1
 
 
 def tile_gnnlayer_pb_kernel(
@@ -35,19 +38,19 @@ def tile_gnnlayer_pb_kernel(
     nc = tc.nc
     with ExitStack() as ctx:
         keep = ctx.enter_context(tc.tile_pool(name="keep", bufs=1))
-        rawp = ctx.enter_context(tc.tile_pool(name="rawp", bufs=RAW_BUFS))
-        grpp = ctx.enter_context(tc.tile_pool(name="grpp", bufs=4))
+        raw_pool = ctx.enter_context(tc.tile_pool(name="raw_pool", bufs=RAW_BUFS))
+        grp_pool = ctx.enter_context(tc.tile_pool(name="grp_pool", bufs=GRP_BUFS))
         psum = ctx.enter_context(tc.psum_pool(name="psum", bufs=1))
-        pass
+
 
         one = keep.tile([P, 1], F32, name="one")
         nc.vector.memset(one[:], 1.0)
-        one_s = keep.tile([P, 1], F32, name="one_s")
-        nc.scalar.activation(out=one_s[:], in_=one[:], func=ACT.Abs_reciprocal_sqrt)
-        eps_t = keep.tile([P, 1], F32, name="eps_t")
-        nc.vector.memset(eps_t[:], EPS_GN)
-        par_raw = keep.tile([P, P], BF16, name="par_raw")
-        nc.vector.memset(par_raw[:], 0.0)
+        warm = keep.tile([P, 1], F32, name="warm")
+        nc.scalar.activation(out=warm[:], in_=one[:], func=ACT.Abs_reciprocal_sqrt)
+        eps = keep.tile([P, 1], F32, name="eps")
+        nc.vector.memset(eps[:], EPS_GN)
+        par_rows = keep.tile([P, P], BF16, name="par_rows")
+        nc.vector.memset(par_rows[:], 0.0)
         ident = keep.tile([P, P], F32, name="ident")
         make_identity(nc, ident[:])
         ident_bf = keep.tile([P, P], BF16, name="ident_bf")
@@ -55,578 +58,327 @@ def tile_gnnlayer_pb_kernel(
 
         x_sb = keep.tile([P, C], BF16, name="x_sb")
         agg_sb = keep.tile([P, 4 * C], BF16, name="agg_sb")
-        agg_f = agg.rearrange("b n c -> (b n) c")
-        out_f = out.rearrange("b n c -> (b n) c")
-        lin_v = W_lin.rearrange("(a p) n -> p a n", p=P)
+        agg_rows = agg.rearrange("b n c -> (b n) c")
+        out_rows = out.rearrange("b n c -> (b n) c")
+        nc.sync.dma_start(out=x_sb[:], in_=x.rearrange("b n c -> (b n) c"))
+        for h in range(2):
+            cols = slice(2 * C * h, 2 * C * (h + 1))
+            nc.sync.dma_start(out=agg_sb[:, cols], in_=agg_rows[:, cols])
+        for v, vec in enumerate((b_post, b_lin, gn_weight, gn_bias, gn_alpha)):
+            nc.scalar.dma_start(
+                out=par_rows[N_TILES * v : N_TILES * (v + 1), :],
+                in_=vec.rearrange("(t p) -> t p", p=P),
+            )
 
-        raw = {}
-        grp = {}
-        codes = {}
-        scales = {}
-        lraw = {}
-        lgrp = {}
-        lcodes = {}
-        lscales = {}
-        pts = {}
-        acc = {}
-        o_ps = {}
-        y_t = {}
+        raw = []
 
-        x_w = x_sb[:].bitcast(F32).rearrange("n (g p u) -> n g p u", p=P, u=2)
-        agg_w = agg_sb[:].bitcast(F32).rearrange("n (g p u) -> n g p u", p=P, u=2)
-        a_grp = keep.tile([P, N_POST * 512], BF16, name="a_grp", align_bytes=64)
+        def load_next():
+            i = len(raw)
+            if i < N_POST:
+                r = raw_pool.tile([P, PACK, C], BF16, name="raw%d" % i, tag="raw")
+                rows = W_post[K_PASS * i : K_PASS * (i + 1), :]
+                nc.sync.dma_start(out=r[:], in_=rows.rearrange("(p j) c -> p j c", j=PACK))
+                raw.append(r)
+            elif i < N_POST + 2:
+                h = i - N_POST
+                r = raw_pool.tile([P, N_LIN * PACK, C // 2], BF16, name="raw%d" % i, tag="raw")
+                nc.sync.dma_start(
+                    out=r[:],
+                    in_=W_lin.rearrange("(a p) n -> p a n", p=P)[:, :, (C // 2) * h : (C // 2) * (h + 1)],
+                )
+                raw.append(r)
+
+        for i in range(RAW_BUFS - 1):
+            load_next()
+
+        def regroup(copy, dst, src):
+            copy(
+                out=dst.rearrange("p (c i) t -> p c t i", i=4),
+                in_=src.rearrange("p t (c i) -> p c t i", i=4),
+            )
+
+        def quantise(codes, scales, grouped):
+            nc.vector.quantize_mx(out=codes.bitcast(FP8X4), scales=scales, in_=grouped)
+
+        x_words = x_sb[:].bitcast(F32).rearrange("n (g p u) -> n g p u", p=P, u=2)
+        agg_words = agg_sb[:].bitcast(F32).rearrange("n (g p u) -> n g p u", p=P, u=2)
+        a_grp = keep.tile([P, N_POST * K_PASS], BF16, name="a_grp", align_bytes=64)
         a_codes = keep.tile([P, N_POST * P], U32, name="a_codes", align_bytes=64)
         a_scales = keep.tile([P, N_POST * P], U8, name="a_scales", align_bytes=64)
-        a_grp_w = a_grp[:].bitcast(F32)
-        par = keep.tile([P, 40], F32, name="par")
+        a_grp_words = a_grp[:].bitcast(F32)
+        for b in range(N_POST // 2):
+            turned = psum.tile([P, 4, P], F32, name="turned%d" % b, tag="bank%d" % (b + 2))
+            for j in range(4):
+                g = 2 * b + j // 2
+                words = x_words[:, g, :, :] if g < 2 else agg_words[:, g - 2, :, :]
+                nc.tensor.transpose(turned[:, j, :], words[:, :, j % 2], ident[:])
+            nc.scalar.copy(
+                out=a_grp_words[:, 512 * b : 512 * (b + 1)].rearrange(
+                    "p (g n u) -> p g n u", g=2, u=2
+                ),
+                in_=turned[:].rearrange("p (g u) n -> p g n u", u=2),
+            )
+            if b == 0:
+                quantise(a_codes[:, 0:256], a_scales[:, 0:256], a_grp[:, 0:1024])
+        quantise(a_codes[:, 256:1280], a_scales[:, 256:1280], a_grp[:, 1024:5120])
+
+        par_t = psum.tile([P, P], BF16, name="par_t", tag="bank7")
+        nc.tensor.transpose(par_t[:], par_rows[:], ident_bf[:])
+        par = keep.tile([P, 5 * N_TILES], F32, name="par")
+        nc.vector.tensor_copy(out=par[:], in_=par_t[:, 0 : 5 * N_TILES])
         bpost = par[:, 0:8]
         blin = par[:, 8:16]
         gw = par[:, 16:24]
         gb = par[:, 24:32]
         alpha = par[:, 32:40]
-        a1 = keep.tile([P, 8], F32, name="a1")
-        p1 = keep.tile([P, 8], F32, name="p1")
-        nal = keep.tile([P, 8], F32, name="nal")
-        h_grp = keep.tile([P, 2, P, 4], BF16, name="h_grp", align_bytes=64)
-        h_codes = keep.tile([P, 2, P], U32, name="h_codes", align_bytes=64)
-        h_scales = keep.tile([P, 2, P], U8, name="h_scales", align_bytes=64)
-        st = keep.tile([P, 8, 6], F32, name="st")
-        mv = keep.tile([P, 8, 2], F32, name="mv")
-        shift_v = keep.tile([P, 8], F32, name="shift_v")
-        dd = keep.tile([P, 8], F32, name="dd")
-        vv = keep.tile([P, 8], F32, name="vv")
-        qq = keep.tile([P, 8], F32, name="qq")
-        rr_v = keep.tile([P, 8], F32, name="rr_v")
-        scl_v = keep.tile([P, 8], F32, name="scl_v")
-        b2_v = keep.tile([P, 8], F32, name="b2_v")
-        junk = keep.tile([P, P], BF16, name="junk")
-        ssum = keep.tile([P, 8], F32, name="ssum")
-        ssq = keep.tile([P, 8], F32, name="ssq")
-        shift_s = keep.tile([P, 8], F32, name="shift_s")
-        rr_s = keep.tile([P, 8], F32, name="rr_s")
-        scl_s = keep.tile([P, 8], F32, name="scl_s")
-        b2_s = keep.tile([P, 8], F32, name="b2_s")
-        y_sb = keep.tile([P, 8, P], F32, name="y_sb")
-        o_sb = keep.tile([P, C], F32, name="o_sb")
+        one_m_alpha = keep.tile([P, N_TILES], F32, name="one_m_alpha")
+        nc.vector.tensor_scalar(
+            out=one_m_alpha[:], in0=alpha, scalar1=-1.0, scalar2=1.0, op0=ALU.mult, op1=ALU.add
+        )
+        neg_alpha_n = keep.tile([P, N_TILES], F32, name="neg_alpha_n")
+        nc.vector.tensor_scalar(
+            out=neg_alpha_n[:], in0=alpha, scalar1=-1.0 / P, scalar2=None, op0=ALU.mult
+        )
+        rest = keep.tile([P, N_TILES], F32, name="rest")
+        nc.vector.tensor_tensor(out=rest[:], in0=one_m_alpha[:], in1=blin, op=ALU.mult)
 
-        def ld_x():
-            nc.sync.dma_start(out=x_sb[:], in_=x.rearrange("b n c -> (b n) c"))
+        h_acc = []
+        for b in range(2):
+            acc_b = psum.tile([P, HALF, P], F32, name="h_acc%d" % b, tag="bank%d" % b)
+            h_acc.append(acc_b)
+        grouped = {}
+        w_codes = {}
+        w_scales = {}
 
-        def ld_agg(h):
-            nc.sync.dma_start(
-                out=agg_sb[:, 2048 * h : 2048 * (h + 1)], in_=agg_f[:, 2048 * h : 2048 * (h + 1)]
+        def regroup_chunk(i):
+            v_cols = C // 2 if i == N_POST - 1 else V_COLS
+            g = grp_pool.tile([P, C, PACK], BF16, name="grp%d" % i, tag="grp", align_bytes=64)
+            regroup(nc.vector.tensor_copy, g[:, 0:v_cols, :], raw[i][:, :, 0:v_cols])
+            regroup(nc.scalar.copy, g[:, v_cols:C, :], raw[i][:, :, v_cols:C])
+            grouped[i] = g
+            cd = keep.tile([P, C], U32, name="w_codes%d" % i, align_bytes=64)
+            sc = keep.tile([P, C], U8, name="w_scales%d" % i, align_bytes=64)
+            w_codes[i] = cd
+            w_scales[i] = sc
+
+        def quantise_chunk(i, lo, hi):
+            quantise(
+                w_codes[i][:, lo:hi],
+                w_scales[i][:, lo:hi],
+                grouped[i][:, lo:hi, :].rearrange("p c t -> p (c t)"),
             )
 
-        def ld_par():
-            for v, vec in enumerate((b_post, b_lin, gn_weight, gn_bias, gn_alpha)):
-                nc.scalar.dma_start(
-                    out=par_raw[8 * v : 8 * v + 8, :], in_=vec.rearrange("(t p) -> t p", p=P)
+        def first_product(i, tiles):
+            for m in tiles:
+                t = m % HALF
+                nc.tensor.matmul_mx(
+                    out=h_acc[m // HALF][:, t, :],
+                    lhsT=w_codes[i][:, P * m : P * (m + 1)].bitcast(FP8X4),
+                    lhsT_scale=w_scales[i][:, P * m : P * (m + 1)],
+                    rhs=a_codes[:, P * i : P * (i + 1)].bitcast(FP8X4),
+                    rhs_scale=a_scales[:, P * i : P * (i + 1)],
+                    start=(i == 0 and t == 0),
+                    stop=(i == N_POST - 1 and t == HALF - 1),
                 )
 
-        def ld_w(i):
-            r = rawp.tile([P, 4, C], BF16, name="raw%d" % i, tag="raw")
-            nc.sync.dma_start(
-                out=r[:], in_=W_post[512 * i : 512 * (i + 1), :].rearrange("(p j) c -> p j c", j=4)
+        for i in range(N_POST):
+            regroup_chunk(i)
+            load_next()
+            if i > 0:
+                quantise_chunk(i - 1, 0, C)
+                first_product(i - 1, range(N_TILES))
+
+        l_grp = {}
+        l_codes = {}
+        l_scales = {}
+
+        def regroup_piece(j):
+            g = keep.tile([P, N_LIN, LIN_COLS, PACK], BF16, name="l_grp%d" % j, align_bytes=64)
+            c0 = LIN_COLS * j
+            r = raw[N_POST + c0 // (C // 2)]
+            c0 = c0 % (C // 2)
+            for gg in range(N_LIN):
+                on_vector = (j, gg) in LIN_ON_VECTOR
+                regroup(
+                    nc.vector.tensor_copy if on_vector else nc.scalar.copy,
+                    g[:, gg, :, :],
+                    r[:, PACK * gg : PACK * (gg + 1), c0 : c0 + LIN_COLS],
+                )
+            l_grp[j] = g
+
+        def quantise_piece(j):
+            cd = keep.tile([P, N_LIN, LIN_COLS], U32, name="l_codes%d" % j, align_bytes=64)
+            sc = keep.tile([P, N_LIN, LIN_COLS], U8, name="l_scales%d" % j, align_bytes=64)
+            quantise(
+                cd[:].rearrange("p g c -> p (g c)"),
+                sc[:].rearrange("p g c -> p (g c)"),
+                l_grp[j][:].rearrange("p g c t -> p (g c t)"),
             )
-            raw[i] = r
+            l_codes[j] = cd
+            l_scales[j] = sc
 
-        def ld_lin(h):
-            r = rawp.tile([P, 8, 512], BF16, name="lraw%d" % h, tag="raw")
-            nc.sync.dma_start(out=r[:], in_=lin_v[:, :, 512 * h : 512 * (h + 1)])
-            lraw[h] = r
+        h_grp = keep.tile([P, N_LIN, P, PACK], BF16, name="h_grp", align_bytes=64)
+        h_codes = keep.tile([P, N_LIN, P], U32, name="h_codes", align_bytes=64)
+        h_scales = keep.tile([P, N_LIN, P], U8, name="h_scales", align_bytes=64)
 
-        def t_act(b):
-            pt = psum.tile([P, 4, P], F32, name="pt%d" % b, tag="bk%d" % (b + 2))
-            for gg in range(2):
-                g = 2 * b + gg
-                words = x_w[:, g, :, :] if g < 2 else agg_w[:, g - 2, :, :]
-                for u in range(2):
-                    nc.tensor.transpose(pt[:, 2 * gg + u, :], words[:, :, u], ident[:])
-            pts[b] = pt
-
-        def copy_on(eng):
-            return nc.vector.tensor_copy if eng == VE else nc.scalar.copy
-
-        def ae(b, eng):
-            dst = a_grp_w[:, 512 * b : 512 * (b + 1)].rearrange("p (g n u) -> p g n u", g=2, u=2)
-            copy_on(eng)(out=dst, in_=pts[b][:].rearrange("p (g u) n -> p g n u", u=2))
-
-        def aq(b):
-            nc.vector.quantize_mx(
-                out=a_codes[:, 256 * b : 256 * (b + 1)].bitcast(FP8X4),
-                scales=a_scales[:, 256 * b : 256 * (b + 1)],
-                in_=a_grp[:, 1024 * b : 1024 * (b + 1)],
-            )
-
-        def aq_agg():
-            nc.vector.quantize_mx(
-                out=a_codes[:, 256:1280].bitcast(FP8X4),
-                scales=a_scales[:, 256:1280],
-                in_=a_grp[:, 1024:5120],
-            )
-
-        def par_t():
-            par_ps = psum.tile([P, P], BF16, name="par_ps", tag="bk7")
-            nc.tensor.transpose(par_ps[:], par_raw[:], ident_bf[:])
-            pts[9] = par_ps
-
-        def par_v():
-            nc.vector.tensor_copy(out=par[:], in_=pts[9][:, 0:40])
-            nc.vector.tensor_scalar(
-                out=a1[:], in0=alpha, scalar1=-1.0, scalar2=1.0, op0=ALU.mult, op1=ALU.add
-            )
-            nc.vector.tensor_scalar(
-                out=nal[:], in0=alpha, scalar1=-1.0 / P, scalar2=None, op0=ALU.mult
-            )
-            nc.vector.tensor_tensor(out=p1[:], in0=a1[:], in1=blin, op=ALU.mult)
-
-        def regroup_copy(eng, dst, src):
-            copy_on(eng)(
-                out=dst.rearrange("p (c i) t -> p c t i", i=4),
-                in_=src.rearrange("p t (c i) -> p c t i", i=4),
-            )
-
-        def unit_grp(i):
-            if i not in grp:
-                g = grpp.tile([P, C, 4], BF16, name="grp%d" % i, tag="grp", align_bytes=64)
-                grp[i] = g
-            return grp[i]
-
-        def v_cols(i):
-            return 512 if i == N_POST - 1 else V_COLS
-
-        def rv(i):
-            regroup_copy(VE, unit_grp(i)[:, 0 : v_cols(i), :], raw[i][:, :, 0 : v_cols(i)])
-
-        def rs(i):
-            regroup_copy(SE, unit_grp(i)[:, v_cols(i) : C, :], raw[i][:, :, v_cols(i) : C])
-
-        def q(i, lo, hi):
-            if i not in codes:
-                cd = keep.tile([P, C], U32, name="wc%d" % i, align_bytes=64)
-                sc_ = keep.tile([P, C], U8, name="ws%d" % i, align_bytes=64)
-                codes[i] = cd
-                scales[i] = sc_
-            nc.vector.quantize_mx(
-                out=codes[i][:, lo:hi].bitcast(FP8X4),
-                scales=scales[i][:, lo:hi],
-                in_=grp[i][:, lo:hi, :].rearrange("p c t -> p (c t)"),
-            )
-
-        def mm(g, m):
-            b = m // 4
-            t = m % 4
-            if b not in acc:
-                acc_b = psum.tile([P, 4, P], F32, name="acc%d" % b, tag="bk%d" % b)
-                acc[b] = acc_b
-            nc.tensor.matmul_mx(
-                out=acc[b][:, t, :],
-                lhsT=codes[g][:, P * m : P * (m + 1)].bitcast(FP8X4),
-                lhsT_scale=scales[g][:, P * m : P * (m + 1)],
-                rhs=a_codes[:, P * g : P * (g + 1)].bitcast(FP8X4),
-                rhs_scale=a_scales[:, P * g : P * (g + 1)],
-                start=(g == 0 and t == 0),
-                stop=(g == N_POST - 1 and t == 3),
-            )
-
-        def r_lin(j, gg, lo, hi, eng):
-            if j not in lgrp:
-                g = keep.tile([P, 2, LW, 4], BF16, name="lgrp%d" % j, align_bytes=64)
-                lgrp[j] = g
-            c0 = LW * j
-            r = lraw[c0 // 512]
-            c0 = c0 % 512
-            regroup_copy(
-                eng, lgrp[j][:, gg, lo:hi, :], r[:, 4 * gg : 4 * gg + 4, c0 + lo : c0 + hi]
-            )
-
-        def q_lin(j):
-            cd = keep.tile([P, 2, LW], U32, name="lc%d" % j, align_bytes=64)
-            sc_ = keep.tile([P, 2, LW], U8, name="ls%d" % j, align_bytes=64)
-            nc.vector.quantize_mx(
-                out=cd[:].rearrange("p g c -> p (g c)").bitcast(FP8X4),
-                scales=sc_[:].rearrange("p g c -> p (g c)"),
-                in_=lgrp[j][:].rearrange("p g c t -> p (g c t)"),
-            )
-            lcodes[j] = cd
-            lscales[j] = sc_
-
-        def hw(gg):
+        def finish_h(gg):
             nc.vector.tensor_tensor(
                 out=h_grp[:, gg, :, :],
-                in0=acc[gg][:].rearrange("p t n -> p n t"),
-                in1=bpost[:, 4 * gg : 4 * gg + 4].unsqueeze(1).to_broadcast([P, P, 4]),
+                in0=h_acc[gg][:].rearrange("p t n -> p n t"),
+                in1=bpost[:, HALF * gg : HALF * (gg + 1)].unsqueeze(1).to_broadcast([P, P, PACK]),
                 op=ALU.add,
             )
-
-        def hq(gg):
-            nc.vector.quantize_mx(
-                out=h_codes[:, gg, :].bitcast(FP8X4),
-                scales=h_scales[:, gg, :],
-                in_=h_grp[:, gg, :, :].rearrange("p n t -> p (n t)"),
+            quantise(
+                h_codes[:, gg, :], h_scales[:, gg, :], h_grp[:, gg, :, :].rearrange("p n t -> p (n t)")
             )
 
-        def s2(m, gg):
-            if m not in o_ps:
-                o_m = psum.tile([P, P], F32, name="o%d" % m, tag="bk%d" % O_BANK[m])
-                o_ps[m] = o_m
-            j = (P * m) // LW
-            k = (P * m) % LW
-            nc.tensor.matmul_mx(
-                out=o_ps[m][:],
-                lhsT=lcodes[j][:, gg, k : k + P].bitcast(FP8X4),
-                lhsT_scale=lscales[j][:, gg, k : k + P],
-                rhs=h_codes[:, gg, :].bitcast(FP8X4),
-                rhs_scale=h_scales[:, gg, :],
-                start=(gg == 0),
-                stop=(gg == 1),
-            )
+        o_acc = {}
 
-        def bs(m):
-            nc.vector.bn_stats(out=st[:, m, :], in_=o_ps[m][:])
+        def second_product(m):
+            o_m = psum.tile([P, P], F32, name="o_acc%d" % m, tag="bank%d" % O_BANK[m])
+            j = (P * m) // LIN_COLS
+            k = (P * m) % LIN_COLS
+            for gg in range(N_LIN):
+                nc.tensor.matmul_mx(
+                    out=o_m[:],
+                    lhsT=l_codes[j][:, gg, k : k + P].bitcast(FP8X4),
+                    lhsT_scale=l_scales[j][:, gg, k : k + P],
+                    rhs=h_codes[:, gg, :].bitcast(FP8X4),
+                    rhs_scale=h_scales[:, gg, :],
+                    start=(gg == 0),
+                    stop=(gg == N_LIN - 1),
+                )
+            o_acc[m] = o_m
 
-        def ba(m):
-            nc.vector.bn_aggr(out=mv[:, m, :], in_=st[:, m, :])
+        y_sb = keep.tile([P, N_TILES, P], F32, name="y_sb")
+        o_sb = keep.tile([P, C], F32, name="o_sb")
 
-        def tt_v(o, a, b, op):
-            nc.vector.tensor_tensor(out=o, in0=a, in1=b, op=op)
-
-        def rsqrt_s(o, a, scale):
-            nc.scalar.activation(out=o, in_=a, func=ACT.Abs_reciprocal_sqrt, bias=eps_t[:, 0:1], scale=scale)
-
-        def sm(kind):
-            sl = slice(0, NVT)
-            mean = mv[:, sl, 0]
-            var = mv[:, sl, 1]
-            if kind == "d1":
-                tt_v(dd[:, sl], mean, a1[:, sl], ALU.mult)
-            elif kind == "d2":
-                tt_v(dd[:, sl], dd[:, sl], p1[:, sl], ALU.add)
-            elif kind == "v1":
-                tt_v(vv[:, sl], dd[:, sl], dd[:, sl], ALU.mult)
-            elif kind == "v2":
-                tt_v(vv[:, sl], vv[:, sl], var, ALU.add)
-            elif kind == "sh":
-                tt_v(shift_v[:, sl], dd[:, sl], mean, ALU.subtract)
-            elif kind == "qq":
-                tt_v(qq[:, sl], shift_v[:, sl], gw[:, sl], ALU.mult)
-            elif kind == "RRv":
-                rsqrt_s(rr_v[:, sl], vv[:, sl], 1.0)
-            elif kind == "sc":
-                tt_v(scl_v[:, sl], rr_v[:, sl], gw[:, sl], ALU.mult)
-            elif kind == "b2a":
-                tt_v(b2_v[:, sl], rr_v[:, sl], qq[:, sl], ALU.mult)
-            else:
-                tt_v(b2_v[:, sl], b2_v[:, sl], gb[:, sl], ALU.add)
+        def small(name):
+            t = keep.tile([P, N_TILES], F32, name=name)
+            return t
 
         def col(t, m):
             return t[:, m : m + 1]
 
-        def p1_s(m):
+        def vec_op(o, a, b, op):
+            nc.vector.tensor_tensor(out=o, in0=a, in1=b, op=op)
+
+        stats = keep.tile([P, HALF, 6], F32, name="stats")
+        mean_var = keep.tile([P, HALF, 2], F32, name="mean_var")
+        v_mu = small("v_mu")
+        v_var = small("v_var")
+        v_shift = small("v_shift")
+        v_ws = small("v_ws")
+        v_rstd = small("v_rstd")
+        v_scale = small("v_scale")
+        v_bias = small("v_bias")
+
+        def norm_on_vector_stats(m):
+            nc.vector.bn_stats(out=stats[:, m, :], in_=o_acc[m][:])
+            nc.vector.bn_aggr(out=mean_var[:, m, :], in_=stats[:, m, :])
+
+        def norm_on_vector_scalars():
+            sl = slice(0, HALF)
+            mean = mean_var[:, :, 0]
+            var = mean_var[:, :, 1]
+            vec_op(v_mu[:, sl], mean, one_m_alpha[:, sl], ALU.mult)
+            vec_op(v_mu[:, sl], v_mu[:, sl], rest[:, sl], ALU.add)
+            vec_op(v_var[:, sl], v_mu[:, sl], v_mu[:, sl], ALU.mult)
+            vec_op(v_var[:, sl], v_var[:, sl], var, ALU.add)
             nc.scalar.activation(
-                out=junk[:], in_=o_ps[m][:], func=ACT.Identity, accum_out=col(ssum, m)
+                out=v_rstd[:, sl], in_=v_var[:, sl], func=ACT.Abs_reciprocal_sqrt,
+                bias=eps[:, 0:1], scale=1.0,
             )
+            vec_op(v_shift[:, sl], v_mu[:, sl], mean, ALU.subtract)
+            vec_op(v_ws[:, sl], v_shift[:, sl], gw[:, sl], ALU.mult)
+            vec_op(v_scale[:, sl], v_rstd[:, sl], gw[:, sl], ALU.mult)
+            vec_op(v_bias[:, sl], v_rstd[:, sl], v_ws[:, sl], ALU.mult)
+            vec_op(v_bias[:, sl], v_bias[:, sl], gb[:, sl], ALU.add)
 
-        def sh_s(m):
-            nc.scalar.activation(
-                out=col(shift_s, m), in_=col(ssum, m), func=ACT.Identity,
-                bias=col(p1, m), scale=col(nal, m),
-            )
+        junk = keep.tile([P, P], BF16, name="junk")
+        s_sum = small("s_sum")
+        s_sq = small("s_sq")
+        s_shift = small("s_shift")
+        s_rstd = small("s_rstd")
+        s_scale = small("s_scale")
+        s_bias = small("s_bias")
 
-        def p2_s(m):
-            nc.scalar.activation(
-                out=junk[:], in_=o_ps[m][:], func=ACT.Square, bias=col(shift_s, m), scale=1.0,
-                accum_out=col(ssq, m),
-            )
-
-        def rr_sg(k):
-            m0, nb = SGRP[k]
-            rsqrt_s(rr_s[:, m0 : m0 + nb], ssq[:, m0 : m0 + nb], 1.0 / P)
-
-        def sc_s(m):
-            nc.scalar.activation(
-                out=col(scl_s, m), in_=col(rr_s, m), func=ACT.Copy, scale=gw[:, m : m + 1]
-            )
-
-        def b2_sm(m):
-            nc.scalar.activation(
-                out=col(b2_s, m), in_=col(shift_s, m), func=ACT.Identity,
-                bias=gb[:, m : m + 1], scale=col(scl_s, m),
-            )
-
-        def y(m, eng):
-            sc_t = scl_v if m < NVT else scl_s
-            b2_t = b2_v if m < NVT else b2_s
-            if eng == SE:
+        def norm_on_scalar(tiles):
+            for m in tiles:
                 nc.scalar.activation(
-                    out=y_sb[:, m, :], in_=o_ps[m][:], func=ACT.Relu,
-                    bias=col(b2_t, m), scale=col(sc_t, m),
+                    out=junk[:], in_=o_acc[m][:], func=ACT.Identity, accum_out=col(s_sum, m)
                 )
-            else:
-                nc.vector.tensor_scalar(
-                    out=y_sb[:, m, :], in0=o_ps[m][:], scalar1=col(sc_t, m),
-                    scalar2=col(b2_t, m), op0=ALU.mult, op1=ALU.add,
+            for m in tiles:
+                nc.scalar.activation(
+                    out=col(s_shift, m), in_=col(s_sum, m), func=ACT.Identity,
+                    bias=col(rest, m), scale=col(neg_alpha_n, m),
+                )
+            for m in tiles:
+                nc.scalar.activation(
+                    out=junk[:], in_=o_acc[m][:], func=ACT.Square, bias=col(s_shift, m), scale=1.0,
+                    accum_out=col(s_sq, m),
+                )
+            sl = slice(tiles[0], tiles[-1] + 1)
+            nc.scalar.activation(
+                out=s_rstd[:, sl], in_=s_sq[:, sl], func=ACT.Abs_reciprocal_sqrt,
+                bias=eps[:, 0:1], scale=1.0 / P,
+            )
+            for m in tiles:
+                nc.scalar.activation(
+                    out=col(s_scale, m), in_=col(s_rstd, m), func=ACT.Copy, scale=gw[:, m : m + 1]
+                )
+            for m in tiles:
+                nc.scalar.activation(
+                    out=col(s_bias, m), in_=col(s_shift, m), func=ACT.Identity,
+                    bias=gb[:, m : m + 1], scale=col(s_scale, m),
                 )
 
-        def group_of(m):
-            for g, (m0, nb) in enumerate(ADG):
-                if m0 <= m < m0 + nb:
-                    return g
-            return -1
-
-        def tt(m):
-            g = group_of(m)
-            m0, nb = ADG[g]
-            if g not in y_t:
-                y_g = psum.tile([P, P * nb], F32, name="yt%d" % g, tag="bk%d" % O_BANK[m0])
-                y_t[g] = y_g
-            nc.tensor.transpose(y_t[g][:, P * (m - m0) : P * (m - m0 + 1)], y_sb[:, m, :], ident[:])
-
-        def ad(g):
-            m0, nb = ADG[g]
-            cols = slice(P * m0, P * (m0 + nb))
-            nc.vector.scalar_tensor_tensor(
-                out=o_sb[:, cols], in0=y_t[g][:], scalar=0.0, in1=x_sb[:, cols],
-                op0=ALU.max, op1=ALU.add,
+        def apply_on_scalar(m, scale, bias):
+            nc.scalar.activation(
+                out=y_sb[:, m, :], in_=o_acc[m][:], func=ACT.Relu, bias=col(bias, m), scale=col(scale, m)
             )
 
-        def st_out(g):
-            m0, nb = ADG[g]
-            cols = slice(P * m0, P * (m0 + nb))
-            nc.sync.dma_start(out=out_f[:, cols], in_=o_sb[:, cols])
+        def apply_on_vector(m, scale, bias):
+            nc.vector.tensor_scalar(
+                out=y_sb[:, m, :], in0=o_acc[m][:], scalar1=col(scale, m), scalar2=col(bias, m),
+                op0=ALU.mult, op1=ALU.add,
+            )
 
-        ld_par()
-        ld_x()
-        ld_agg(0)
-        ld_agg(1)
-        t_act(0)
-        par_t()
-        ld_w(0)
-        ae(0, SE)
-        t_act(1)
-        t_act(2)
-        aq(0)
-        ae(1, SE)
-        t_act(3)
-        ld_w(1)
-        t_act(4)
-        ae(2, SE)
-        ae(3, SE)
-        ae(4, SE)
-        rs(0)
-        rv(0)
-        ld_w(2)
-        aq_agg()
-        par_v()
-        rv(1)
-        ld_w(3)
-        rs(1)
-        q(0, 0, 1024)
-        rv(2)
-        ld_w(4)
-        mm(0, 0)
-        mm(0, 1)
-        mm(0, 2)
-        rs(2)
-        mm(0, 3)
-        mm(0, 4)
-        mm(0, 5)
-        mm(0, 6)
-        mm(0, 7)
-        q(1, 0, 1024)
-        rv(3)
-        ld_w(5)
-        mm(1, 0)
-        mm(1, 1)
-        mm(1, 2)
-        mm(1, 3)
-        mm(1, 4)
-        mm(1, 5)
-        rs(3)
-        mm(1, 6)
-        mm(1, 7)
-        q(2, 0, 1024)
-        rv(4)
-        ld_w(6)
-        mm(2, 0)
-        mm(2, 1)
-        mm(2, 2)
-        mm(2, 3)
-        mm(2, 4)
-        mm(2, 5)
-        mm(2, 6)
-        mm(2, 7)
-        rs(4)
-        q(3, 0, 1024)
-        ld_w(7)
-        rv(5)
-        mm(3, 0)
-        mm(3, 1)
-        mm(3, 2)
-        mm(3, 3)
-        mm(3, 4)
-        mm(3, 5)
-        mm(3, 6)
-        mm(3, 7)
-        rs(5)
-        q(4, 0, 1024)
-        ld_w(8)
-        rv(6)
-        mm(4, 0)
-        mm(4, 1)
-        mm(4, 2)
-        mm(4, 3)
-        mm(4, 4)
-        mm(4, 5)
-        mm(4, 6)
-        mm(4, 7)
-        rs(6)
-        q(5, 0, 1024)
-        ld_w(9)
-        rv(7)
-        mm(5, 0)
-        mm(5, 1)
-        mm(5, 2)
-        mm(5, 3)
-        mm(5, 4)
-        mm(5, 5)
-        mm(5, 6)
-        mm(5, 7)
-        rs(7)
-        q(6, 0, 1024)
-        ld_lin(0)
-        rv(8)
-        mm(6, 0)
-        mm(6, 1)
-        mm(6, 2)
-        mm(6, 3)
-        mm(6, 4)
-        mm(6, 5)
-        mm(6, 6)
-        mm(6, 7)
-        rs(8)
-        rv(9)
-        ld_lin(1)
-        q(7, 0, 1024)
-        rs(9)
-        q(9, 0, 512)
-        mm(7, 0)
-        mm(7, 1)
-        mm(7, 2)
-        q(8, 0, 1024)
-        mm(7, 3)
-        mm(7, 4)
-        mm(7, 5)
-        mm(7, 6)
-        mm(7, 7)
-        r_lin(0, 0, 0, 256, VE)
-        mm(8, 0)
-        r_lin(0, 1, 0, 256, SE)
-        mm(8, 1)
-        mm(9, 0)
-        mm(8, 2)
-        r_lin(1, 0, 0, 256, VE)
-        mm(9, 1)
-        mm(8, 3)
-        mm(9, 2)
-        mm(8, 4)
-        mm(9, 3)
-        mm(8, 5)
-        mm(8, 6)
-        mm(8, 7)
-        q(9, 512, 1024)
-        r_lin(1, 1, 0, 256, SE)
-        hw(0)
-        mm(9, 4)
-        mm(9, 5)
-        mm(9, 6)
-        mm(9, 7)
-        q_lin(0)
-        r_lin(2, 0, 0, 256, SE)
-        hq(0)
-        hw(1)
-        s2(0, 0)
-        s2(1, 0)
-        q_lin(1)
-        r_lin(2, 1, 0, 256, SE)
-        hq(1)
-        s2(2, 0)
-        s2(3, 0)
-        s2(0, 1)
-        s2(1, 1)
-        r_lin(3, 0, 0, 256, SE)
-        s2(2, 1)
-        s2(3, 1)
-        q_lin(2)
-        bs(0)
-        r_lin(3, 1, 0, 256, SE)
-        bs(1)
-        s2(4, 0)
-        s2(5, 0)
-        bs(2)
-        s2(4, 1)
-        s2(5, 1)
-        bs(3)
-        ba(0)
-        ba(1)
-        ba(2)
-        ba(3)
-        p1_s(4)
-        p1_s(5)
-        sm("d1")
-        q_lin(3)
-        sh_s(4)
-        sh_s(5)
-        p2_s(4)
-        sm("d2")
-        p2_s(5)
-        s2(6, 0)
-        sm("v1")
-        s2(7, 0)
-        sm("sh")
-        s2(6, 1)
-        s2(7, 1)
-        sm("v2")
-        rr_sg(0)
-        sm("qq")
-        p1_s(6)
-        p1_s(7)
-        sm("RRv")
-        sh_s(6)
-        sc_s(4)
-        sc_s(5)
-        sh_s(7)
-        sm("b2a")
-        p2_s(6)
-        sm("sc")
-        p2_s(7)
-        sm("b2b")
-        b2_sm(4)
-        b2_sm(5)
-        y(0, VE)
-        y(3, SE)
-        y(1, VE)
-        rr_sg(1)
-        y(5, SE)
-        y(2, VE)
-        tt(0)
-        y(4, VE)
-        tt(3)
-        sc_s(6)
-        sc_s(7)
-        tt(1)
-        tt(5)
-        b2_sm(6)
-        tt(2)
-        b2_sm(7)
-        tt(4)
-        y(6, VE)
-        y(7, SE)
-        ad(0)
-        tt(6)
-        tt(7)
-        ad(1)
-        st_out(0)
-        ad(2)
-        st_out(1)
-        st_out(2)
+        def finish(tiles):
+            m0 = tiles[0]
+            cols = slice(P * m0, P * (tiles[-1] + 1))
+            y_t = psum.tile([P, P * len(tiles)], F32, name="y_t%d" % m0, tag="bank%d" % O_BANK[m0])
+            for m in tiles:
+                nc.tensor.transpose(y_t[:, P * (m - m0) : P * (m - m0 + 1)], y_sb[:, m, :], ident[:])
+            nc.vector.scalar_tensor_tensor(
+                out=o_sb[:, cols], in0=y_t[:], scalar=0.0, in1=x_sb[:, cols], op0=ALU.max, op1=ALU.add
+            )
+            nc.sync.dma_start(out=out_rows[:, cols], in_=o_sb[:, cols])
+
+        last = N_POST - 1
+        regroup_piece(0)
+        for gg in range(2):
+            quantise_chunk(last, (C // 2) * gg, (C // 2) * (gg + 1))
+            first_product(last, range(HALF * gg, HALF * (gg + 1)))
+        regroup_piece(1)
+        for gg in range(2):
+            finish_h(gg)
+        for j in range(N_PIECES):
+            quantise_piece(j)
+            if j + 2 < N_PIECES:
+                regroup_piece(j + 2)
+            for m in (2 * j, 2 * j + 1):
+                second_product(m)
+                if m < HALF:
+                    norm_on_vector_stats(m)
+            if j == 1:
+                norm_on_vector_scalars()
+                for m in range(HALF):
+                    apply_on_vector(m, v_scale, v_bias)
+                finish((0, 1, 2, 3))
+            if j >= 2:
+                tiles = (2 * j, 2 * j + 1)
+                norm_on_scalar(tiles)
+                apply_on_scalar(tiles[0], s_scale, s_bias)
+                apply_on_vector(tiles[1], s_scale, s_bias)
+                finish(tiles)

@@ -28,7 +28,7 @@ RAW_BUFS = 7
 GRP_BUFS = 4
 LIN_COLS = 256
 N_PIECES = C // LIN_COLS
-LIN_ON_VECTOR = ((0, 0), (1, 0))
+LIN_ON_VECTOR = ((0, 0),)
 O_BANK = (2, 3, 4, 5, 6, 7, 0, 1)
 
 
@@ -41,7 +41,7 @@ def tile_gnnlayer_pb_kernel(
         raw_pool = ctx.enter_context(tc.tile_pool(name="raw_pool", bufs=RAW_BUFS))
         grp_pool = ctx.enter_context(tc.tile_pool(name="grp_pool", bufs=GRP_BUFS))
         psum = ctx.enter_context(tc.psum_pool(name="psum", bufs=1))
-
+        ctx.enter_context(tc.manual_schedule())
 
         one = keep.tile([P, 1], F32, name="one")
         nc.vector.memset(one[:], 1.0)
@@ -273,9 +273,11 @@ def tile_gnnlayer_pb_kernel(
         v_scale = small("v_scale")
         v_bias = small("v_bias")
 
-        def norm_on_vector_stats(m):
-            nc.vector.bn_stats(out=stats[:, m, :], in_=o_acc[m][:])
-            nc.vector.bn_aggr(out=mean_var[:, m, :], in_=stats[:, m, :])
+        def norm_on_vector_stats(tiles):
+            for m in tiles:
+                nc.vector.bn_stats(out=stats[:, m, :], in_=o_acc[m][:])
+            for m in tiles:
+                nc.vector.bn_aggr(out=mean_var[:, m, :], in_=stats[:, m, :])
 
         def norm_on_vector_scalars():
             sl = slice(0, HALF)
@@ -338,47 +340,41 @@ def tile_gnnlayer_pb_kernel(
                 out=y_sb[:, m, :], in_=o_acc[m][:], func=ACT.Relu, bias=col(bias, m), scale=col(scale, m)
             )
 
-        def apply_on_vector(m, scale, bias):
-            nc.vector.tensor_scalar(
-                out=y_sb[:, m, :], in0=o_acc[m][:], scalar1=col(scale, m), scalar2=col(bias, m),
-                op0=ALU.mult, op1=ALU.add,
-            )
-
         def finish(tiles):
             m0 = tiles[0]
             cols = slice(P * m0, P * (tiles[-1] + 1))
             y_t = psum.tile([P, P * len(tiles)], F32, name="y_t%d" % m0, tag="bank%d" % O_BANK[m0])
             for m in tiles:
                 nc.tensor.transpose(y_t[:, P * (m - m0) : P * (m - m0 + 1)], y_sb[:, m, :], ident[:])
-            nc.vector.scalar_tensor_tensor(
-                out=o_sb[:, cols], in0=y_t[:], scalar=0.0, in1=x_sb[:, cols], op0=ALU.max, op1=ALU.add
-            )
+            nc.vector.tensor_tensor(out=o_sb[:, cols], in0=y_t[:], in1=x_sb[:, cols], op=ALU.add)
             nc.sync.dma_start(out=out_rows[:, cols], in_=o_sb[:, cols])
 
         last = N_POST - 1
+        quantise_chunk(last, 0, C // 2)
+        first_product(last, range(0, HALF))
         regroup_piece(0)
-        for gg in range(2):
-            quantise_chunk(last, (C // 2) * gg, (C // 2) * (gg + 1))
-            first_product(last, range(HALF * gg, HALF * (gg + 1)))
+        quantise_chunk(last, C // 2, C)
+        first_product(last, range(HALF, N_TILES))
         regroup_piece(1)
-        for gg in range(2):
-            finish_h(gg)
+        regroup_piece(2)
+        finish_h(0)
+        finish_h(1)
+        regroup_piece(3)
         for j in range(N_PIECES):
             quantise_piece(j)
-            if j + 2 < N_PIECES:
-                regroup_piece(j + 2)
-            for m in (2 * j, 2 * j + 1):
-                second_product(m)
-                if m < HALF:
-                    norm_on_vector_stats(m)
-            if j == 1:
-                norm_on_vector_scalars()
-                for m in range(HALF):
-                    apply_on_vector(m, v_scale, v_bias)
-                finish((0, 1, 2, 3))
-            if j >= 2:
-                tiles = (2 * j, 2 * j + 1)
-                norm_on_scalar(tiles)
-                apply_on_scalar(tiles[0], s_scale, s_bias)
-                apply_on_vector(tiles[1], s_scale, s_bias)
-                finish(tiles)
+            second_product(2 * j)
+            second_product(2 * j + 1)
+            if j == 2:
+                norm_on_vector_stats((0, 1, 2, 3))
+        norm_on_scalar((4, 5))
+        for m in (4, 5):
+            apply_on_scalar(m, s_scale, s_bias)
+        norm_on_vector_scalars()
+        finish((4, 5))
+        norm_on_scalar((6, 7))
+        for m in range(HALF):
+            apply_on_scalar(m, v_scale, v_bias)
+        finish((0, 1, 2, 3))
+        for m in (6, 7):
+            apply_on_scalar(m, s_scale, s_bias)
+        finish((6, 7))

@@ -23,12 +23,12 @@ HALF = N_TILES // 2
 EPS_GN = 1e-5
 FLOPS = 2 * P * (K_POST * C + C * C)
 
-V_COLS = 496
+V_COLS = 464
 RAW_BUFS = 7
 GRP_BUFS = 4
 LIN_COLS = 256
 N_PIECES = C // LIN_COLS
-LIN_ON_VECTOR = ((0, 0),)
+LIN_ON_VECTOR = ((0, 0), (1, 0))
 O_BANK = (2, 3, 4, 5, 6, 7, 0, 1)
 
 
@@ -221,13 +221,15 @@ def tile_gnnlayer_pb_kernel(
         h_codes = keep.tile([P, N_LIN, P], U32, name="h_codes", align_bytes=64)
         h_scales = keep.tile([P, N_LIN, P], U8, name="h_scales", align_bytes=64)
 
-        def finish_h(gg):
+        def add_bias(gg):
             nc.vector.tensor_tensor(
                 out=h_grp[:, gg, :, :],
                 in0=h_acc[gg][:].rearrange("p t n -> p n t"),
                 in1=bpost[:, HALF * gg : HALF * (gg + 1)].unsqueeze(1).to_broadcast([P, P, PACK]),
                 op=ALU.add,
             )
+
+        def quantise_h(gg):
             quantise(
                 h_codes[:, gg, :], h_scales[:, gg, :], h_grp[:, gg, :, :].rearrange("p n t -> p (n t)")
             )
@@ -340,13 +342,21 @@ def tile_gnnlayer_pb_kernel(
                 out=y_sb[:, m, :], in_=o_acc[m][:], func=ACT.Relu, bias=col(bias, m), scale=col(scale, m)
             )
 
+        def apply_on_vector(m, scale, bias):
+            nc.vector.tensor_scalar(
+                out=y_sb[:, m, :], in0=o_acc[m][:], scalar1=col(scale, m), scalar2=col(bias, m),
+                op0=ALU.mult, op1=ALU.add,
+            )
+
         def finish(tiles):
             m0 = tiles[0]
             cols = slice(P * m0, P * (tiles[-1] + 1))
             y_t = psum.tile([P, P * len(tiles)], F32, name="y_t%d" % m0, tag="bank%d" % O_BANK[m0])
             for m in tiles:
                 nc.tensor.transpose(y_t[:, P * (m - m0) : P * (m - m0 + 1)], y_sb[:, m, :], ident[:])
-            nc.vector.tensor_tensor(out=o_sb[:, cols], in0=y_t[:], in1=x_sb[:, cols], op=ALU.add)
+            nc.vector.scalar_tensor_tensor(
+                out=o_sb[:, cols], in0=y_t[:], scalar=0.0, in1=x_sb[:, cols], op0=ALU.max, op1=ALU.add
+            )
             nc.sync.dma_start(out=out_rows[:, cols], in_=o_sb[:, cols])
 
         last = N_POST - 1
@@ -357,11 +367,15 @@ def tile_gnnlayer_pb_kernel(
         first_product(last, range(HALF, N_TILES))
         regroup_piece(1)
         regroup_piece(2)
-        finish_h(0)
-        finish_h(1)
+        add_bias(0)
+        quantise_piece(0)
+        quantise_h(0)
+        add_bias(1)
+        quantise_h(1)
         regroup_piece(3)
         for j in range(N_PIECES):
-            quantise_piece(j)
+            if j > 0:
+                quantise_piece(j)
             second_product(2 * j)
             second_product(2 * j + 1)
             if j == 2:
@@ -370,10 +384,10 @@ def tile_gnnlayer_pb_kernel(
         for m in (4, 5):
             apply_on_scalar(m, s_scale, s_bias)
         norm_on_vector_scalars()
+        for m in range(HALF):
+            apply_on_vector(m, v_scale, v_bias)
         finish((4, 5))
         norm_on_scalar((6, 7))
-        for m in range(HALF):
-            apply_on_scalar(m, v_scale, v_bias)
         finish((0, 1, 2, 3))
         for m in (6, 7):
             apply_on_scalar(m, s_scale, s_bias)

@@ -23,7 +23,10 @@ HALF = N_TILES // 2
 EPS_GN = 1e-5
 FLOPS = 2 * P * (K_POST * C + C * C)
 
-V_COLS = 464
+V_COLS = 480
+FIRST_PIECES = (((0, 256), (256, 512), (512, 1024)), ((0, 512), (512, 1024)))
+FIRST_V_COLS = {256: 120, 512: 240}
+A_AFTER = 4
 RAW_BUFS = 7
 GRP_BUFS = 4
 LIN_COLS = 256
@@ -43,14 +46,14 @@ def tile_gnnlayer_pb_kernel(
         psum = ctx.enter_context(tc.psum_pool(name="psum", bufs=1))
         ctx.enter_context(tc.manual_schedule())
 
+        par_rows = keep.tile([P, P], BF16, name="par_rows")
+        nc.vector.memset(par_rows[:], 0.0)
         one = keep.tile([P, 1], F32, name="one")
         nc.vector.memset(one[:], 1.0)
         warm = keep.tile([P, 1], F32, name="warm")
         nc.scalar.activation(out=warm[:], in_=one[:], func=ACT.Abs_reciprocal_sqrt)
         eps = keep.tile([P, 1], F32, name="eps")
         nc.vector.memset(eps[:], EPS_GN)
-        par_rows = keep.tile([P, P], BF16, name="par_rows")
-        nc.vector.memset(par_rows[:], 0.0)
         ident = keep.tile([P, P], F32, name="ident")
         make_identity(nc, ident[:])
         ident_bf = keep.tile([P, P], BF16, name="ident_bf")
@@ -60,24 +63,26 @@ def tile_gnnlayer_pb_kernel(
         agg_sb = keep.tile([P, 4 * C], BF16, name="agg_sb")
         agg_rows = agg.rearrange("b n c -> (b n) c")
         out_rows = out.rearrange("b n c -> (b n) c")
-        nc.sync.dma_start(out=x_sb[:], in_=x.rearrange("b n c -> (b n) c"))
-        for h in range(2):
-            cols = slice(2 * C * h, 2 * C * (h + 1))
-            nc.sync.dma_start(out=agg_sb[:, cols], in_=agg_rows[:, cols])
-        for v, vec in enumerate((b_post, b_lin, gn_weight, gn_bias, gn_alpha)):
-            nc.scalar.dma_start(
-                out=par_rows[N_TILES * v : N_TILES * (v + 1), :],
-                in_=vec.rearrange("(t p) -> t p", p=P),
-            )
 
         raw = []
+        first_raw = {}
+
+        def post_rows(i):
+            return W_post[K_PASS * i : K_PASS * (i + 1), :].rearrange("(p j) c -> p j c", j=PACK)
+
+        def load_pieces():
+            for i in range(len(FIRST_PIECES)):
+                raw.append(None)
+                for lo, hi in FIRST_PIECES[i]:
+                    r = keep.tile([P, PACK, hi - lo], BF16, name="raw%d_%d" % (i, lo))
+                    nc.sync.dma_start(out=r[:], in_=post_rows(i)[:, :, lo:hi])
+                    first_raw[(i, lo)] = r
 
         def load_next():
             i = len(raw)
             if i < N_POST:
                 r = raw_pool.tile([P, PACK, C], BF16, name="raw%d" % i, tag="raw")
-                rows = W_post[K_PASS * i : K_PASS * (i + 1), :]
-                nc.sync.dma_start(out=r[:], in_=rows.rearrange("(p j) c -> p j c", j=PACK))
+                nc.sync.dma_start(out=r[:], in_=post_rows(i))
                 raw.append(r)
             elif i < N_POST + 2:
                 h = i - N_POST
@@ -88,7 +93,23 @@ def tile_gnnlayer_pb_kernel(
                 )
                 raw.append(r)
 
-        for i in range(RAW_BUFS - 1):
+        def load_agg(h):
+            cols = slice(2 * C * h, 2 * C * (h + 1))
+            nc.sync.dma_start(out=agg_sb[:, cols], in_=agg_rows[:, cols])
+
+        load_pieces()
+        for i in range(len(FIRST_PIECES), A_AFTER):
+            load_next()
+        nc.sync.dma_start(out=x_sb[:], in_=x.rearrange("b n c -> (b n) c"))
+        load_agg(0)
+        load_agg(1)
+        load_next()
+        for v, vec in enumerate((b_post, b_lin, gn_weight, gn_bias, gn_alpha)):
+            nc.sync.dma_start(
+                out=par_rows[N_TILES * v : N_TILES * (v + 1), :],
+                in_=vec.rearrange("(t p) -> t p", p=P),
+            )
+        for i in range(A_AFTER + 1, RAW_BUFS + 1):
             load_next()
 
         def regroup(copy, dst, src):
@@ -106,7 +127,8 @@ def tile_gnnlayer_pb_kernel(
         a_codes = keep.tile([P, N_POST * P], U32, name="a_codes", align_bytes=64)
         a_scales = keep.tile([P, N_POST * P], U8, name="a_scales", align_bytes=64)
         a_grp_words = a_grp[:].bitcast(F32)
-        for b in range(N_POST // 2):
+
+        def turn(b):
             turned = psum.tile([P, 4, P], F32, name="turned%d" % b, tag="bank%d" % (b + 2))
             for j in range(4):
                 g = 2 * b + j // 2
@@ -118,29 +140,11 @@ def tile_gnnlayer_pb_kernel(
                 ),
                 in_=turned[:].rearrange("p (g u) n -> p g n u", u=2),
             )
-            if b == 0:
-                quantise(a_codes[:, 0:256], a_scales[:, 0:256], a_grp[:, 0:1024])
-        quantise(a_codes[:, 256:1280], a_scales[:, 256:1280], a_grp[:, 1024:5120])
 
-        par_t = psum.tile([P, P], BF16, name="par_t", tag="bank7")
-        nc.tensor.transpose(par_t[:], par_rows[:], ident_bf[:])
-        par = keep.tile([P, 5 * N_TILES], F32, name="par")
-        nc.vector.tensor_copy(out=par[:], in_=par_t[:, 0 : 5 * N_TILES])
-        bpost = par[:, 0:8]
-        blin = par[:, 8:16]
-        gw = par[:, 16:24]
-        gb = par[:, 24:32]
-        alpha = par[:, 32:40]
-        one_m_alpha = keep.tile([P, N_TILES], F32, name="one_m_alpha")
-        nc.vector.tensor_scalar(
-            out=one_m_alpha[:], in0=alpha, scalar1=-1.0, scalar2=1.0, op0=ALU.mult, op1=ALU.add
-        )
-        neg_alpha_n = keep.tile([P, N_TILES], F32, name="neg_alpha_n")
-        nc.vector.tensor_scalar(
-            out=neg_alpha_n[:], in0=alpha, scalar1=-1.0 / P, scalar2=None, op0=ALU.mult
-        )
-        rest = keep.tile([P, N_TILES], F32, name="rest")
-        nc.vector.tensor_tensor(out=rest[:], in0=one_m_alpha[:], in1=blin, op=ALU.mult)
+        def quantise_a(b0, b1):
+            quantise(
+                a_codes[:, 256 * b0 : 256 * b1], a_scales[:, 256 * b0 : 256 * b1], a_grp[:, 1024 * b0 : 1024 * b1]
+            )
 
         h_acc = []
         for b in range(2):
@@ -150,11 +154,14 @@ def tile_gnnlayer_pb_kernel(
         w_codes = {}
         w_scales = {}
 
-        def regroup_chunk(i):
-            v_cols = C // 2 if i == N_POST - 1 else V_COLS
+        def regroup_cols(i, r, lo, hi, v_cols):
+            g = grouped[i]
+            mid = lo + v_cols
+            regroup(nc.vector.tensor_copy, g[:, lo:mid, :], r[:, :, 0:v_cols])
+            regroup(nc.scalar.copy, g[:, mid:hi, :], r[:, :, v_cols : hi - lo])
+
+        def open_chunk(i):
             g = grp_pool.tile([P, C, PACK], BF16, name="grp%d" % i, tag="grp", align_bytes=64)
-            regroup(nc.vector.tensor_copy, g[:, 0:v_cols, :], raw[i][:, :, 0:v_cols])
-            regroup(nc.scalar.copy, g[:, v_cols:C, :], raw[i][:, :, v_cols:C])
             grouped[i] = g
             cd = keep.tile([P, C], U32, name="w_codes%d" % i, align_bytes=64)
             sc = keep.tile([P, C], U8, name="w_scales%d" % i, align_bytes=64)
@@ -181,12 +188,61 @@ def tile_gnnlayer_pb_kernel(
                     stop=(i == N_POST - 1 and t == HALF - 1),
                 )
 
-        for i in range(N_POST):
-            regroup_chunk(i)
+        for i in range(len(FIRST_PIECES)):
+            open_chunk(i)
+            for lo, hi in FIRST_PIECES[i]:
+                regroup_cols(i, first_raw[(i, lo)], lo, hi, FIRST_V_COLS[hi - lo])
+                if hi % (C // 2) == 0:
+                    quantise_chunk(i, hi - C // 2, hi)
+
+        def regroup_chunk(i, v_cols):
+            open_chunk(i)
+            regroup_cols(i, raw[i], 0, C, v_cols)
             load_next()
-            if i > 0:
-                quantise_chunk(i - 1, 0, C)
-                first_product(i - 1, range(N_TILES))
+
+        regroup_chunk(2, V_COLS)
+        regroup_chunk(3, V_COLS)
+        quantise_chunk(2, 0, C)
+        for b in range(N_POST // 2):
+            turn(b)
+        quantise_chunk(3, 0, C)
+        quantise_a(0, 1)
+        regroup_chunk(4, V_COLS)
+        quantise_a(1, 5)
+        for i in range(A_AFTER):
+            first_product(i, range(N_TILES))
+        regroup_chunk(5, V_COLS)
+        quantise_chunk(4, 0, C)
+        first_product(4, range(N_TILES))
+        par_t = psum.tile([P, P], BF16, name="par_t", tag="bank7")
+        nc.tensor.transpose(par_t[:], par_rows[:], ident_bf[:])
+        for i in range(A_AFTER + 2, N_POST - 2):
+            regroup_chunk(i, C // 2 if i == N_POST - 1 else V_COLS)
+            quantise_chunk(i - 1, 0, C)
+            first_product(i - 1, range(N_TILES))
+
+        par = keep.tile([P, 5 * N_TILES], F32, name="par")
+        nc.scalar.copy(out=par[:], in_=par_t[:, 0 : 5 * N_TILES])
+        bpost = par[:, 0:8]
+        blin = par[:, 8:16]
+        gw = par[:, 16:24]
+        gb = par[:, 24:32]
+        alpha = par[:, 32:40]
+        one_m_alpha = keep.tile([P, N_TILES], F32, name="one_m_alpha")
+        nc.gpsimd.tensor_scalar(
+            out=one_m_alpha[:], in0=alpha, scalar1=-1.0, scalar2=1.0, op0=ALU.mult, op1=ALU.add
+        )
+        neg_alpha_n = keep.tile([P, N_TILES], F32, name="neg_alpha_n")
+        nc.gpsimd.tensor_scalar(
+            out=neg_alpha_n[:], in0=alpha, scalar1=-1.0 / P, scalar2=0.0, op0=ALU.mult, op1=ALU.add
+        )
+        rest = keep.tile([P, N_TILES], F32, name="rest")
+        nc.gpsimd.tensor_tensor(out=rest[:], in0=one_m_alpha[:], in1=blin, op=ALU.mult)
+
+        for i in range(N_POST - 2, N_POST):
+            regroup_chunk(i, C // 2 if i == N_POST - 1 else V_COLS)
+            quantise_chunk(i - 1, 0, C)
+            first_product(i - 1, range(N_TILES))
 
         l_grp = {}
         l_codes = {}
@@ -299,7 +355,7 @@ def tile_gnnlayer_pb_kernel(
             vec_op(v_bias[:, sl], v_rstd[:, sl], v_ws[:, sl], ALU.mult)
             vec_op(v_bias[:, sl], v_bias[:, sl], gb[:, sl], ALU.add)
 
-        junk = keep.tile([P, P], BF16, name="junk")
+        junk = [keep.tile([P, P], BF16, name="junk%d" % m) for m in range(2 * HALF)]
         s_sum = small("s_sum")
         s_sq = small("s_sq")
         s_shift = small("s_shift")
@@ -310,7 +366,7 @@ def tile_gnnlayer_pb_kernel(
         def norm_on_scalar(tiles):
             for m in tiles:
                 nc.scalar.activation(
-                    out=junk[:], in_=o_acc[m][:], func=ACT.Identity, accum_out=col(s_sum, m)
+                    out=junk[m - HALF][:], in_=o_acc[m][:], func=ACT.Identity, accum_out=col(s_sum, m)
                 )
             for m in tiles:
                 nc.scalar.activation(
@@ -319,7 +375,7 @@ def tile_gnnlayer_pb_kernel(
                 )
             for m in tiles:
                 nc.scalar.activation(
-                    out=junk[:], in_=o_acc[m][:], func=ACT.Square, bias=col(s_shift, m), scale=1.0,
+                    out=junk[m][:], in_=o_acc[m][:], func=ACT.Square, bias=col(s_shift, m), scale=1.0,
                     accum_out=col(s_sq, m),
                 )
             sl = slice(tiles[0], tiles[-1] + 1)

@@ -23,15 +23,12 @@ HALF = N_TILES // 2
 EPS_GN = 1e-5
 FLOPS = 2 * P * (K_POST * C + C * C)
 
-V_COLS = 480
-FIRST_PIECES = (((0, 256), (256, 512), (512, 1024)), ((0, 512), (512, 1024)))
-FIRST_V_COLS = {256: 120, 512: 240}
+V_COLS = 512
 A_AFTER = 4
 RAW_BUFS = 7
 GRP_BUFS = 4
-LIN_COLS = 256
-N_PIECES = C // LIN_COLS
-LIN_ON_VECTOR = ((0, 0), (1, 0))
+LAST_V_COLS = 256
+LIN_V_COLS = (192, 128)
 O_BANK = (2, 3, 4, 5, 6, 7, 0, 1)
 
 
@@ -61,22 +58,12 @@ def tile_gnnlayer_pb_kernel(
 
         x_sb = keep.tile([P, C], BF16, name="x_sb")
         agg_sb = keep.tile([P, 4 * C], BF16, name="agg_sb")
-        agg_rows = agg.rearrange("b n c -> (b n) c")
         out_rows = out.rearrange("b n c -> (b n) c")
 
         raw = []
-        first_raw = {}
 
         def post_rows(i):
             return W_post[K_PASS * i : K_PASS * (i + 1), :].rearrange("(p j) c -> p j c", j=PACK)
-
-        def load_pieces():
-            for i in range(len(FIRST_PIECES)):
-                raw.append(None)
-                for lo, hi in FIRST_PIECES[i]:
-                    r = keep.tile([P, PACK, hi - lo], BF16, name="raw%d_%d" % (i, lo))
-                    nc.sync.dma_start(out=r[:], in_=post_rows(i)[:, :, lo:hi])
-                    first_raw[(i, lo)] = r
 
         def load_next():
             i = len(raw)
@@ -85,31 +72,25 @@ def tile_gnnlayer_pb_kernel(
                 nc.sync.dma_start(out=r[:], in_=post_rows(i))
                 raw.append(r)
             elif i < N_POST + 2:
-                h = i - N_POST
-                r = raw_pool.tile([P, N_LIN * PACK, C // 2], BF16, name="raw%d" % i, tag="raw")
+                gg = i - N_POST
+                r = raw_pool.tile([P, PACK, C], BF16, name="raw%d" % i, tag="raw")
                 nc.sync.dma_start(
                     out=r[:],
-                    in_=W_lin.rearrange("(a p) n -> p a n", p=P)[:, :, (C // 2) * h : (C // 2) * (h + 1)],
+                    in_=W_lin[K_PASS * gg : K_PASS * (gg + 1), :].rearrange("(a p) n -> p a n", p=P),
                 )
                 raw.append(r)
 
-        def load_agg(h):
-            cols = slice(2 * C * h, 2 * C * (h + 1))
-            nc.sync.dma_start(out=agg_sb[:, cols], in_=agg_rows[:, cols])
-
-        load_pieces()
-        for i in range(len(FIRST_PIECES), A_AFTER):
+        for i in range(A_AFTER):
             load_next()
         nc.sync.dma_start(out=x_sb[:], in_=x.rearrange("b n c -> (b n) c"))
-        load_agg(0)
-        load_agg(1)
+        nc.sync.dma_start(out=agg_sb[:], in_=agg.rearrange("b n c -> (b n) c"))
         load_next()
         for v, vec in enumerate((b_post, b_lin, gn_weight, gn_bias, gn_alpha)):
             nc.sync.dma_start(
                 out=par_rows[N_TILES * v : N_TILES * (v + 1), :],
                 in_=vec.rearrange("(t p) -> t p", p=P),
             )
-        for i in range(A_AFTER + 1, RAW_BUFS + 1):
+        for i in range(A_AFTER + 1, RAW_BUFS - 1):
             load_next()
 
         def regroup(copy, dst, src):
@@ -154,11 +135,10 @@ def tile_gnnlayer_pb_kernel(
         w_codes = {}
         w_scales = {}
 
-        def regroup_cols(i, r, lo, hi, v_cols):
-            g = grouped[i]
+        def regroup_cols(i, lo, hi, v_cols):
             mid = lo + v_cols
-            regroup(nc.vector.tensor_copy, g[:, lo:mid, :], r[:, :, 0:v_cols])
-            regroup(nc.scalar.copy, g[:, mid:hi, :], r[:, :, v_cols : hi - lo])
+            regroup(nc.vector.tensor_copy, grouped[i][:, lo:mid, :], raw[i][:, :, lo:mid])
+            regroup(nc.scalar.copy, grouped[i][:, mid:hi, :], raw[i][:, :, mid:hi])
 
         def open_chunk(i):
             g = grp_pool.tile([P, C, PACK], BF16, name="grp%d" % i, tag="grp", align_bytes=64)
@@ -188,36 +168,33 @@ def tile_gnnlayer_pb_kernel(
                     stop=(i == N_POST - 1 and t == HALF - 1),
                 )
 
-        for i in range(len(FIRST_PIECES)):
+        def regroup_chunk(i):
             open_chunk(i)
-            for lo, hi in FIRST_PIECES[i]:
-                regroup_cols(i, first_raw[(i, lo)], lo, hi, FIRST_V_COLS[hi - lo])
-                if hi % (C // 2) == 0:
-                    quantise_chunk(i, hi - C // 2, hi)
-
-        def regroup_chunk(i, v_cols):
-            open_chunk(i)
-            regroup_cols(i, raw[i], 0, C, v_cols)
+            regroup_cols(i, 0, C, V_COLS)
             load_next()
 
-        regroup_chunk(2, V_COLS)
-        regroup_chunk(3, V_COLS)
+        regroup_chunk(0)
+        regroup_chunk(1)
+        quantise_chunk(0, 0, C)
+        regroup_chunk(2)
+        quantise_chunk(1, 0, C)
+        regroup_chunk(3)
         quantise_chunk(2, 0, C)
         for b in range(N_POST // 2):
             turn(b)
         quantise_chunk(3, 0, C)
         quantise_a(0, 1)
-        regroup_chunk(4, V_COLS)
+        regroup_chunk(4)
         quantise_a(1, 5)
         for i in range(A_AFTER):
             first_product(i, range(N_TILES))
-        regroup_chunk(5, V_COLS)
+        regroup_chunk(5)
         quantise_chunk(4, 0, C)
         first_product(4, range(N_TILES))
         par_t = psum.tile([P, P], BF16, name="par_t", tag="bank7")
         nc.tensor.transpose(par_t[:], par_rows[:], ident_bf[:])
         for i in range(A_AFTER + 2, N_POST - 2):
-            regroup_chunk(i, C // 2 if i == N_POST - 1 else V_COLS)
+            regroup_chunk(i)
             quantise_chunk(i - 1, 0, C)
             first_product(i - 1, range(N_TILES))
 
@@ -239,39 +216,31 @@ def tile_gnnlayer_pb_kernel(
         rest = keep.tile([P, N_TILES], F32, name="rest")
         nc.gpsimd.tensor_tensor(out=rest[:], in0=one_m_alpha[:], in1=blin, op=ALU.mult)
 
-        for i in range(N_POST - 2, N_POST):
-            regroup_chunk(i, C // 2 if i == N_POST - 1 else V_COLS)
-            quantise_chunk(i - 1, 0, C)
-            first_product(i - 1, range(N_TILES))
+        regroup_chunk(N_POST - 2)
+        quantise_chunk(N_POST - 3, 0, C)
+        first_product(N_POST - 3, range(N_TILES))
 
-        l_grp = {}
-        l_codes = {}
-        l_scales = {}
+        l_grp = []
+        for gg in range(N_LIN):
+            g = keep.tile([P, C, PACK], BF16, name="l_grp%d" % gg, align_bytes=64)
+            l_grp.append(g)
+        l_codes = keep.tile([P, N_LIN, C], U32, name="l_codes", align_bytes=64)
+        l_scales = keep.tile([P, N_LIN, C], U8, name="l_scales", align_bytes=64)
 
-        def regroup_piece(j):
-            g = keep.tile([P, N_LIN, LIN_COLS, PACK], BF16, name="l_grp%d" % j, align_bytes=64)
-            c0 = LIN_COLS * j
-            r = raw[N_POST + c0 // (C // 2)]
-            c0 = c0 % (C // 2)
-            for gg in range(N_LIN):
-                on_vector = (j, gg) in LIN_ON_VECTOR
-                regroup(
-                    nc.vector.tensor_copy if on_vector else nc.scalar.copy,
-                    g[:, gg, :, :],
-                    r[:, PACK * gg : PACK * (gg + 1), c0 : c0 + LIN_COLS],
-                )
-            l_grp[j] = g
+        def regroup_lin(gg, lo, hi, v_cols):
+            mid = lo + v_cols
+            r = raw[N_POST + gg]
+            if v_cols > 0:
+                regroup(nc.vector.tensor_copy, l_grp[gg][:, lo:mid, :], r[:, :, lo:mid])
+            if mid < hi:
+                regroup(nc.scalar.copy, l_grp[gg][:, mid:hi, :], r[:, :, mid:hi])
 
-        def quantise_piece(j):
-            cd = keep.tile([P, N_LIN, LIN_COLS], U32, name="l_codes%d" % j, align_bytes=64)
-            sc = keep.tile([P, N_LIN, LIN_COLS], U8, name="l_scales%d" % j, align_bytes=64)
+        def quantise_lin(gg, lo, hi):
             quantise(
-                cd[:].rearrange("p g c -> p (g c)"),
-                sc[:].rearrange("p g c -> p (g c)"),
-                l_grp[j][:].rearrange("p g c t -> p (g c t)"),
+                l_codes[:, gg, lo:hi],
+                l_scales[:, gg, lo:hi],
+                l_grp[gg][:, lo:hi, :].rearrange("p c t -> p (c t)"),
             )
-            l_codes[j] = cd
-            l_scales[j] = sc
 
         h_grp = keep.tile([P, N_LIN, P, PACK], BF16, name="h_grp", align_bytes=64)
         h_codes = keep.tile([P, N_LIN, P], U32, name="h_codes", align_bytes=64)
@@ -294,13 +263,12 @@ def tile_gnnlayer_pb_kernel(
 
         def second_product(m):
             o_m = psum.tile([P, P], F32, name="o_acc%d" % m, tag="bank%d" % O_BANK[m])
-            j = (P * m) // LIN_COLS
-            k = (P * m) % LIN_COLS
+            k = P * m
             for gg in range(N_LIN):
                 nc.tensor.matmul_mx(
                     out=o_m[:],
-                    lhsT=l_codes[j][:, gg, k : k + P].bitcast(FP8X4),
-                    lhsT_scale=l_scales[j][:, gg, k : k + P],
+                    lhsT=l_codes[:, gg, k : k + P].bitcast(FP8X4),
+                    lhsT_scale=l_scales[:, gg, k : k + P],
                     rhs=h_codes[:, gg, :].bitcast(FP8X4),
                     rhs_scale=h_scales[:, gg, :],
                     start=(gg == 0),
@@ -318,91 +286,115 @@ def tile_gnnlayer_pb_kernel(
         def col(t, m):
             return t[:, m : m + 1]
 
+        def span(t, tiles):
+            return t[:, tiles[0] : tiles[-1] + 1]
+
         def vec_op(o, a, b, op):
             nc.vector.tensor_tensor(out=o, in0=a, in1=b, op=op)
 
-        stats = keep.tile([P, HALF, 6], F32, name="stats")
-        mean_var = keep.tile([P, HALF, 2], F32, name="mean_var")
-        v_mu = small("v_mu")
-        v_var = small("v_var")
-        v_shift = small("v_shift")
-        v_ws = small("v_ws")
-        v_rstd = small("v_rstd")
-        v_scale = small("v_scale")
-        v_bias = small("v_bias")
+        stats = keep.tile([P, N_TILES, 6], F32, name="stats")
+        mean_var = keep.tile([P, N_TILES, 2], F32, name="mean_var")
+        sums = small("sums")
+        squares = small("squares")
+        junk = [keep.tile([P, P], BF16, name="junk%d" % m) for m in range(2 * N_TILES)]
+        centre = small("centre")
+        second = small("second")
+        shift = small("shift")
+        shift_w = small("shift_w")
+        rstd = small("rstd")
+        scale = small("scale")
+        bias = small("bias")
 
-        def norm_on_vector_stats(tiles):
+        def stats_on_vector(tiles):
             for m in tiles:
                 nc.vector.bn_stats(out=stats[:, m, :], in_=o_acc[m][:])
             for m in tiles:
                 nc.vector.bn_aggr(out=mean_var[:, m, :], in_=stats[:, m, :])
 
-        def norm_on_vector_scalars():
-            sl = slice(0, HALF)
-            mean = mean_var[:, :, 0]
-            var = mean_var[:, :, 1]
-            vec_op(v_mu[:, sl], mean, one_m_alpha[:, sl], ALU.mult)
-            vec_op(v_mu[:, sl], v_mu[:, sl], rest[:, sl], ALU.add)
-            vec_op(v_var[:, sl], v_mu[:, sl], v_mu[:, sl], ALU.mult)
-            vec_op(v_var[:, sl], v_var[:, sl], var, ALU.add)
+        def centre_on_vector(tiles):
+            for m in tiles:
+                nc.vector.tensor_scalar(
+                    out=col(centre, m), in0=mean_var[:, m, 0:1], scalar1=col(one_m_alpha, m),
+                    scalar2=col(rest, m), op0=ALU.mult, op1=ALU.add,
+                )
+            for m in tiles:
+                nc.vector.scalar_tensor_tensor(
+                    out=col(second, m), in0=col(centre, m), scalar=col(centre, m),
+                    in1=mean_var[:, m, 1:2], op0=ALU.mult, op1=ALU.add,
+                )
+            first = tiles[0]
+            last_one = tiles[-1] + 1
+            vec_op(span(shift, tiles), span(centre, tiles), mean_var[:, first:last_one, 0], ALU.subtract)
+            vec_op(span(shift_w, tiles), span(shift, tiles), span(gw, tiles), ALU.mult)
+
+        def centre_wide(tiles):
+            first = tiles[0]
+            end = tiles[-1] + 1
+            vec_op(span(centre, tiles), mean_var[:, first:end, 0], span(one_m_alpha, tiles), ALU.mult)
+            vec_op(span(centre, tiles), span(centre, tiles), span(rest, tiles), ALU.add)
+            vec_op(span(second, tiles), span(centre, tiles), span(centre, tiles), ALU.mult)
+            vec_op(span(second, tiles), span(second, tiles), mean_var[:, first:end, 1], ALU.add)
+            vec_op(span(shift, tiles), span(centre, tiles), mean_var[:, first:end, 0], ALU.subtract)
+            vec_op(span(shift_w, tiles), span(shift, tiles), span(gw, tiles), ALU.mult)
+
+        def affine_wide(tiles):
+            vec_op(span(scale, tiles), span(rstd, tiles), span(gw, tiles), ALU.mult)
+            vec_op(span(bias, tiles), span(rstd, tiles), span(shift_w, tiles), ALU.mult)
+            vec_op(span(bias, tiles), span(bias, tiles), span(gb, tiles), ALU.add)
+
+        def rstd_on_scalar(tiles, moments, factor):
             nc.scalar.activation(
-                out=v_rstd[:, sl], in_=v_var[:, sl], func=ACT.Abs_reciprocal_sqrt,
-                bias=eps[:, 0:1], scale=1.0,
+                out=span(rstd, tiles), in_=span(moments, tiles), func=ACT.Abs_reciprocal_sqrt,
+                bias=eps[:, 0:1], scale=factor,
             )
-            vec_op(v_shift[:, sl], v_mu[:, sl], mean, ALU.subtract)
-            vec_op(v_ws[:, sl], v_shift[:, sl], gw[:, sl], ALU.mult)
-            vec_op(v_scale[:, sl], v_rstd[:, sl], gw[:, sl], ALU.mult)
-            vec_op(v_bias[:, sl], v_rstd[:, sl], v_ws[:, sl], ALU.mult)
-            vec_op(v_bias[:, sl], v_bias[:, sl], gb[:, sl], ALU.add)
 
-        junk = [keep.tile([P, P], BF16, name="junk%d" % m) for m in range(2 * HALF)]
-        s_sum = small("s_sum")
-        s_sq = small("s_sq")
-        s_shift = small("s_shift")
-        s_rstd = small("s_rstd")
-        s_scale = small("s_scale")
-        s_bias = small("s_bias")
+        def affine_on_vector(tiles):
+            vec_op(span(scale, tiles), span(rstd, tiles), span(gw, tiles), ALU.mult)
+            for m in tiles:
+                nc.vector.scalar_tensor_tensor(
+                    out=col(bias, m), in0=col(shift_w, m), scalar=col(rstd, m), in1=col(gb, m),
+                    op0=ALU.mult, op1=ALU.add,
+                )
 
-        def norm_on_scalar(tiles):
+        def moments_on_scalar(tiles):
             for m in tiles:
                 nc.scalar.activation(
-                    out=junk[m - HALF][:], in_=o_acc[m][:], func=ACT.Identity, accum_out=col(s_sum, m)
+                    out=junk[m][:], in_=o_acc[m][:], func=ACT.Identity, accum_out=col(sums, m)
                 )
             for m in tiles:
                 nc.scalar.activation(
-                    out=col(s_shift, m), in_=col(s_sum, m), func=ACT.Identity,
+                    out=col(shift, m), in_=col(sums, m), func=ACT.Identity,
                     bias=col(rest, m), scale=col(neg_alpha_n, m),
                 )
             for m in tiles:
                 nc.scalar.activation(
-                    out=junk[m][:], in_=o_acc[m][:], func=ACT.Square, bias=col(s_shift, m), scale=1.0,
-                    accum_out=col(s_sq, m),
+                    out=junk[N_TILES + m][:], in_=o_acc[m][:], func=ACT.Square, bias=col(shift, m), scale=1.0,
+                    accum_out=col(squares, m),
                 )
-            sl = slice(tiles[0], tiles[-1] + 1)
-            nc.scalar.activation(
-                out=s_rstd[:, sl], in_=s_sq[:, sl], func=ACT.Abs_reciprocal_sqrt,
-                bias=eps[:, 0:1], scale=1.0 / P,
-            )
+
+        def affine_on_scalar(tiles):
             for m in tiles:
                 nc.scalar.activation(
-                    out=col(s_scale, m), in_=col(s_rstd, m), func=ACT.Copy, scale=gw[:, m : m + 1]
+                    out=col(scale, m), in_=col(rstd, m), func=ACT.Copy, scale=col(gw, m)
                 )
             for m in tiles:
                 nc.scalar.activation(
-                    out=col(s_bias, m), in_=col(s_shift, m), func=ACT.Identity,
-                    bias=gb[:, m : m + 1], scale=col(s_scale, m),
+                    out=col(bias, m), in_=col(shift, m), func=ACT.Identity,
+                    bias=col(gb, m), scale=col(scale, m),
                 )
 
-        def apply_on_scalar(m, scale, bias):
-            nc.scalar.activation(
-                out=y_sb[:, m, :], in_=o_acc[m][:], func=ACT.Relu, bias=col(bias, m), scale=col(scale, m)
-            )
+        def apply_on_scalar(tiles):
+            for m in tiles:
+                nc.scalar.activation(
+                    out=y_sb[:, m, :], in_=o_acc[m][:], func=ACT.Relu, bias=col(bias, m), scale=col(scale, m)
+                )
 
-        def apply_on_vector(m, scale, bias):
-            nc.vector.tensor_scalar(
-                out=y_sb[:, m, :], in0=o_acc[m][:], scalar1=col(scale, m), scalar2=col(bias, m),
-                op0=ALU.mult, op1=ALU.add,
-            )
+        def apply_on_vector(tiles):
+            for m in tiles:
+                nc.vector.tensor_scalar(
+                    out=y_sb[:, m, :], in0=o_acc[m][:], scalar1=col(scale, m), scalar2=col(bias, m),
+                    op0=ALU.mult, op1=ALU.add,
+                )
 
         def finish(tiles):
             m0 = tiles[0]
@@ -416,35 +408,46 @@ def tile_gnnlayer_pb_kernel(
             nc.sync.dma_start(out=out_rows[:, cols], in_=o_sb[:, cols])
 
         last = N_POST - 1
-        quantise_chunk(last, 0, C // 2)
+        half = C // 2
+        open_chunk(last)
+        regroup_cols(last, 0, half, LAST_V_COLS)
+        quantise_chunk(last - 1, 0, C)
+        first_product(last - 1, range(N_TILES))
+        regroup_cols(last, half, C, LAST_V_COLS)
+        quantise_chunk(last, 0, half)
         first_product(last, range(0, HALF))
-        regroup_piece(0)
-        quantise_chunk(last, C // 2, C)
+        quantise_chunk(last, half, C)
         first_product(last, range(HALF, N_TILES))
-        regroup_piece(1)
-        regroup_piece(2)
+        regroup_lin(0, 0, half, LIN_V_COLS[0])
         add_bias(0)
-        quantise_piece(0)
-        quantise_h(0)
+        regroup_lin(0, half, C, LIN_V_COLS[0])
         add_bias(1)
+        quantise_lin(0, 0, half)
+        quantise_h(0)
         quantise_h(1)
-        regroup_piece(3)
-        for j in range(N_PIECES):
-            if j > 0:
-                quantise_piece(j)
-            second_product(2 * j)
-            second_product(2 * j + 1)
-            if j == 2:
-                norm_on_vector_stats((0, 1, 2, 3))
-        norm_on_scalar((4, 5))
-        for m in (4, 5):
-            apply_on_scalar(m, s_scale, s_bias)
-        norm_on_vector_scalars()
+        regroup_lin(1, 0, half, LIN_V_COLS[1])
+        quantise_lin(0, half, C)
+        quantise_lin(1, 0, half)
         for m in range(HALF):
-            apply_on_vector(m, v_scale, v_bias)
+            second_product(m)
+        regroup_lin(1, half, C, LIN_V_COLS[1])
+        quantise_lin(1, half, C)
+        for m in range(HALF, N_TILES):
+            second_product(m)
+        early = (0, 1, 2, 3)
+        late = (4, 5, 6, 7)
+        moments_on_scalar(early)
+        stats_on_vector(late)
+        rstd_on_scalar(early, squares, 1.0 / P)
+        centre_wide(late)
+        affine_on_scalar(early)
+        apply_on_scalar((0, 1))
+        rstd_on_scalar(late, second, 1.0)
+        apply_on_scalar((2, 3))
+        affine_wide(late)
+        finish((0, 1))
+        finish((2, 3))
+        apply_on_scalar((4, 5))
+        apply_on_vector((6, 7))
         finish((4, 5))
-        norm_on_scalar((6, 7))
-        finish((0, 1, 2, 3))
-        for m in (6, 7):
-            apply_on_scalar(m, s_scale, s_bias)
         finish((6, 7))

@@ -23,12 +23,12 @@ HALF = N_TILES // 2
 EPS_GN = 1e-5
 FLOPS = 2 * P * (K_POST * C + C * C)
 
-V_COLS = 512
+V_COLS = 496
 A_AFTER = 4
 RAW_BUFS = 7
 GRP_BUFS = 4
 LAST_V_COLS = 256
-LIN_V_COLS = (192, 128)
+LIN_V_COLS = 128
 O_BANK = (2, 3, 4, 5, 6, 7, 0, 1)
 
 
@@ -83,7 +83,9 @@ def tile_gnnlayer_pb_kernel(
         for i in range(A_AFTER):
             load_next()
         nc.sync.dma_start(out=x_sb[:], in_=x.rearrange("b n c -> (b n) c"))
-        nc.sync.dma_start(out=agg_sb[:], in_=agg.rearrange("b n c -> (b n) c"))
+        agg_rows = agg.rearrange("b n c -> (b n) c")
+        for lo in (0, 2 * C):
+            nc.sync.dma_start(out=agg_sb[:, lo : lo + 2 * C], in_=agg_rows[:, lo : lo + 2 * C])
         load_next()
         for v, vec in enumerate((b_post, b_lin, gn_weight, gn_bias, gn_alpha)):
             nc.sync.dma_start(
@@ -261,20 +263,20 @@ def tile_gnnlayer_pb_kernel(
 
         o_acc = {}
 
-        def second_product(m):
-            o_m = psum.tile([P, P], F32, name="o_acc%d" % m, tag="bank%d" % O_BANK[m])
-            k = P * m
-            for gg in range(N_LIN):
+        def second_product(gg, tiles):
+            for m in tiles:
+                if gg == 0:
+                    o_m = psum.tile([P, P], F32, name="o_acc%d" % m, tag="bank%d" % O_BANK[m])
+                    o_acc[m] = o_m
                 nc.tensor.matmul_mx(
-                    out=o_m[:],
-                    lhsT=l_codes[:, gg, k : k + P].bitcast(FP8X4),
-                    lhsT_scale=l_scales[:, gg, k : k + P],
+                    out=o_acc[m][:],
+                    lhsT=l_codes[:, gg, P * m : P * (m + 1)].bitcast(FP8X4),
+                    lhsT_scale=l_scales[:, gg, P * m : P * (m + 1)],
                     rhs=h_codes[:, gg, :].bitcast(FP8X4),
                     rhs_scale=h_scales[:, gg, :],
                     start=(gg == 0),
                     stop=(gg == N_LIN - 1),
                 )
-            o_acc[m] = o_m
 
         y_sb = keep.tile([P, N_TILES, P], F32, name="y_sb")
         o_sb = keep.tile([P, C], F32, name="o_sb")
@@ -409,6 +411,8 @@ def tile_gnnlayer_pb_kernel(
 
         last = N_POST - 1
         half = C // 2
+        early = (0, 1, 2, 3)
+        late = (4, 5, 6, 7)
         open_chunk(last)
         regroup_cols(last, 0, half, LAST_V_COLS)
         quantise_chunk(last - 1, 0, C)
@@ -418,36 +422,32 @@ def tile_gnnlayer_pb_kernel(
         first_product(last, range(0, HALF))
         quantise_chunk(last, half, C)
         first_product(last, range(HALF, N_TILES))
-        regroup_lin(0, 0, half, LIN_V_COLS[0])
+        regroup_lin(0, 0, half, LIN_V_COLS)
         add_bias(0)
-        regroup_lin(0, half, C, LIN_V_COLS[0])
+        regroup_lin(0, half, C, LIN_V_COLS)
         add_bias(1)
         quantise_lin(0, 0, half)
         quantise_h(0)
+        second_product(0, early)
         quantise_h(1)
-        regroup_lin(1, 0, half, LIN_V_COLS[1])
+        regroup_lin(1, 0, half, LIN_V_COLS)
         quantise_lin(0, half, C)
+        second_product(0, late)
         quantise_lin(1, 0, half)
-        for m in range(HALF):
-            second_product(m)
-        regroup_lin(1, half, C, LIN_V_COLS[1])
+        second_product(1, early)
+        regroup_lin(1, half, C, LIN_V_COLS)
         quantise_lin(1, half, C)
-        for m in range(HALF, N_TILES):
-            second_product(m)
-        early = (0, 1, 2, 3)
-        late = (4, 5, 6, 7)
+        second_product(1, late)
         moments_on_scalar(early)
         stats_on_vector(late)
         rstd_on_scalar(early, squares, 1.0 / P)
         centre_wide(late)
         affine_on_scalar(early)
-        apply_on_scalar((0, 1))
+        apply_on_scalar(early)
         rstd_on_scalar(late, second, 1.0)
-        apply_on_scalar((2, 3))
         affine_wide(late)
         finish((0, 1))
         finish((2, 3))
-        apply_on_scalar((4, 5))
-        apply_on_vector((6, 7))
+        apply_on_scalar(late)
         finish((4, 5))
         finish((6, 7))

@@ -23,12 +23,12 @@ HALF = N_TILES // 2
 EPS_GN = 1e-5
 FLOPS = 2 * P * (K_POST * C + C * C)
 
-V_COLS = 496
+V_COLS = C // 2
 A_AFTER = 4
 RAW_BUFS = 7
 GRP_BUFS = 4
-LAST_V_COLS = 256
-LIN_V_COLS = 128
+LAST_V_COLS = C // 4
+LIN_V_COLS = (192, 128)
 O_BANK = (2, 3, 4, 5, 6, 7, 0, 1)
 
 
@@ -298,7 +298,7 @@ def tile_gnnlayer_pb_kernel(
         mean_var = keep.tile([P, N_TILES, 2], F32, name="mean_var")
         sums = small("sums")
         squares = small("squares")
-        junk = [keep.tile([P, P], BF16, name="junk%d" % m) for m in range(2 * N_TILES)]
+        junk = [keep.tile([P, P], BF16, name="junk%d" % m) for m in range(N_TILES)]
         centre = small("centre")
         second = small("second")
         shift = small("shift")
@@ -329,21 +329,6 @@ def tile_gnnlayer_pb_kernel(
             vec_op(span(shift, tiles), span(centre, tiles), mean_var[:, first:last_one, 0], ALU.subtract)
             vec_op(span(shift_w, tiles), span(shift, tiles), span(gw, tiles), ALU.mult)
 
-        def centre_wide(tiles):
-            first = tiles[0]
-            end = tiles[-1] + 1
-            vec_op(span(centre, tiles), mean_var[:, first:end, 0], span(one_m_alpha, tiles), ALU.mult)
-            vec_op(span(centre, tiles), span(centre, tiles), span(rest, tiles), ALU.add)
-            vec_op(span(second, tiles), span(centre, tiles), span(centre, tiles), ALU.mult)
-            vec_op(span(second, tiles), span(second, tiles), mean_var[:, first:end, 1], ALU.add)
-            vec_op(span(shift, tiles), span(centre, tiles), mean_var[:, first:end, 0], ALU.subtract)
-            vec_op(span(shift_w, tiles), span(shift, tiles), span(gw, tiles), ALU.mult)
-
-        def affine_wide(tiles):
-            vec_op(span(scale, tiles), span(rstd, tiles), span(gw, tiles), ALU.mult)
-            vec_op(span(bias, tiles), span(rstd, tiles), span(shift_w, tiles), ALU.mult)
-            vec_op(span(bias, tiles), span(bias, tiles), span(gb, tiles), ALU.add)
-
         def rstd_on_scalar(tiles, moments, factor):
             nc.scalar.activation(
                 out=span(rstd, tiles), in_=span(moments, tiles), func=ACT.Abs_reciprocal_sqrt,
@@ -370,7 +355,7 @@ def tile_gnnlayer_pb_kernel(
                 )
             for m in tiles:
                 nc.scalar.activation(
-                    out=junk[N_TILES + m][:], in_=o_acc[m][:], func=ACT.Square, bias=col(shift, m), scale=1.0,
+                    out=junk[HALF + m][:], in_=o_acc[m][:], func=ACT.Square, bias=col(shift, m), scale=1.0,
                     accum_out=col(squares, m),
                 )
 
@@ -422,32 +407,35 @@ def tile_gnnlayer_pb_kernel(
         first_product(last, range(0, HALF))
         quantise_chunk(last, half, C)
         first_product(last, range(HALF, N_TILES))
-        regroup_lin(0, 0, half, LIN_V_COLS)
+        regroup_lin(0, 0, half, LIN_V_COLS[0])
         add_bias(0)
-        regroup_lin(0, half, C, LIN_V_COLS)
+        regroup_lin(0, half, C, LIN_V_COLS[0])
         add_bias(1)
         quantise_lin(0, 0, half)
         quantise_h(0)
         second_product(0, early)
         quantise_h(1)
-        regroup_lin(1, 0, half, LIN_V_COLS)
+        regroup_lin(1, 0, half, LIN_V_COLS[1])
         quantise_lin(0, half, C)
         second_product(0, late)
         quantise_lin(1, 0, half)
         second_product(1, early)
-        regroup_lin(1, half, C, LIN_V_COLS)
-        quantise_lin(1, half, C)
-        second_product(1, late)
+        regroup_lin(1, half, C, LIN_V_COLS[1])
+        for lo in (half, half + C // 4):
+            quantise_lin(1, lo, lo + C // 4)
+            second_product(1, (lo // P, lo // P + 1))
         moments_on_scalar(early)
         stats_on_vector(late)
         rstd_on_scalar(early, squares, 1.0 / P)
-        centre_wide(late)
+        centre_on_vector(late)
         affine_on_scalar(early)
-        apply_on_scalar(early)
+        apply_on_scalar(early[:1])
         rstd_on_scalar(late, second, 1.0)
-        affine_wide(late)
+        apply_on_scalar(early[1:])
+        affine_on_vector(late)
+        apply_on_scalar((6, 7))
+        apply_on_vector((4, 5))
         finish((0, 1))
         finish((2, 3))
-        apply_on_scalar(late)
         finish((4, 5))
         finish((6, 7))

@@ -28,7 +28,7 @@ A_AFTER = 4
 RAW_BUFS = 7
 GRP_BUFS = 4
 LAST_V_COLS = C // 4
-LIN_V_COLS = (192, 128)
+LIN_V_COLS = (384, 128)
 O_BANK = (2, 3, 4, 5, 6, 7, 0, 1)
 
 
@@ -256,9 +256,10 @@ def tile_gnnlayer_pb_kernel(
                 op=ALU.add,
             )
 
-        def quantise_h(gg):
+        def quantise_h():
             quantise(
-                h_codes[:, gg, :], h_scales[:, gg, :], h_grp[:, gg, :, :].rearrange("p n t -> p (n t)")
+                h_codes[:].rearrange("p g n -> p (g n)"), h_scales[:].rearrange("p g n -> p (g n)"),
+                h_grp[:].rearrange("p g n t -> p (g n t)"),
             )
 
         o_acc = {}
@@ -407,20 +408,18 @@ def tile_gnnlayer_pb_kernel(
         first_product(last, range(0, HALF))
         quantise_chunk(last, half, C)
         first_product(last, range(HALF, N_TILES))
-        regroup_lin(0, 0, half, LIN_V_COLS[0])
+        regroup_lin(0, 0, C, LIN_V_COLS[0])
         add_bias(0)
-        regroup_lin(0, half, C, LIN_V_COLS[0])
         add_bias(1)
-        quantise_lin(0, 0, half)
-        quantise_h(0)
-        second_product(0, early)
-        quantise_h(1)
         regroup_lin(1, 0, half, LIN_V_COLS[1])
-        quantise_lin(0, half, C)
-        second_product(0, late)
+        quantise_lin(0, 0, half)
+        quantise_h()
+        second_product(0, early)
         quantise_lin(1, 0, half)
         second_product(1, early)
         regroup_lin(1, half, C, LIN_V_COLS[1])
+        quantise_lin(0, half, C)
+        second_product(0, late)
         for lo in (half, half + C // 4):
             quantise_lin(1, lo, lo + C // 4)
             second_product(1, (lo // P, lo // P + 1))

@@ -97,8 +97,8 @@ def tile_gnnlayer_pb_kernel(
 
         def regroup(copy, dst, src):
             copy(
-                out=dst.rearrange("p (c i) t -> p c t i", i=4),
-                in_=src.rearrange("p t (c i) -> p c t i", i=4),
+                out=dst.rearrange("p (c i) t -> p c t i", i=8),
+                in_=src.rearrange("p t (c i) -> p c t i", i=8),
             )
 
         def quantise(codes, scales, grouped):

@@ -23,11 +23,9 @@ HALF = N_TILES // 2
 EPS_GN = 1e-5
 FLOPS = 2 * P * (K_POST * C + C * C)
 
-V_COLS = C // 2
 A_AFTER = 4
 RAW_BUFS = 7
 GRP_BUFS = 4
-LAST_V_COLS = C // 4
 LIN_V_COLS = (384, 128)
 O_BANK = (2, 3, 4, 5, 6, 7, 0, 1)
 
@@ -45,10 +43,17 @@ def tile_gnnlayer_pb_kernel(
 
         par_rows = keep.tile([P, P], BF16, name="par_rows")
         nc.vector.memset(par_rows[:], 0.0)
+        bpost = keep.tile([P, N_LIN, PACK], BF16, name="bpost")
         one = keep.tile([P, 1], F32, name="one")
         nc.vector.memset(one[:], 1.0)
         warm = keep.tile([P, 1], F32, name="warm")
         nc.scalar.activation(out=warm[:], in_=one[:], func=ACT.Abs_reciprocal_sqrt)
+        nc.scalar.dma_start(out=bpost[:], in_=b_post.rearrange("(g p t) -> p g t", p=P, t=PACK))
+        for v, vec in enumerate((b_lin, gn_weight, gn_bias, gn_alpha)):
+            nc.scalar.dma_start(
+                out=par_rows[N_TILES * v : N_TILES * (v + 1), :],
+                in_=vec.rearrange("(t p) -> t p", p=P),
+            )
         eps = keep.tile([P, 1], F32, name="eps")
         nc.vector.memset(eps[:], EPS_GN)
         ident = keep.tile([P, P], F32, name="ident")
@@ -76,7 +81,7 @@ def tile_gnnlayer_pb_kernel(
                 r = raw_pool.tile([P, PACK, C], BF16, name="raw%d" % i, tag="raw")
                 nc.sync.dma_start(
                     out=r[:],
-                    in_=W_lin[K_PASS * gg : K_PASS * (gg + 1), :].rearrange("(a p) n -> p a n", p=P),
+                    in_=W_lin[K_PASS * gg : K_PASS * (gg + 1), :].rearrange("(p j) n -> p j n", j=PACK),
                 )
                 raw.append(r)
 
@@ -87,11 +92,6 @@ def tile_gnnlayer_pb_kernel(
         for lo in (0, 2 * C):
             nc.sync.dma_start(out=agg_sb[:, lo : lo + 2 * C], in_=agg_rows[:, lo : lo + 2 * C])
         load_next()
-        for v, vec in enumerate((b_post, b_lin, gn_weight, gn_bias, gn_alpha)):
-            nc.sync.dma_start(
-                out=par_rows[N_TILES * v : N_TILES * (v + 1), :],
-                in_=vec.rearrange("(t p) -> t p", p=P),
-            )
         for i in range(A_AFTER + 1, RAW_BUFS - 1):
             load_next()
 
@@ -137,10 +137,12 @@ def tile_gnnlayer_pb_kernel(
         w_codes = {}
         w_scales = {}
 
-        def regroup_cols(i, lo, hi, v_cols):
-            mid = lo + v_cols
-            regroup(nc.vector.tensor_copy, grouped[i][:, lo:mid, :], raw[i][:, :, lo:mid])
-            regroup(nc.scalar.copy, grouped[i][:, mid:hi, :], raw[i][:, :, mid:hi])
+        def regroup_half(copy, i, gg, m_lo, m_hi):
+            half = slice(K_PASS * gg, K_PASS * (gg + 1))
+            copy(
+                out=grouped[i][:, half, :].rearrange("p (t m i) j -> p m j i t", t=PACK, i=2)[:, m_lo // 2 : m_hi // 2],
+                in_=raw[i][:, :, half].rearrange("p j (m i t) -> p m j i t", t=PACK, i=2)[:, m_lo // 2 : m_hi // 2],
+            )
 
         def open_chunk(i):
             g = grp_pool.tile([P, C, PACK], BF16, name="grp%d" % i, tag="grp", align_bytes=64)
@@ -172,7 +174,8 @@ def tile_gnnlayer_pb_kernel(
 
         def regroup_chunk(i):
             open_chunk(i)
-            regroup_cols(i, 0, C, V_COLS)
+            regroup_half(nc.vector.tensor_copy, i, 0, 0, P)
+            regroup_half(nc.scalar.copy, i, 1, 0, P)
             load_next()
 
         regroup_chunk(0)
@@ -200,13 +203,12 @@ def tile_gnnlayer_pb_kernel(
             quantise_chunk(i - 1, 0, C)
             first_product(i - 1, range(N_TILES))
 
-        par = keep.tile([P, 5 * N_TILES], F32, name="par")
-        nc.scalar.copy(out=par[:], in_=par_t[:, 0 : 5 * N_TILES])
-        bpost = par[:, 0:8]
-        blin = par[:, 8:16]
-        gw = par[:, 16:24]
-        gb = par[:, 24:32]
-        alpha = par[:, 32:40]
+        par = keep.tile([P, 4 * N_TILES], F32, name="par")
+        nc.scalar.copy(out=par[:], in_=par_t[:, 0 : 4 * N_TILES])
+        blin = par[:, 0:8]
+        gw = par[:, 8:16]
+        gb = par[:, 16:24]
+        alpha = par[:, 24:32]
         one_m_alpha = keep.tile([P, N_TILES], F32, name="one_m_alpha")
         nc.gpsimd.tensor_scalar(
             out=one_m_alpha[:], in0=alpha, scalar1=-1.0, scalar2=1.0, op0=ALU.mult, op1=ALU.add
@@ -252,7 +254,7 @@ def tile_gnnlayer_pb_kernel(
             nc.vector.tensor_tensor(
                 out=h_grp[:, gg, :, :],
                 in0=h_acc[gg][:].rearrange("p t n -> p n t"),
-                in1=bpost[:, HALF * gg : HALF * (gg + 1)].unsqueeze(1).to_broadcast([P, P, PACK]),
+                in1=bpost[:, gg, :].unsqueeze(1).to_broadcast([P, P, PACK]),
                 op=ALU.add,
             )
 
@@ -400,10 +402,12 @@ def tile_gnnlayer_pb_kernel(
         early = (0, 1, 2, 3)
         late = (4, 5, 6, 7)
         open_chunk(last)
-        regroup_cols(last, 0, half, LAST_V_COLS)
+        regroup_half(nc.vector.tensor_copy, last, 0, 0, P // 2)
+        regroup_half(nc.scalar.copy, last, 0, P // 2, P)
         quantise_chunk(last - 1, 0, C)
         first_product(last - 1, range(N_TILES))
-        regroup_cols(last, half, C, LAST_V_COLS)
+        regroup_half(nc.vector.tensor_copy, last, 1, 0, P // 2)
+        regroup_half(nc.scalar.copy, last, 1, P // 2, P)
         quantise_chunk(last, 0, half)
         first_product(last, range(0, HALF))
         quantise_chunk(last, half, C)

from contextlib import ExitStack

import concourse.mybir as mybir
from concourse.masks import make_identity

F32 = mybir.dt.float32
BF16 = mybir.dt.bfloat16
U32 = mybir.dt.uint32
U8 = mybir.dt.uint8
FP8X4 = mybir.dt.float8_e4m3fn_x4
ALU = mybir.AluOpType
ACT = mybir.ActivationFunctionType

P = 128
PACK = 4
K_PASS = P * PACK
C = 1024
K_POST = 5 * C
N_POST = K_POST // K_PASS
N_LIN = C // K_PASS
N_TILES = C // P
HALF = N_TILES // 2
EPS_GN = 1e-5
FLOPS = 2 * P * (K_POST * C + C * C)

A_AFTER = 4
RAW_BUFS = 7
GRP_BUFS = 4
LIN_V_COLS = (384, 128)
O_BANK = (2, 3, 4, 5, 6, 7, 0, 1)


def tile_gnnlayer_pb_kernel(
    tc, x, agg, W_post, b_post, W_lin, b_lin, gn_weight, gn_bias, gn_alpha, out
):
    nc = tc.nc
    with ExitStack() as ctx:
        keep = ctx.enter_context(tc.tile_pool(name="keep", bufs=1))
        raw_pool = ctx.enter_context(tc.tile_pool(name="raw_pool", bufs=RAW_BUFS))
        grp_pool = ctx.enter_context(tc.tile_pool(name="grp_pool", bufs=GRP_BUFS))
        psum = ctx.enter_context(tc.psum_pool(name="psum", bufs=1))
        ctx.enter_context(tc.manual_schedule())

        par_rows = keep.tile([P, P], BF16, name="par_rows")
        nc.vector.memset(par_rows[:], 0.0)
        bpost = keep.tile([P, N_LIN, PACK], BF16, name="bpost")
        one = keep.tile([P, 1], F32, name="one")
        nc.vector.memset(one[:], 1.0)
        warm = keep.tile([P, 1], F32, name="warm")
        nc.scalar.activation(out=warm[:], in_=one[:], func=ACT.Abs_reciprocal_sqrt)
        nc.scalar.dma_start(out=bpost[:], in_=b_post.rearrange("(g p t) -> p g t", p=P, t=PACK))
        for v, vec in enumerate((b_lin, gn_weight, gn_bias, gn_alpha)):
            nc.scalar.dma_start(
                out=par_rows[N_TILES * v : N_TILES * (v + 1), :],
                in_=vec.rearrange("(t p) -> t p", p=P),
            )
        eps = keep.tile([P, 1], F32, name="eps")
        nc.vector.memset(eps[:], EPS_GN)
        ident = keep.tile([P, P], F32, name="ident")
        make_identity(nc, ident[:])
        ident_bf = keep.tile([P, P], BF16, name="ident_bf")
        make_identity(nc, ident_bf[:])

        x_sb = keep.tile([P, C], BF16, name="x_sb")
        agg_sb = keep.tile([P, 4 * C], BF16, name="agg_sb")
        out_rows = out.rearrange("b n c -> (b n) c")

        raw = []

        def post_rows(i):
            return W_post[K_PASS * i : K_PASS * (i + 1), :].rearrange("(p j) c -> p j c", j=PACK)

        def load_next():
            i = len(raw)
            if i < N_POST:
                r = raw_pool.tile([P, PACK, C], BF16, name="raw%d" % i, tag="raw")
                nc.sync.dma_start(out=r[:], in_=post_rows(i))
                raw.append(r)
            elif i < N_POST + 2:
                gg = i - N_POST
                r = raw_pool.tile([P, PACK, C], BF16, name="raw%d" % i, tag="raw")
                nc.sync.dma_start(
                    out=r[:],
                    in_=W_lin[K_PASS * gg : K_PASS * (gg + 1), :].rearrange("(p j) n -> p j n", j=PACK),
                )
                raw.append(r)

        for i in range(A_AFTER):
            load_next()
        nc.sync.dma_start(out=x_sb[:], in_=x.rearrange("b n c -> (b n) c"))
        agg_rows = agg.rearrange("b n c -> (b n) c")
        for lo in (0, 2 * C):
            nc.sync.dma_start(out=agg_sb[:, lo : lo + 2 * C], in_=agg_rows[:, lo : lo + 2 * C])
        load_next()
        for i in range(A_AFTER + 1, RAW_BUFS - 1):
            load_next()

        def regroup(copy, dst, src):
            copy(
                out=dst.rearrange("p (c i) t -> p c t i", i=8),
                in_=src.rearrange("p t (c i) -> p c t i", i=8),
            )

        def quantise(codes, scales, grouped):
            nc.vector.quantize_mx(out=codes.bitcast(FP8X4), scales=scales, in_=grouped)

        x_words = x_sb[:].bitcast(F32).rearrange("n (g p u) -> n g p u", p=P, u=2)
        agg_words = agg_sb[:].bitcast(F32).rearrange("n (g p u) -> n g p u", p=P, u=2)
        a_grp = keep.tile([P, N_POST * K_PASS], BF16, name="a_grp", align_bytes=64)
        a_codes = keep.tile([P, N_POST * P], U32, name="a_codes", align_bytes=64)
        a_scales = keep.tile([P, N_POST * P], U8, name="a_scales", align_bytes=64)
        a_grp_words = a_grp[:].bitcast(F32)

        def turn(b):
            turned = psum.tile([P, 4, P], F32, name="turned%d" % b, tag="bank%d" % (b + 2))
            for j in range(4):
                g = 2 * b + j // 2
                words = x_words[:, g, :, :] if g < 2 else agg_words[:, g - 2, :, :]
                nc.tensor.transpose(turned[:, j, :], words[:, :, j % 2], ident[:])
            nc.scalar.copy(
                out=a_grp_words[:, 512 * b : 512 * (b + 1)].rearrange(
                    "p (g n u) -> p g n u", g=2, u=2
                ),
                in_=turned[:].rearrange("p (g u) n -> p g n u", u=2),
            )

        def quantise_a(b0, b1):
            quantise(
                a_codes[:, 256 * b0 : 256 * b1], a_scales[:, 256 * b0 : 256 * b1], a_grp[:, 1024 * b0 : 1024 * b1]
            )

        h_acc = []
        for b in range(2):
            acc_b = psum.tile([P, HALF, P], F32, name="h_acc%d" % b, tag="bank%d" % b)
            h_acc.append(acc_b)
        grouped = {}
        w_codes = {}
        w_scales = {}

        def regroup_half(copy, i, gg, m_lo, m_hi):
            half = slice(K_PASS * gg, K_PASS * (gg + 1))
            copy(
                out=grouped[i][:, half, :].rearrange("p (t m i) j -> p m j i t", t=PACK, i=2)[:, m_lo // 2 : m_hi // 2],
                in_=raw[i][:, :, half].rearrange("p j (m i t) -> p m j i t", t=PACK, i=2)[:, m_lo // 2 : m_hi // 2],
            )

        def open_chunk(i):
            g = grp_pool.tile([P, C, PACK], BF16, name="grp%d" % i, tag="grp", align_bytes=64)
            grouped[i] = g
            cd = keep.tile([P, C], U32, name="w_codes%d" % i, align_bytes=64)
            sc = keep.tile([P, C], U8, name="w_scales%d" % i, align_bytes=64)
            w_codes[i] = cd
            w_scales[i] = sc

        def quantise_chunk(i, lo, hi):
            quantise(
                w_codes[i][:, lo:hi],
                w_scales[i][:, lo:hi],
                grouped[i][:, lo:hi, :].rearrange("p c t -> p (c t)"),
            )

        def first_product(i, tiles):
            for m in tiles:
                t = m % HALF
                nc.tensor.matmul_mx(
                    out=h_acc[m // HALF][:, t, :],
                    lhsT=w_codes[i][:, P * m : P * (m + 1)].bitcast(FP8X4),
                    lhsT_scale=w_scales[i][:, P * m : P * (m + 1)],
                    rhs=a_codes[:, P * i : P * (i + 1)].bitcast(FP8X4),
                    rhs_scale=a_scales[:, P * i : P * (i + 1)],
                    start=(i == 0 and t == 0),
                    stop=(i == N_POST - 1 and t == HALF - 1),
                )

        def regroup_chunk(i):
            open_chunk(i)
            regroup_half(nc.vector.tensor_copy, i, 0, 0, P)
            regroup_half(nc.scalar.copy, i, 1, 0, P)
            load_next()

        regroup_chunk(0)
        regroup_chunk(1)
        quantise_chunk(0, 0, C)
        regroup_chunk(2)
        quantise_chunk(1, 0, C)
        regroup_chunk(3)
        quantise_chunk(2, 0, C)
        for b in range(N_POST // 2):
            turn(b)
        quantise_chunk(3, 0, C)
        quantise_a(0, 1)
        regroup_chunk(4)
        quantise_a(1, 5)
        for i in range(A_AFTER):
            first_product(i, range(N_TILES))
        regroup_chunk(5)
        quantise_chunk(4, 0, C)
        first_product(4, range(N_TILES))
        par_t = psum.tile([P, P], BF16, name="par_t", tag="bank7")
        nc.tensor.transpose(par_t[:], par_rows[:], ident_bf[:])
        for i in range(A_AFTER + 2, N_POST - 2):
            regroup_chunk(i)
            quantise_chunk(i - 1, 0, C)
            first_product(i - 1, range(N_TILES))

        par = keep.tile([P, 4 * N_TILES], F32, name="par")
        nc.scalar.copy(out=par[:], in_=par_t[:, 0 : 4 * N_TILES])
        blin = par[:, 0:8]
        gw = par[:, 8:16]
        gb = par[:, 16:24]
        alpha = par[:, 24:32]
        one_m_alpha = keep.tile([P, N_TILES], F32, name="one_m_alpha")
        nc.gpsimd.tensor_scalar(
            out=one_m_alpha[:], in0=alpha, scalar1=-1.0, scalar2=1.0, op0=ALU.mult, op1=ALU.add
        )
        neg_alpha_n = keep.tile([P, N_TILES], F32, name="neg_alpha_n")
        nc.gpsimd.tensor_scalar(
            out=neg_alpha_n[:], in0=alpha, scalar1=-1.0 / P, scalar2=0.0, op0=ALU.mult, op1=ALU.add
        )
        rest = keep.tile([P, N_TILES], F32, name="rest")
        nc.gpsimd.tensor_tensor(out=rest[:], in0=one_m_alpha[:], in1=blin, op=ALU.mult)

        regroup_chunk(N_POST - 2)
        quantise_chunk(N_POST - 3, 0, C)
        first_product(N_POST - 3, range(N_TILES))

        l_grp = []
        for gg in range(N_LIN):
            g = keep.tile([P, C, PACK], BF16, name="l_grp%d" % gg, align_bytes=64)
            l_grp.append(g)
        l_codes = keep.tile([P, N_LIN, C], U32, name="l_codes", align_bytes=64)
        l_scales = keep.tile([P, N_LIN, C], U8, name="l_scales", align_bytes=64)

        def regroup_lin(gg, lo, hi, v_cols):
            mid = lo + v_cols
            r = raw[N_POST + gg]
            if v_cols > 0:
                regroup(nc.vector.tensor_copy, l_grp[gg][:, lo:mid, :], r[:, :, lo:mid])
            if mid < hi:
                regroup(nc.scalar.copy, l_grp[gg][:, mid:hi, :], r[:, :, mid:hi])

        def quantise_lin(gg, lo, hi):
            quantise(
                l_codes[:, gg, lo:hi],
                l_scales[:, gg, lo:hi],
                l_grp[gg][:, lo:hi, :].rearrange("p c t -> p (c t)"),
            )

        h_grp = keep.tile([P, N_LIN, P, PACK], BF16, name="h_grp", align_bytes=64)
        h_codes = keep.tile([P, N_LIN, P], U32, name="h_codes", align_bytes=64)
        h_scales = keep.tile([P, N_LIN, P], U8, name="h_scales", align_bytes=64)

        def add_bias(gg):
            nc.vector.tensor_tensor(
                out=h_grp[:, gg, :, :],
                in0=h_acc[gg][:].rearrange("p t n -> p n t"),
                in1=bpost[:, gg, :].unsqueeze(1).to_broadcast([P, P, PACK]),
                op=ALU.add,
            )

        def quantise_h():
            quantise(
                h_codes[:].rearrange("p g n -> p (g n)"), h_scales[:].rearrange("p g n -> p (g n)"),
                h_grp[:].rearrange("p g n t -> p (g n t)"),
            )

        o_acc = {}

        def second_product(gg, tiles):
            for m in tiles:
                if gg == 0:
                    o_m = psum.tile([P, P], F32, name="o_acc%d" % m, tag="bank%d" % O_BANK[m])
                    o_acc[m] = o_m
                nc.tensor.matmul_mx(
                    out=o_acc[m][:],
                    lhsT=l_codes[:, gg, P * m : P * (m + 1)].bitcast(FP8X4),
                    lhsT_scale=l_scales[:, gg, P * m : P * (m + 1)],
                    rhs=h_codes[:, gg, :].bitcast(FP8X4),
                    rhs_scale=h_scales[:, gg, :],
                    start=(gg == 0),
                    stop=(gg == N_LIN - 1),
                )

        y_sb = keep.tile([P, N_TILES, P], F32, name="y_sb")
        o_sb = keep.tile([P, C], F32, name="o_sb")

        def small(name):
            t = keep.tile([P, N_TILES], F32, name=name)
            return t

        def col(t, m):
            return t[:, m : m + 1]

        def span(t, tiles):
            return t[:, tiles[0] : tiles[-1] + 1]

        def vec_op(o, a, b, op):
            nc.vector.tensor_tensor(out=o, in0=a, in1=b, op=op)

        stats = keep.tile([P, N_TILES, 6], F32, name="stats")
        mean_var = keep.tile([P, N_TILES, 2], F32, name="mean_var")
        sums = small("sums")
        squares = small("squares")
        junk = [keep.tile([P, P], BF16, name="junk%d" % m) for m in range(N_TILES)]
        centre = small("centre")
        second = small("second")
        shift = small("shift")
        shift_w = small("shift_w")
        rstd = small("rstd")
        scale = small("scale")
        bias = small("bias")

        def stats_on_vector(tiles):
            for m in tiles:
                nc.vector.bn_stats(out=stats[:, m, :], in_=o_acc[m][:])
            for m in tiles:
                nc.vector.bn_aggr(out=mean_var[:, m, :], in_=stats[:, m, :])

        def centre_on_vector(tiles):
            for m in tiles:
                nc.vector.tensor_scalar(
                    out=col(centre, m), in0=mean_var[:, m, 0:1], scalar1=col(one_m_alpha, m),
                    scalar2=col(rest, m), op0=ALU.mult, op1=ALU.add,
                )
            for m in tiles:
                nc.vector.scalar_tensor_tensor(
                    out=col(second, m), in0=col(centre, m), scalar=col(centre, m),
                    in1=mean_var[:, m, 1:2], op0=ALU.mult, op1=ALU.add,
                )
            first = tiles[0]
            last_one = tiles[-1] + 1
            vec_op(span(shift, tiles), span(centre, tiles), mean_var[:, first:last_one, 0], ALU.subtract)
            vec_op(span(shift_w, tiles), span(shift, tiles), span(gw, tiles), ALU.mult)

        def rstd_on_scalar(tiles, moments, factor):
            nc.scalar.activation(
                out=span(rstd, tiles), in_=span(moments, tiles), func=ACT.Abs_reciprocal_sqrt,
                bias=eps[:, 0:1], scale=factor,
            )

        def affine_on_vector(tiles):
            vec_op(span(scale, tiles), span(rstd, tiles), span(gw, tiles), ALU.mult)
            for m in tiles:
                nc.vector.scalar_tensor_tensor(
                    out=col(bias, m), in0=col(shift_w, m), scalar=col(rstd, m), in1=col(gb, m),
                    op0=ALU.mult, op1=ALU.add,
                )

        def moments_on_scalar(tiles):
            for m in tiles:
                nc.scalar.activation(
                    out=junk[m][:], in_=o_acc[m][:], func=ACT.Identity, accum_out=col(sums, m)
                )
            for m in tiles:
                nc.scalar.activation(
                    out=col(shift, m), in_=col(sums, m), func=ACT.Identity,
                    bias=col(rest, m), scale=col(neg_alpha_n, m),
                )
            for m in tiles:
                nc.scalar.activation(
                    out=junk[HALF + m][:], in_=o_acc[m][:], func=ACT.Square, bias=col(shift, m), scale=1.0,
                    accum_out=col(squares, m),
                )

        def affine_on_scalar(tiles):
            for m in tiles:
                nc.scalar.activation(
                    out=col(scale, m), in_=col(rstd, m), func=ACT.Copy, scale=col(gw, m)
                )
            for m in tiles:
                nc.scalar.activation(
                    out=col(bias, m), in_=col(shift, m), func=ACT.Identity,
                    bias=col(gb, m), scale=col(scale, m),
                )

        def apply_on_scalar(tiles):
            for m in tiles:
                nc.scalar.activation(
                    out=y_sb[:, m, :], in_=o_acc[m][:], func=ACT.Relu, bias=col(bias, m), scale=col(scale, m)
                )

        def apply_on_vector(tiles):
            for m in tiles:
                nc.vector.tensor_scalar(
                    out=y_sb[:, m, :], in0=o_acc[m][:], scalar1=col(scale, m), scalar2=col(bias, m),
                    op0=ALU.mult, op1=ALU.add,
                )

        def finish(tiles):
            m0 = tiles[0]
            cols = slice(P * m0, P * (tiles[-1] + 1))
            y_t = psum.tile([P, P * len(tiles)], F32, name="y_t%d" % m0, tag="bank%d" % O_BANK[m0])
            for m in tiles:
                nc.tensor.transpose(y_t[:, P * (m - m0) : P * (m - m0 + 1)], y_sb[:, m, :], ident[:])
            nc.vector.scalar_tensor_tensor(
                out=o_sb[:, cols], in0=y_t[:], scalar=0.0, in1=x_sb[:, cols], op0=ALU.max, op1=ALU.add
            )
            nc.sync.dma_start(out=out_rows[:, cols], in_=o_sb[:, cols])

        last = N_POST - 1
        half = C // 2
        early = (0, 1, 2, 3)
        late = (4, 5, 6, 7)
        open_chunk(last)
        regroup_half(nc.vector.tensor_copy, last, 0, 0, P // 2)
        regroup_half(nc.scalar.copy, last, 0, P // 2, P)
        quantise_chunk(last - 1, 0, C)
        first_product(last - 1, range(N_TILES))
        regroup_half(nc.vector.tensor_copy, last, 1, 0, P // 2)
        regroup_half(nc.scalar.copy, last, 1, P // 2, P)
        quantise_chunk(last, 0, half)
        first_product(last, range(0, HALF))
        quantise_chunk(last, half, C)
        first_product(last, range(HALF, N_TILES))
        regroup_lin(0, 0, C, LIN_V_COLS[0])
        add_bias(0)
        add_bias(1)
        regroup_lin(1, 0, half, LIN_V_COLS[1])
        quantise_lin(0, 0, half)
        quantise_h()
        second_product(0, early)
        quantise_lin(1, 0, half)
        second_product(1, early)
        regroup_lin(1, half, C, LIN_V_COLS[1])
        quantise_lin(0, half, C)
        second_product(0, late)
        for lo in (half, half + C // 4):
            quantise_lin(1, lo, lo + C // 4)
            second_product(1, (lo // P, lo // P + 1))
        moments_on_scalar(early)
        stats_on_vector(late)
        rstd_on_scalar(early, squares, 1.0 / P)
        centre_on_vector(late)
        affine_on_scalar(early)
        apply_on_scalar(early[:1])
        rstd_on_scalar(late, second, 1.0)
        apply_on_scalar(early[1:])
        affine_on_vector(late)
        apply_on_scalar((6, 7))
        apply_on_vector((4, 5))
        finish((0, 1))
        finish((2, 3))
        finish((4, 5))
        finish((6, 7))
